import numpy as np
import ml_dtypes


def mxq(x, axis, fmt="e4m3"):
    dtype, down = {"e4m3": (ml_dtypes.float8_e4m3fn, 7), "e5m2": (ml_dtypes.float8_e5m2, 14)}[fmt]
    v = np.moveaxis(np.asarray(x, np.float32).astype(ml_dtypes.bfloat16).astype(np.float64), axis, -1)
    blocks = v.reshape(v.shape[:-1] + (-1, 32))
    amax = np.abs(blocks).max(-1, keepdims=True)
    byte = np.maximum(np.where(amax > 0, np.frexp(amax)[1] - 1 + 127, 0) - down, 1)
    scale = np.exp2(byte - 127.0)
    codes = (blocks / scale).astype(np.float32).astype(dtype).astype(np.float64)
    return np.moveaxis((codes * scale).reshape(v.shape), -1, axis)


WIDE = False


def mx_kscale(k):
    if not WIDE:
        return np.ones(k)
    levels = np.array([10, -10, 5, -5, 0])
    a = np.random.permutation(np.resize(levels, k // 512 * 4)).reshape(k // 512, 4)
    idx = np.arange(k)
    return np.exp2(a[idx // 512, idx % 128 // 32])


BF16 = ml_dtypes.bfloat16


def bf(x):
    return np.asarray(x, np.float32).astype(BF16)


def f64(x):
    return np.asarray(x).astype(np.float64)


B, N, H, F, M, G, C = 16, 16, 1024, 1024, 1024, 1024, 3


def silu(v):
    return v / (1.0 + np.exp(-v))


def setup_inputs():
    s = mx_kscale(H)
    w_nodes = np.random.standard_normal((2, H, F)) / np.sqrt(2 * H) / s[None, :, None]
    w_dist = np.random.standard_normal((1, F)) * 0.3
    return {"node_state": bf(np.random.standard_normal((B, N, H)) * s),
            "positions": bf(np.random.standard_normal((B, N, C))),
            "We1": bf(np.concatenate([w_nodes.reshape(2 * H, F), w_dist], 0)),
            "be1": bf(np.random.standard_normal(F) * 0.5),
            "We2": bf(np.random.standard_normal((F, M)) / np.sqrt(F)),
            "be2": bf(np.random.standard_normal(M) * 0.5)}


def reference(node_state, positions, We1, be1, We2, be2):
    x, p, w1 = f64(node_state), f64(positions), f64(We1)
    rel = p[:, :, None, :] - p[:, None, :, :]
    sq = np.sum(rel * rel, axis=-1, keepdims=True)
    dist = np.where(sq > 0, np.sqrt(np.where(sq > 0, sq, 1.0)), 0.0)
    xq = mxq(x, 2, "e4m3")
    a_i = xq @ mxq(w1[:H], 0, "e4m3")
    a_j = xq @ mxq(w1[H:2 * H], 0, "e4m3")
    pre = a_i[:, :, None, :] + a_j[:, None, :, :] + dist * w1[2 * H] + f64(be1)
    h = silu(pre).reshape(B * N * N, F)
    msg = (mxq(h, 1, "e4m3") @ mxq(f64(We2), 0, "e4m3")) + f64(be2)
    return msg.reshape(B, N, N, M)

@@ -1,0 +1,248 @@
+from contextlib import ExitStack
+
+import concourse.mybir as mybir
+from concourse.masks import make_identity
+
+F32 = mybir.dt.float32
+BF16 = mybir.dt.bfloat16
+U32 = mybir.dt.uint32
+U8 = mybir.dt.uint8
+FP8X4 = mybir.dt.float8_e4m3fn_x4
+ALU = mybir.AluOpType
+ACT = mybir.ActivationFunctionType
+
+P = 128
+PACK = 4
+K_PASS = P * PACK
+GRAPHS = 16
+NODES = 16
+COORDS = 3
+WIDTH = 1024
+PASSES = WIDTH // K_PASS
+F_TILES = WIDTH // P
+ALL_NODES = GRAPHS * NODES
+PAIRS = NODES * NODES
+BANK = 512
+CHUNK_GRAPHS = 2
+CHUNK = CHUNK_GRAPHS * PAIRS
+CHUNKS = GRAPHS // CHUNK_GRAPHS
+HALF = NODES // 2
+TINY = 1e-30
+
+FLOPS = 2 * ALL_NODES * WIDTH * 2 * WIDTH + 2 * GRAPHS * PAIRS * WIDTH * WIDTH
+
+
+def tile_graphmessagelayer_pa_kernel(tc, node_state, positions, We1, be1, We2, be2, out):
+    nc = tc.nc
+    out_rows = out.rearrange("b i j m -> (b i j) m")
+
+    with ExitStack() as ctx:
+        keep = ctx.enter_context(tc.tile_pool(name="keep", bufs=1))
+        raw_pool = ctx.enter_context(tc.tile_pool(name="raw", bufs=4))
+        grouped_pool = ctx.enter_context(tc.tile_pool(name="grouped", bufs=2))
+        work = ctx.enter_context(tc.tile_pool(name="work", bufs=2))
+        store_pool = ctx.enter_context(tc.tile_pool(name="store", bufs=4))
+        psum = ctx.enter_context(tc.psum_pool(name="psum", bufs=4))
+
+        x_rows = keep.tile([P, 2, WIDTH], BF16)
+        nc.sync.dma_start(
+            out=x_rows[:], in_=node_state.rearrange("b n h -> (b n) h").rearrange("(a p) h -> p a h", p=P)
+        )
+        vec_rows = keep.tile([P, P], BF16)
+        nc.vector.memset(vec_rows[:], 0.0)
+        nc.scalar.dma_start(out=vec_rows[0:F_TILES, :], in_=be1.rearrange("(r c) -> r c", c=P))
+        nc.scalar.dma_start(
+            out=vec_rows[F_TILES : 2 * F_TILES, :],
+            in_=We1[2 * WIDTH : 2 * WIDTH + 1, :].rearrange("o (r c) -> (o r) c", c=P),
+        )
+        pos_nodes = keep.tile([P, 64], BF16)
+        nc.vector.memset(pos_nodes[:], 0.0)
+        with nc.allow_non_contiguous_dma(reason="768 small values, once"):
+            nc.scalar.dma_start(
+                out=pos_nodes[0:NODES, 0 : GRAPHS * COORDS].rearrange("n (b c) -> n b c", c=COORDS),
+                in_=positions.rearrange("b n c -> n b c"),
+            )
+
+        weight_rows = [
+            We1[0:WIDTH, :],
+            We1[WIDTH : 2 * WIDTH, :],
+            We2,
+        ]
+        w_codes = keep.tile([P, 3 * PASSES, WIDTH], U32, align_bytes=64)
+        w_scales = keep.tile([P, 3 * PASSES, WIDTH], U8, align_bytes=64)
+
+        ident_bf = keep.tile([P, P], BF16)
+        make_identity(nc, ident_bf[:])
+        ident_f = keep.tile([P, P], F32)
+        make_identity(nc, ident_f[:])
+
+        x_grouped = keep.tile([P, PASSES, ALL_NODES, PACK], BF16, align_bytes=64)
+        for a in range(2):
+            for g in range(PASSES):
+                x_t = psum.tile([P, PACK, P], BF16, tag="setup")
+                for t in range(PACK):
+                    k0 = g * K_PASS + t * P
+                    nc.tensor.transpose(x_t[:, t, :], x_rows[:, a, k0 : k0 + P], ident_bf[:])
+                nc.vector.tensor_copy(
+                    out=x_grouped[:, g, a * P : (a + 1) * P, :], in_=x_t[:].rearrange("p t r -> p r t")
+                )
+        x_codes = keep.tile([P, PASSES, ALL_NODES], U32, align_bytes=64)
+        x_scales = keep.tile([P, PASSES, ALL_NODES], U8, align_bytes=64)
+        nc.vector.quantize_mx(
+            out=x_codes[:].rearrange("p g r -> p (g r)").bitcast(FP8X4),
+            scales=x_scales[:].rearrange("p g r -> p (g r)"),
+            in_=x_grouped[:].rearrange("p g r t -> p (g r t)"),
+        )
+
+        vec_t = psum.tile([P, P], BF16, tag="setup")
+        nc.tensor.transpose(vec_t[:], vec_rows[:], ident_bf[:])
+        vecs = keep.tile([P, 2 * F_TILES], F32)
+        nc.vector.tensor_copy(out=vecs[:], in_=vec_t[:, 0 : 2 * F_TILES])
+
+        sel = keep.tile([P, 2, P], BF16)
+        for h in range(2):
+            nc.vector.tensor_tensor(
+                out=sel[:, h, :].rearrange("p (i j) -> p i j", j=NODES),
+                in0=ident_bf[:, h * HALF : (h + 1) * HALF].unsqueeze(2).to_broadcast([P, HALF, NODES]),
+                in1=ident_bf[:, 0:NODES].unsqueeze(1).to_broadcast([P, HALF, NODES]),
+                op=ALU.subtract,
+            )
+        rel = psum.tile([P, 2, 64], F32, tag="setup")
+        for h in range(2):
+            nc.tensor.matmul(out=rel[:, h, :], lhsT=sel[:, h, :], rhs=pos_nodes[:], start=True, stop=True)
+        rel_sq = keep.tile([P, 2, 64], F32)
+        nc.scalar.activation(out=rel_sq[:], in_=rel[:], func=ACT.Square)
+        sq = keep.tile([P, 2, GRAPHS], F32)
+        nc.vector.tensor_reduce(
+            out=sq[:],
+            in_=rel_sq[:, :, 0 : GRAPHS * COORDS].rearrange("p h (b c) -> p h b c", c=COORDS),
+            axis=mybir.AxisListType.X,
+            op=ALU.add,
+        )
+        sq_floor = keep.tile([P, 2, GRAPHS], F32)
+        nc.vector.tensor_scalar_max(out=sq_floor[:], in0=sq[:], scalar1=TINY)
+        root = keep.tile([P, 2, GRAPHS], F32)
+        nc.scalar.activation(out=root[:], in_=sq_floor[:], func=ACT.Sqrt)
+        dist_col = keep.tile([P, 2, GRAPHS], F32)
+        nc.vector.scalar_tensor_tensor(
+            out=dist_col[:].rearrange("p h b -> p (h b)"),
+            in0=sq[:].rearrange("p h b -> p (h b)"),
+            scalar=0.0,
+            in1=root[:].rearrange("p h b -> p (h b)"),
+            op0=ALU.is_gt,
+            op1=ALU.mult,
+        )
+        dist_all = keep.tile([P, GRAPHS * PAIRS], F32)
+        for c in range(CHUNKS):
+            spread = psum.tile([P, BANK], F32, tag="setup")
+            for e in range(CHUNK_GRAPHS):
+                for h in range(2):
+                    b = c * CHUNK_GRAPHS + e
+                    col = e * PAIRS + h * P
+                    nc.tensor.matmul(
+                        out=spread[:, col : col + P],
+                        lhsT=dist_col[:, h, b : b + 1].to_broadcast([P, P]),
+                        rhs=ident_f[:],
+                        start=True,
+                        stop=True,
+                    )
+            nc.scalar.copy(out=dist_all[:, c * CHUNK : (c + 1) * CHUNK], in_=spread[:])
+
+        for w in range(3):
+            for g in range(PASSES):
+                raw = raw_pool.tile([P, PACK, WIDTH], BF16)
+                nc.sync.dma_start(
+                    out=raw[:],
+                    in_=weight_rows[w][g * K_PASS : (g + 1) * K_PASS, :].rearrange("(t p) n -> p t n", p=P),
+                )
+                grouped = grouped_pool.tile([P, WIDTH, PACK], BF16, align_bytes=64)
+                mid = WIDTH // 2
+                nc.vector.tensor_copy(out=grouped[:, 0:mid, :], in_=raw[:, :, 0:mid].rearrange("p t n -> p n t"))
+                nc.scalar.copy(out=grouped[:, mid:WIDTH, :], in_=raw[:, :, mid:WIDTH].rearrange("p t n -> p n t"))
+                nc.vector.quantize_mx(
+                    out=w_codes[:, w * PASSES + g, :].bitcast(FP8X4),
+                    scales=w_scales[:, w * PASSES + g, :],
+                    in_=grouped[:].rearrange("p n t -> p (n t)"),
+                )
+        be2_all = keep.tile([P, WIDTH], BF16)
+        nc.sync.dma_start(out=be2_all[:], in_=be2.partition_broadcast(P))
+
+        a_i = keep.tile([P, F_TILES, ALL_NODES], F32)
+        a_j = keep.tile([P, F_TILES, ALL_NODES], F32)
+        for w in range(2):
+            for pair in range(F_TILES // 2):
+                a_ps = psum.tile([P, 2, ALL_NODES], F32, tag="setup")
+                for e in range(2):
+                    f = 2 * pair + e
+                    for g in range(PASSES):
+                        nc.tensor.matmul_mx(
+                            out=a_ps[:, e, :],
+                            lhsT=w_codes[:, w * PASSES + g, f * P : (f + 1) * P].bitcast(FP8X4),
+                            lhsT_scale=w_scales[:, w * PASSES + g, f * P : (f + 1) * P],
+                            rhs=x_codes[:, g, :].bitcast(FP8X4),
+                            rhs_scale=x_scales[:, g, :],
+                            start=(g == 0),
+                            stop=(g == PASSES - 1),
+                        )
+                    if w == 0:
+                        nc.scalar.activation(
+                            out=a_i[:, f, :], in_=a_ps[:, e, :], func=ACT.Identity, bias=vecs[:, f : f + 1]
+                        )
+                if w == 1:
+                    nc.vector.tensor_copy(out=a_j[:, 2 * pair : 2 * pair + 2, :], in_=a_ps[:])
+
+        for c in range(CHUNKS):
+            pre = work.tile([P, F_TILES, CHUNK], F32)
+            for e in range(CHUNK_GRAPHS):
+                n0 = (c * CHUNK_GRAPHS + e) * NODES
+                nc.gpsimd.tensor_tensor(
+                    out=pre[:, :, e * PAIRS : (e + 1) * PAIRS].rearrange("p f (i j) -> p f i j", j=NODES),
+                    in0=a_i[:, :, n0 : n0 + NODES].unsqueeze(3).to_broadcast([P, F_TILES, NODES, NODES]),
+                    in1=a_j[:, :, n0 : n0 + NODES].unsqueeze(2).to_broadcast([P, F_TILES, NODES, NODES]),
+                    op=ALU.add,
+                )
+            for f in range(F_TILES):
+                nc.vector.scalar_tensor_tensor(
+                    out=pre[:, f, :],
+                    in0=dist_all[:, c * CHUNK : (c + 1) * CHUNK],
+                    scalar=vecs[:, F_TILES + f : F_TILES + f + 1],
+                    in1=pre[:, f, :],
+                    op0=ALU.mult,
+                    op1=ALU.add,
+                )
+            h_grouped = work.tile([P, PASSES, CHUNK, PACK], BF16, align_bytes=64)
+            for g in range(PASSES):
+                nc.scalar.activation(
+                    out=h_grouped[:, g, :, :],
+                    in_=pre[:, g * PACK : (g + 1) * PACK, :].rearrange("p t r -> p r t"),
+                    func=ACT.Silu,
+                )
+            h_codes = work.tile([P, PASSES, CHUNK], U32, align_bytes=64)
+            h_scales = work.tile([P, PASSES, CHUNK], U8, align_bytes=64)
+            nc.vector.quantize_mx(
+                out=h_codes[:].rearrange("p g r -> p (g r)").bitcast(FP8X4),
+                scales=h_scales[:].rearrange("p g r -> p (g r)"),
+                in_=h_grouped[:].rearrange("p g r t -> p (g r t)"),
+            )
+            for r in range(CHUNK // P):
+                msg = store_pool.tile([P, WIDTH], F32)
+                for m in range(WIDTH // BANK):
+                    acc = psum.tile([P, BANK], F32, tag="acc")
+                    for g in range(PASSES):
+                        nc.tensor.matmul_mx(
+                            out=acc[:],
+                            lhsT=h_codes[:, g, r * P : (r + 1) * P].bitcast(FP8X4),
+                            lhsT_scale=h_scales[:, g, r * P : (r + 1) * P],
+                            rhs=w_codes[:, 2 * PASSES + g, m * BANK : (m + 1) * BANK].bitcast(FP8X4),
+                            rhs_scale=w_scales[:, 2 * PASSES + g, m * BANK : (m + 1) * BANK],
+                            start=(g == 0),
+                            stop=(g == PASSES - 1),
+                        )
+                    nc.vector.tensor_tensor(
+                        out=msg[:, m * BANK : (m + 1) * BANK],
+                        in0=acc[:],
+                        in1=be2_all[:, m * BANK : (m + 1) * BANK],
+                        op=ALU.add,
+                    )
+                row0 = c * CHUNK + r * P
+                nc.sync.dma_start(out=out_rows[row0 : row0 + P, :], in_=msg[:])

@@ -5,6 +5,7 @@ from concourse.masks import make_identity
 
 F32 = mybir.dt.float32
 BF16 = mybir.dt.bfloat16
+I32 = mybir.dt.int32
 U32 = mybir.dt.uint32
 U8 = mybir.dt.uint8
 FP8X4 = mybir.dt.float8_e4m3fn_x4
@@ -22,12 +23,21 @@ PASSES = WIDTH // K_PASS
 F_TILES = WIDTH // P
 ALL_NODES = GRAPHS * NODES
 PAIRS = NODES * NODES
+HALVES = PAIRS // P
+HALF = NODES // HALVES
 BANK = 512
-CHUNK_GRAPHS = 2
-CHUNK = CHUNK_GRAPHS * PAIRS
-CHUNKS = GRAPHS // CHUNK_GRAPHS
-HALF = NODES // 2
+RUN = 4
 TINY = 1e-30
+
+HI = 0
+LO = 32
+DIST = 64
+ONE = 67
+USED = 68
+VECTOR_GRAPHS = 2
+TENSOR_GRAPHS = GRAPHS - VECTOR_GRAPHS
+UNITS = GRAPHS * HALVES
+TENSOR_UNITS = TENSOR_GRAPHS * HALVES
 
 FLOPS = 2 * ALL_NODES * WIDTH * 2 * WIDTH + 2 * GRAPHS * PAIRS * WIDTH * WIDTH
 
@@ -40,36 +50,37 @@ def tile_graphmessagelayer_pa_kernel(tc, node_state, positions, We1, be1, We2, b
         keep = ctx.enter_context(tc.tile_pool(name="keep", bufs=1))
         raw_pool = ctx.enter_context(tc.tile_pool(name="raw", bufs=4))
         grouped_pool = ctx.enter_context(tc.tile_pool(name="grouped", bufs=2))
-        work = ctx.enter_context(tc.tile_pool(name="work", bufs=2))
-        store_pool = ctx.enter_context(tc.tile_pool(name="store", bufs=4))
-        psum = ctx.enter_context(tc.psum_pool(name="psum", bufs=4))
+        work = ctx.enter_context(tc.tile_pool(name="work", bufs=4))
+        store_pool = ctx.enter_context(tc.tile_pool(name="store", bufs=6))
+        psum_flip = ctx.enter_context(tc.psum_pool(name="psum_flip", bufs=1))
+        psum_pre = ctx.enter_context(tc.psum_pool(name="psum_pre", bufs=4))
+        psum_acc = ctx.enter_context(tc.psum_pool(name="psum_acc", bufs=3))
+
+        vec_rows = keep.tile([P, P], BF16)
+        nc.vector.memset(vec_rows[:], 0.0)
+        pos_nodes = keep.tile([P, 64], BF16)
+        nc.vector.memset(pos_nodes[:], 0.0)
+        stacked = keep.tile([P, F_TILES, GRAPHS, P], BF16)
+        stacked_words = stacked[:].rearrange("p f b c -> p (f b c)").bitcast(I32).rearrange("p (r c) -> p r c", c=P // 2)
+        nc.vector.memset(stacked_words[:, :, USED // 2 : P // 2], 0)
+        dist_cols = keep.tile([P, HALVES, GRAPHS, P], BF16)
+        nc.vector.memset(dist_cols[:].rearrange("p h b c -> p (h b c)").bitcast(I32), 0)
+        nc.vector.memset(dist_cols[:, :, :, ONE : ONE + 1], 1.0)
 
         x_rows = keep.tile([P, 2, WIDTH], BF16)
         nc.sync.dma_start(
             out=x_rows[:], in_=node_state.rearrange("b n h -> (b n) h").rearrange("(a p) h -> p a h", p=P)
         )
-        vec_rows = keep.tile([P, P], BF16)
-        nc.vector.memset(vec_rows[:], 0.0)
         nc.scalar.dma_start(out=vec_rows[0:F_TILES, :], in_=be1.rearrange("(r c) -> r c", c=P))
         nc.scalar.dma_start(
             out=vec_rows[F_TILES : 2 * F_TILES, :],
             in_=We1[2 * WIDTH : 2 * WIDTH + 1, :].rearrange("o (r c) -> (o r) c", c=P),
         )
-        pos_nodes = keep.tile([P, 64], BF16)
-        nc.vector.memset(pos_nodes[:], 0.0)
         with nc.allow_non_contiguous_dma(reason="768 small values, once"):
             nc.scalar.dma_start(
                 out=pos_nodes[0:NODES, 0 : GRAPHS * COORDS].rearrange("n (b c) -> n b c", c=COORDS),
                 in_=positions.rearrange("b n c -> n b c"),
             )
-
-        weight_rows = [
-            We1[0:WIDTH, :],
-            We1[WIDTH : 2 * WIDTH, :],
-            We2,
-        ]
-        w_codes = keep.tile([P, 3 * PASSES, WIDTH], U32, align_bytes=64)
-        w_scales = keep.tile([P, 3 * PASSES, WIDTH], U8, align_bytes=64)
 
         ident_bf = keep.tile([P, P], BF16)
         make_identity(nc, ident_bf[:])
@@ -79,7 +90,7 @@ def tile_graphmessagelayer_pa_kernel(tc, node_state, positions, We1, be1, We2, b
         x_grouped = keep.tile([P, PASSES, ALL_NODES, PACK], BF16, align_bytes=64)
         for a in range(2):
             for g in range(PASSES):
-                x_t = psum.tile([P, PACK, P], BF16, tag="setup")
+                x_t = psum_pre.tile([P, PACK, P], BF16, tag="pre")
                 for t in range(PACK):
                     k0 = g * K_PASS + t * P
                     nc.tensor.transpose(x_t[:, t, :], x_rows[:, a, k0 : k0 + P], ident_bf[:])
@@ -94,61 +105,108 @@ def tile_graphmessagelayer_pa_kernel(tc, node_state, positions, We1, be1, We2, b
             in_=x_grouped[:].rearrange("p g r t -> p (g r t)"),
         )
 
-        vec_t = psum.tile([P, P], BF16, tag="setup")
+        vec_t = psum_pre.tile([P, P], BF16, tag="pre")
         nc.tensor.transpose(vec_t[:], vec_rows[:], ident_bf[:])
-        vecs = keep.tile([P, 2 * F_TILES], F32)
-        nc.vector.tensor_copy(out=vecs[:], in_=vec_t[:, 0 : 2 * F_TILES])
+        vecs = keep.tile([P, 2, F_TILES], F32)
+        nc.vector.tensor_copy(out=vecs[:].rearrange("p v f -> p (v f)"), in_=vec_t[:, 0 : 2 * F_TILES])
+        nc.vector.tensor_copy(
+            out=stacked[:, :, :, DIST:ONE],
+            in_=vecs[:, 1, :].unsqueeze(2).unsqueeze(3).to_broadcast([P, F_TILES, GRAPHS, ONE - DIST]),
+        )
+        nc.vector.tensor_copy(
+            out=stacked[:, :, :, ONE : ONE + 1],
+            in_=vecs[:, 0, :].unsqueeze(2).unsqueeze(3).to_broadcast([P, F_TILES, GRAPHS, 1]),
+        )
 
-        sel = keep.tile([P, 2, P], BF16)
-        for h in range(2):
+        sel = keep.tile([P, HALVES, P], BF16)
+        for h in range(HALVES):
             nc.vector.tensor_tensor(
                 out=sel[:, h, :].rearrange("p (i j) -> p i j", j=NODES),
                 in0=ident_bf[:, h * HALF : (h + 1) * HALF].unsqueeze(2).to_broadcast([P, HALF, NODES]),
                 in1=ident_bf[:, 0:NODES].unsqueeze(1).to_broadcast([P, HALF, NODES]),
                 op=ALU.subtract,
             )
-        rel = psum.tile([P, 2, 64], F32, tag="setup")
-        for h in range(2):
+        rel = psum_pre.tile([P, HALVES, 64], F32, tag="pre")
+        for h in range(HALVES):
             nc.tensor.matmul(out=rel[:, h, :], lhsT=sel[:, h, :], rhs=pos_nodes[:], start=True, stop=True)
-        rel_sq = keep.tile([P, 2, 64], F32)
+        rel_sq = keep.tile([P, HALVES, 64], F32)
         nc.scalar.activation(out=rel_sq[:], in_=rel[:], func=ACT.Square)
-        sq = keep.tile([P, 2, GRAPHS], F32)
+        sq = keep.tile([P, HALVES, GRAPHS], F32)
         nc.vector.tensor_reduce(
             out=sq[:],
             in_=rel_sq[:, :, 0 : GRAPHS * COORDS].rearrange("p h (b c) -> p h b c", c=COORDS),
             axis=mybir.AxisListType.X,
             op=ALU.add,
         )
-        sq_floor = keep.tile([P, 2, GRAPHS], F32)
+        sq_floor = keep.tile([P, HALVES, GRAPHS], F32)
         nc.vector.tensor_scalar_max(out=sq_floor[:], in0=sq[:], scalar1=TINY)
-        root = keep.tile([P, 2, GRAPHS], F32)
+        root = keep.tile([P, HALVES, GRAPHS], F32)
         nc.scalar.activation(out=root[:], in_=sq_floor[:], func=ACT.Sqrt)
-        dist_col = keep.tile([P, 2, GRAPHS], F32)
+        dist = keep.tile([P, HALVES, GRAPHS], F32)
         nc.vector.scalar_tensor_tensor(
-            out=dist_col[:].rearrange("p h b -> p (h b)"),
+            out=dist[:].rearrange("p h b -> p (h b)"),
             in0=sq[:].rearrange("p h b -> p (h b)"),
             scalar=0.0,
             in1=root[:].rearrange("p h b -> p (h b)"),
             op0=ALU.is_gt,
             op1=ALU.mult,
         )
-        dist_all = keep.tile([P, GRAPHS * PAIRS], F32)
-        for c in range(CHUNKS):
-            spread = psum.tile([P, BANK], F32, tag="setup")
-            for e in range(CHUNK_GRAPHS):
-                for h in range(2):
-                    b = c * CHUNK_GRAPHS + e
-                    col = e * PAIRS + h * P
-                    nc.tensor.matmul(
-                        out=spread[:, col : col + P],
-                        lhsT=dist_col[:, h, b : b + 1].to_broadcast([P, P]),
-                        rhs=ident_f[:],
-                        start=True,
-                        stop=True,
-                    )
-            nc.scalar.copy(out=dist_all[:, c * CHUNK : (c + 1) * CHUNK], in_=spread[:])
+        rest = keep.tile([P, HALVES, GRAPHS], F32)
+        nc.vector.tensor_copy(out=dist_cols[:, :, :, DIST], in_=dist[:])
+        nc.vector.tensor_tensor(out=rest[:], in0=dist[:], in1=dist_cols[:, :, :, DIST], op=ALU.subtract)
+        nc.vector.tensor_copy(out=dist_cols[:, :, :, DIST + 1], in_=rest[:])
+        nc.vector.tensor_tensor(
+            out=dist_cols[:, :, :, DIST + 2], in0=rest[:], in1=dist_cols[:, :, :, DIST + 1], op=ALU.subtract
+        )
 
-        for w in range(3):
+        pick = keep.tile([P, 2 * NODES], BF16)
+        nc.vector.tensor_tensor(
+            out=pick[:], in0=ident_bf[:, HI : HI + 2 * NODES], in1=ident_bf[:, LO : LO + 2 * NODES], op=ALU.add
+        )
+        pick_pairs = keep.tile([P, NODES, NODES], BF16)
+        nc.vector.tensor_tensor(
+            out=pick_pairs[:],
+            in0=pick[:, 0:NODES].unsqueeze(2).to_broadcast([P, NODES, NODES]),
+            in1=pick[:, NODES : 2 * NODES].unsqueeze(1).to_broadcast([P, NODES, NODES]),
+            op=ALU.add,
+        )
+        spread = keep.tile([P, GRAPHS, PAIRS], BF16)
+        nc.vector.tensor_copy(
+            out=spread[0:DIST, :, :],
+            in_=pick_pairs[0:DIST, :, :].rearrange("p i j -> p (i j)").unsqueeze(1).to_broadcast([DIST, GRAPHS, PAIRS]),
+        )
+        per_bank = 2 * BANK // P
+        for q in range(GRAPHS * HALVES // per_bank):
+            dist_t = psum_flip.tile([P, per_bank // HALVES, HALVES, P], BF16, tag="flip")
+            for k in range(per_bank // HALVES):
+                for h in range(HALVES):
+                    b = q * (per_bank // HALVES) + k
+                    nc.tensor.transpose(dist_t[:, k, h, :], dist_cols[:, h, b, :], ident_bf[:])
+            b0 = q * (per_bank // HALVES)
+            nc.scalar.copy(
+                out=spread[DIST:P, b0 : b0 + per_bank // HALVES, :].rearrange("p b q -> p (b q)"),
+                in_=dist_t[DIST:P, :, :, :].rearrange("p k h n -> p (k h n)"),
+            )
+
+        dist_rep = keep.tile([P, VECTOR_GRAPHS, HALVES, P], F32)
+        nc.vector.tensor_copy(
+            out=dist_rep[:],
+            in_=dist[:, :, TENSOR_GRAPHS:GRAPHS].rearrange("p h b -> p b h").unsqueeze(3).to_broadcast(
+                [P, VECTOR_GRAPHS, HALVES, P]
+            ),
+        )
+        dist_flip = psum_pre.tile([P, VECTOR_GRAPHS, HALVES, P], F32, tag="pre")
+        for v in range(VECTOR_GRAPHS):
+            for h in range(HALVES):
+                nc.tensor.transpose(dist_flip[:, v, h, :], dist_rep[:, v, h, :], ident_f[:])
+        dist_all = keep.tile([P, VECTOR_GRAPHS, PAIRS], F32)
+        nc.scalar.copy(out=dist_all[:].rearrange("p v q -> p (v q)"), in_=dist_flip[:].rearrange("p v h n -> p (v h n)"))
+
+        w_codes = keep.tile([P, 3 * PASSES, WIDTH], U32, align_bytes=64)
+        w_scales = keep.tile([P, 3 * PASSES, WIDTH], U8, align_bytes=64)
+        a_last = keep.tile([P, 2, F_TILES, VECTOR_GRAPHS * NODES], F32)
+        weight_rows = [We1[0:WIDTH, :], We1[WIDTH : 2 * WIDTH, :], We2]
+        def quantise_weight(w):
             for g in range(PASSES):
                 raw = raw_pool.tile([P, PACK, WIDTH], BF16)
                 nc.sync.dma_start(
@@ -157,21 +215,23 @@ def tile_graphmessagelayer_pa_kernel(tc, node_state, positions, We1, be1, We2, b
                 )
                 grouped = grouped_pool.tile([P, WIDTH, PACK], BF16, align_bytes=64)
                 mid = WIDTH // 2
-                nc.vector.tensor_copy(out=grouped[:, 0:mid, :], in_=raw[:, :, 0:mid].rearrange("p t n -> p n t"))
-                nc.scalar.copy(out=grouped[:, mid:WIDTH, :], in_=raw[:, :, mid:WIDTH].rearrange("p t n -> p n t"))
+                nc.vector.tensor_copy(
+                    out=grouped[:, 0:mid, :].rearrange("p (c i) t -> p c t i", i=RUN),
+                    in_=raw[:, :, 0:mid].rearrange("p t (c i) -> p c t i", i=RUN),
+                )
+                nc.scalar.copy(
+                    out=grouped[:, mid:WIDTH, :].rearrange("p (c i) t -> p c t i", i=RUN),
+                    in_=raw[:, :, mid:WIDTH].rearrange("p t (c i) -> p c t i", i=RUN),
+                )
                 nc.vector.quantize_mx(
                     out=w_codes[:, w * PASSES + g, :].bitcast(FP8X4),
                     scales=w_scales[:, w * PASSES + g, :],
                     in_=grouped[:].rearrange("p n t -> p (n t)"),
                 )
-        be2_all = keep.tile([P, WIDTH], BF16)
-        nc.sync.dma_start(out=be2_all[:], in_=be2.partition_broadcast(P))
 
-        a_i = keep.tile([P, F_TILES, ALL_NODES], F32)
-        a_j = keep.tile([P, F_TILES, ALL_NODES], F32)
-        for w in range(2):
+        def node_products(w):
             for pair in range(F_TILES // 2):
-                a_ps = psum.tile([P, 2, ALL_NODES], F32, tag="setup")
+                a_ps = psum_pre.tile([P, 2, ALL_NODES], F32, tag="pre")
                 for e in range(2):
                     f = 2 * pair + e
                     for g in range(PASSES):
@@ -184,65 +244,137 @@ def tile_graphmessagelayer_pa_kernel(tc, node_state, positions, We1, be1, We2, b
                             start=(g == 0),
                             stop=(g == PASSES - 1),
                         )
-                    if w == 0:
-                        nc.scalar.activation(
-                            out=a_i[:, f, :], in_=a_ps[:, e, :], func=ACT.Identity, bias=vecs[:, f : f + 1]
-                        )
-                if w == 1:
-                    nc.vector.tensor_copy(out=a_j[:, 2 * pair : 2 * pair + 2, :], in_=a_ps[:])
+                f_pair = slice(2 * pair, 2 * pair + 2)
+                by_graph = a_ps[:].rearrange("p e (b n) -> p e b n", n=NODES)
+                high = stacked[:, f_pair, :, HI + w * NODES : HI + (w + 1) * NODES]
+                nc.scalar.copy(out=high, in_=by_graph)
+                nc.vector.tensor_tensor(
+                    out=stacked[:, f_pair, :, LO + w * NODES : LO + (w + 1) * NODES],
+                    in0=by_graph,
+                    in1=high,
+                    op=ALU.subtract,
+                )
+                nc.scalar.copy(out=a_last[:, w, f_pair, :], in_=a_ps[:, :, TENSOR_GRAPHS * NODES : ALL_NODES])
 
-        for c in range(CHUNKS):
-            pre = work.tile([P, F_TILES, CHUNK], F32)
-            for e in range(CHUNK_GRAPHS):
-                n0 = (c * CHUNK_GRAPHS + e) * NODES
-                nc.gpsimd.tensor_tensor(
-                    out=pre[:, :, e * PAIRS : (e + 1) * PAIRS].rearrange("p f (i j) -> p f i j", j=NODES),
-                    in0=a_i[:, :, n0 : n0 + NODES].unsqueeze(3).to_broadcast([P, F_TILES, NODES, NODES]),
-                    in1=a_j[:, :, n0 : n0 + NODES].unsqueeze(2).to_broadcast([P, F_TILES, NODES, NODES]),
-                    op=ALU.add,
-                )
+        quantise_weight(0)
+        node_products(0)
+        quantise_weight(1)
+        node_products(1)
+        quantise_weight(2)
+        be2_all = keep.tile([P, WIDTH], BF16)
+        nc.sync.dma_start(out=be2_all[:], in_=be2.partition_broadcast(P))
+
+        sums = keep.tile([P, VECTOR_GRAPHS, F_TILES, PAIRS], F32)
+        flipped = {}
+        terms = {}
+        pre = {}
+        h_grouped = {}
+        h_words = {}
+
+        def flip_terms(b):
+            flipped[b] = psum_flip.tile([P, F_TILES, P], BF16, tag="flip", name="flipped")
             for f in range(F_TILES):
-                nc.vector.scalar_tensor_tensor(
-                    out=pre[:, f, :],
-                    in0=dist_all[:, c * CHUNK : (c + 1) * CHUNK],
-                    scalar=vecs[:, F_TILES + f : F_TILES + f + 1],
-                    in1=pre[:, f, :],
-                    op0=ALU.mult,
-                    op1=ALU.add,
-                )
-            h_grouped = work.tile([P, PASSES, CHUNK, PACK], BF16, align_bytes=64)
+                nc.tensor.transpose(flipped[b][:, f, :], stacked[:, f, b, :], ident_bf[:])
+
+        def copy_terms(b):
+            terms[b] = work.tile([P, F_TILES, P], BF16, tag="terms", name="terms")
+            nc.scalar.copy(out=terms[b][:], in_=flipped[b][:])
+
+        def form_pre(u):
+            b, h = divmod(u, HALVES)
+            pre[u] = []
+            for g in range(PASSES):
+                pre_ps = psum_pre.tile([P, PACK, P], F32, tag="pre")
+                for t in range(PACK):
+                    nc.tensor.matmul(
+                        out=pre_ps[:, t, :],
+                        lhsT=terms[b][:, g * PACK + t, :],
+                        rhs=spread[:, b, h * P : (h + 1) * P],
+                        start=True,
+                        stop=True,
+                    )
+                pre[u].append(pre_ps[:])
+
+        def vector_sums(v, f):
+            nodes = slice(v * NODES, (v + 1) * NODES)
+            nc.vector.scalar_tensor_tensor(
+                out=sums[:, v, f, :].rearrange("p (i j) -> p i j", j=NODES),
+                in0=a_last[:, 0, f, nodes].unsqueeze(2).to_broadcast([P, NODES, NODES]),
+                scalar=vecs[:, 0, f : f + 1],
+                in1=a_last[:, 1, f, nodes].unsqueeze(1).to_broadcast([P, NODES, NODES]),
+                op0=ALU.add,
+                op1=ALU.add,
+            )
+            nc.vector.scalar_tensor_tensor(
+                out=sums[:, v, f, :],
+                in0=dist_all[:, v, :],
+                scalar=vecs[:, 1, f : f + 1],
+                in1=sums[:, v, f, :],
+                op0=ALU.mult,
+                op1=ALU.add,
+            )
+
+        def activate(u):
+            if u >= TENSOR_UNITS:
+                v, h = divmod(u - TENSOR_UNITS, HALVES)
+                pre[u] = [sums[:, v, g * PACK : (g + 1) * PACK, h * P : (h + 1) * P] for g in range(PASSES)]
+            grouped = work.tile([P, PASSES, P, PACK], BF16, align_bytes=64, tag="h_grouped")
             for g in range(PASSES):
                 nc.scalar.activation(
-                    out=h_grouped[:, g, :, :],
-                    in_=pre[:, g * PACK : (g + 1) * PACK, :].rearrange("p t r -> p r t"),
-                    func=ACT.Silu,
+                    out=grouped[:, g, :, :], in_=pre[u][g].rearrange("p t r -> p r t"), func=ACT.Silu
                 )
-            h_codes = work.tile([P, PASSES, CHUNK], U32, align_bytes=64)
-            h_scales = work.tile([P, PASSES, CHUNK], U8, align_bytes=64)
+            return grouped
+
+        def quantise(grouped):
+            h_codes = work.tile([P, PASSES, P], U32, align_bytes=64)
+            h_scales = work.tile([P, PASSES, P], U8, align_bytes=64)
             nc.vector.quantize_mx(
                 out=h_codes[:].rearrange("p g r -> p (g r)").bitcast(FP8X4),
                 scales=h_scales[:].rearrange("p g r -> p (g r)"),
-                in_=h_grouped[:].rearrange("p g r t -> p (g r t)"),
+                in_=grouped[:].rearrange("p g r t -> p (g r t)"),
             )
-            for r in range(CHUNK // P):
-                msg = store_pool.tile([P, WIDTH], F32)
-                for m in range(WIDTH // BANK):
-                    acc = psum.tile([P, BANK], F32, tag="acc")
-                    for g in range(PASSES):
-                        nc.tensor.matmul_mx(
-                            out=acc[:],
-                            lhsT=h_codes[:, g, r * P : (r + 1) * P].bitcast(FP8X4),
-                            lhsT_scale=h_scales[:, g, r * P : (r + 1) * P],
-                            rhs=w_codes[:, 2 * PASSES + g, m * BANK : (m + 1) * BANK].bitcast(FP8X4),
-                            rhs_scale=w_scales[:, 2 * PASSES + g, m * BANK : (m + 1) * BANK],
-                            start=(g == 0),
-                            stop=(g == PASSES - 1),
-                        )
-                    nc.vector.tensor_tensor(
-                        out=msg[:, m * BANK : (m + 1) * BANK],
-                        in0=acc[:],
-                        in1=be2_all[:, m * BANK : (m + 1) * BANK],
-                        op=ALU.add,
+            return h_codes, h_scales
+
+        def multiply(u, words):
+            h_codes, h_scales = words
+            msg = store_pool.tile([P, WIDTH], F32)
+            for m in range(WIDTH // BANK):
+                acc = psum_acc.tile([P, BANK], F32, tag="acc")
+                for g in range(PASSES):
+                    nc.tensor.matmul_mx(
+                        out=acc[:],
+                        lhsT=h_codes[:, g, :].bitcast(FP8X4),
+                        lhsT_scale=h_scales[:, g, :],
+                        rhs=w_codes[:, 2 * PASSES + g, m * BANK : (m + 1) * BANK].bitcast(FP8X4),
+                        rhs_scale=w_scales[:, 2 * PASSES + g, m * BANK : (m + 1) * BANK],
+                        start=(g == 0),
+                        stop=(g == PASSES - 1),
                     )
-                row0 = c * CHUNK + r * P
-                nc.sync.dma_start(out=out_rows[row0 : row0 + P, :], in_=msg[:])
+                nc.vector.tensor_tensor(
+                    out=msg[:, m * BANK : (m + 1) * BANK],
+                    in0=acc[:],
+                    in1=be2_all[:, m * BANK : (m + 1) * BANK],
+                    op=ALU.add,
+                )
+            nc.sync.dma_start(out=out_rows[u * P : (u + 1) * P, :], in_=msg[:])
+
+        with tc.manual_schedule():
+            flip_terms(0)
+            copy_terms(0)
+            form_pre(0)
+            flip_terms(1)
+            for u in range(UNITS + 2):
+                if u % HALVES == 0 and u // HALVES + 1 < TENSOR_GRAPHS:
+                    copy_terms(u // HALVES + 1)
+                if u < UNITS:
+                    h_grouped[u] = activate(u)
+                if u + 1 < TENSOR_UNITS:
+                    form_pre(u + 1)
+                if 1 <= u <= UNITS:
+                    h_words[u - 1] = quantise(h_grouped[u - 1])
+                if u < VECTOR_GRAPHS * F_TILES:
+                    vector_sums(u // F_TILES, u % F_TILES)
+                if u >= 2:
+                    multiply(u - 2, h_words[u - 2])
+                if u % HALVES == 1 and (u + 3) // HALVES < TENSOR_GRAPHS:
+                    flip_terms((u + 3) // HALVES)

@@ -27,6 +27,7 @@ HALVES = PAIRS // P
 HALF = NODES // HALVES
 BANK = 512
 RUN = 4
+RAW_BUFS = 4
 TINY = 1e-30
 
 HI = 0
@@ -48,7 +49,7 @@ def tile_graphmessagelayer_pa_kernel(tc, node_state, positions, We1, be1, We2, b
 
     with ExitStack() as ctx:
         keep = ctx.enter_context(tc.tile_pool(name="keep", bufs=1))
-        raw_pool = ctx.enter_context(tc.tile_pool(name="raw", bufs=4))
+        raw_pool = ctx.enter_context(tc.tile_pool(name="raw", bufs=RAW_BUFS))
         grouped_pool = ctx.enter_context(tc.tile_pool(name="grouped", bufs=2))
         work = ctx.enter_context(tc.tile_pool(name="work", bufs=4))
         store_pool = ctx.enter_context(tc.tile_pool(name="store", bufs=6))
@@ -56,21 +57,105 @@ def tile_graphmessagelayer_pa_kernel(tc, node_state, positions, We1, be1, We2, b
         psum_pre = ctx.enter_context(tc.psum_pool(name="psum_pre", bufs=4))
         psum_acc = ctx.enter_context(tc.psum_pool(name="psum_acc", bufs=3))
 
-        vec_rows = keep.tile([P, P], BF16)
-        nc.vector.memset(vec_rows[:], 0.0)
-        pos_nodes = keep.tile([P, 64], BF16)
-        nc.vector.memset(pos_nodes[:], 0.0)
-        stacked = keep.tile([P, F_TILES, GRAPHS, P], BF16)
-        stacked_words = stacked[:].rearrange("p f b c -> p (f b c)").bitcast(I32).rearrange("p (r c) -> p r c", c=P // 2)
-        nc.vector.memset(stacked_words[:, :, USED // 2 : P // 2], 0)
-        dist_cols = keep.tile([P, HALVES, GRAPHS, P], BF16)
-        nc.vector.memset(dist_cols[:].rearrange("p h b c -> p (h b c)").bitcast(I32), 0)
-        nc.vector.memset(dist_cols[:, :, :, ONE : ONE + 1], 1.0)
+        ctx.enter_context(tc.manual_schedule())
 
+        vec_rows = keep.tile([P, P], BF16)
+        pos_nodes = keep.tile([P, 64], BF16)
+        stacked = keep.tile([P, F_TILES, GRAPHS, P], BF16)
+        dist_cols = keep.tile([P, HALVES, GRAPHS, P], BF16)
         x_rows = keep.tile([P, 2, WIDTH], BF16)
-        nc.sync.dma_start(
-            out=x_rows[:], in_=node_state.rearrange("b n h -> (b n) h").rearrange("(a p) h -> p a h", p=P)
-        )
+        ident_bf = keep.tile([P, P], BF16)
+        ident_f = keep.tile([P, P], F32)
+        x_grouped = keep.tile([P, PASSES, ALL_NODES, PACK], BF16, align_bytes=64)
+        x_codes = keep.tile([P, PASSES, ALL_NODES], U32, align_bytes=64)
+        x_scales = keep.tile([P, PASSES, ALL_NODES], U8, align_bytes=64)
+        vecs = keep.tile([P, 2, F_TILES], F32)
+        w_codes = keep.tile([P, 3 * PASSES, WIDTH], U32, align_bytes=64)
+        w_scales = keep.tile([P, 3 * PASSES, WIDTH], U8, align_bytes=64)
+        a_last = keep.tile([P, 2, F_TILES, VECTOR_GRAPHS * NODES], F32)
+        be2_all = keep.tile([P, WIDTH], BF16)
+        spread = keep.tile([P, GRAPHS, PAIRS], BF16)
+        weight_rows = [We1[0:WIDTH, :], We1[WIDTH : 2 * WIDTH, :], We2]
+        raw = {}
+        grouped = {}
+        a_ps = {}
+
+        def load_weight(k):
+            w, g = divmod(k, PASSES)
+            raw[k] = raw_pool.tile([P, PACK, WIDTH], BF16, tag="raw", name="raw")
+            nc.sync.dma_start(
+                out=raw[k][:],
+                in_=weight_rows[w][g * K_PASS : (g + 1) * K_PASS, :].rearrange("(t p) n -> p t n", p=P),
+            )
+
+        def regroup_weight(k):
+            grouped[k] = grouped_pool.tile([P, WIDTH, PACK], BF16, align_bytes=64, tag="grouped", name="grouped")
+            mid = WIDTH // 2
+            nc.vector.tensor_copy(
+                out=grouped[k][:, 0:mid, :].rearrange("p (c i) t -> p c t i", i=RUN),
+                in_=raw[k][:, :, 0:mid].rearrange("p t (c i) -> p c t i", i=RUN),
+            )
+            nc.scalar.copy(
+                out=grouped[k][:, mid:WIDTH, :].rearrange("p (c i) t -> p c t i", i=RUN),
+                in_=raw[k][:, :, mid:WIDTH].rearrange("p t (c i) -> p c t i", i=RUN),
+            )
+
+        def quantise_weight(k):
+            nc.vector.quantize_mx(
+                out=w_codes[:, k, :].bitcast(FP8X4),
+                scales=w_scales[:, k, :],
+                in_=grouped[k][:].rearrange("p n t -> p (n t)"),
+            )
+
+        def node_products(w):
+            for pair in range(F_TILES // 2):
+                a_ps[w, pair] = psum_pre.tile([P, 2, ALL_NODES], F32, tag="pre", name="a_ps")
+                for e in range(2):
+                    f = 2 * pair + e
+                    for g in range(PASSES):
+                        nc.tensor.matmul_mx(
+                            out=a_ps[w, pair][:, e, :],
+                            lhsT=w_codes[:, w * PASSES + g, f * P : (f + 1) * P].bitcast(FP8X4),
+                            lhsT_scale=w_scales[:, w * PASSES + g, f * P : (f + 1) * P],
+                            rhs=x_codes[:, g, :].bitcast(FP8X4),
+                            rhs_scale=x_scales[:, g, :],
+                            start=(g == 0),
+                            stop=(g == PASSES - 1),
+                        )
+
+        def split_products(w):
+            for pair in range(F_TILES // 2):
+                f_pair = slice(2 * pair, 2 * pair + 2)
+                by_graph = a_ps[w, pair][:].rearrange("p e (b n) -> p e b n", n=NODES)
+                high = stacked[:, f_pair, :, HI + w * NODES : HI + (w + 1) * NODES]
+                nc.scalar.copy(out=high, in_=by_graph)
+                nc.scalar.copy(out=a_last[:, w, f_pair, :], in_=a_ps[w, pair][:, :, TENSOR_GRAPHS * NODES : ALL_NODES])
+                nc.vector.tensor_tensor(
+                    out=stacked[:, f_pair, :, LO + w * NODES : LO + (w + 1) * NODES],
+                    in0=by_graph,
+                    in1=high,
+                    op=ALU.subtract,
+                )
+
+        per_bank = 2 * BANK // P // HALVES
+        dist_t = {}
+
+        def flip_spread(q):
+            dist_t[q] = psum_acc.tile([P, per_bank, HALVES, P], BF16, tag="acc", name="dist_t")
+            for k in range(per_bank):
+                for h in range(HALVES):
+                    nc.tensor.transpose(dist_t[q][:, k, h, :], dist_cols[:, h, q * per_bank + k, :], ident_bf[:])
+
+        def copy_spread(q):
+            nc.scalar.copy(
+                out=spread[DIST:P, q * per_bank : (q + 1) * per_bank, :].rearrange("p b q -> p (b q)"),
+                in_=dist_t[q][DIST:P, :, :, :].rearrange("p k h n -> p (k h n)"),
+            )
+
+        warm = keep.tile([P, 2], F32)
+        nc.vector.memset(warm[:], 1.0)
+        nc.vector.memset(vec_rows[:], 0.0)
+        nc.vector.memset(pos_nodes[:], 0.0)
         nc.scalar.dma_start(out=vec_rows[0:F_TILES, :], in_=be1.rearrange("(r c) -> r c", c=P))
         nc.scalar.dma_start(
             out=vec_rows[F_TILES : 2 * F_TILES, :],
@@ -81,13 +166,43 @@ def tile_graphmessagelayer_pa_kernel(tc, node_state, positions, We1, be1, We2, b
                 out=pos_nodes[0:NODES, 0 : GRAPHS * COORDS].rearrange("n (b c) -> n b c", c=COORDS),
                 in_=positions.rearrange("b n c -> n b c"),
             )
-
-        ident_bf = keep.tile([P, P], BF16)
+        nc.scalar.activation(out=warm[:, 1:2], in_=warm[:, 0:1], func=ACT.Sqrt)
+        nc.sync.dma_start(
+            out=x_rows[:], in_=node_state.rearrange("b n h -> (b n) h").rearrange("(a p) h -> p a h", p=P)
+        )
+        for k in range(RAW_BUFS):
+            load_weight(k)
         make_identity(nc, ident_bf[:])
-        ident_f = keep.tile([P, P], F32)
         make_identity(nc, ident_f[:])
 
-        x_grouped = keep.tile([P, PASSES, ALL_NODES, PACK], BF16, align_bytes=64)
+        stacked_words = stacked[:].rearrange("p f b c -> p (f b c)").bitcast(I32).rearrange("p (r c) -> p r c", c=P // 2)
+        nc.vector.memset(stacked_words[:, :, USED // 2 : P // 2], 0)
+        nc.vector.memset(dist_cols[:].rearrange("p h b c -> p (h b c)").bitcast(I32), 0)
+        nc.vector.memset(dist_cols[:, :, :, ONE : ONE + 1], 1.0)
+        sel = keep.tile([P, HALVES, P], BF16)
+        for h in range(HALVES):
+            nc.vector.tensor_tensor(
+                out=sel[:, h, :].rearrange("p (i j) -> p i j", j=NODES),
+                in0=ident_bf[:, h * HALF : (h + 1) * HALF].unsqueeze(2).to_broadcast([P, HALF, NODES]),
+                in1=ident_bf[:, 0:NODES].unsqueeze(1).to_broadcast([P, HALF, NODES]),
+                op=ALU.subtract,
+            )
+        pick = keep.tile([P, 2 * NODES], BF16)
+        nc.vector.tensor_tensor(
+            out=pick[:], in0=ident_bf[:, HI : HI + 2 * NODES], in1=ident_bf[:, LO : LO + 2 * NODES], op=ALU.add
+        )
+        pick_pairs = keep.tile([P, NODES, NODES], BF16)
+        nc.vector.tensor_tensor(
+            out=pick_pairs[:],
+            in0=pick[:, 0:NODES].unsqueeze(2).to_broadcast([P, NODES, NODES]),
+            in1=pick[:, NODES : 2 * NODES].unsqueeze(1).to_broadcast([P, NODES, NODES]),
+            op=ALU.add,
+        )
+        nc.vector.tensor_copy(
+            out=spread[0:DIST, :, :],
+            in_=pick_pairs[0:DIST, :, :].rearrange("p i j -> p (i j)").unsqueeze(1).to_broadcast([DIST, GRAPHS, PAIRS]),
+        )
+
         for a in range(2):
             for g in range(PASSES):
                 x_t = psum_pre.tile([P, PACK, P], BF16, tag="pre")
@@ -97,17 +212,19 @@ def tile_graphmessagelayer_pa_kernel(tc, node_state, positions, We1, be1, We2, b
                 nc.vector.tensor_copy(
                     out=x_grouped[:, g, a * P : (a + 1) * P, :], in_=x_t[:].rearrange("p t r -> p r t")
                 )
-        x_codes = keep.tile([P, PASSES, ALL_NODES], U32, align_bytes=64)
-        x_scales = keep.tile([P, PASSES, ALL_NODES], U8, align_bytes=64)
+        vec_t = psum_acc.tile([P, P], BF16, tag="acc")
+        nc.tensor.transpose(vec_t[:], vec_rows[:], ident_bf[:])
+        rel = psum_acc.tile([P, HALVES, 64], F32, tag="acc")
+        for h in range(HALVES):
+            nc.tensor.matmul(out=rel[:, h, :], lhsT=sel[:, h, :], rhs=pos_nodes[:], start=True, stop=True)
+
+        regroup_weight(0)
+        load_weight(RAW_BUFS)
         nc.vector.quantize_mx(
             out=x_codes[:].rearrange("p g r -> p (g r)").bitcast(FP8X4),
             scales=x_scales[:].rearrange("p g r -> p (g r)"),
             in_=x_grouped[:].rearrange("p g r t -> p (g r t)"),
         )
-
-        vec_t = psum_pre.tile([P, P], BF16, tag="pre")
-        nc.tensor.transpose(vec_t[:], vec_rows[:], ident_bf[:])
-        vecs = keep.tile([P, 2, F_TILES], F32)
         nc.vector.tensor_copy(out=vecs[:].rearrange("p v f -> p (v f)"), in_=vec_t[:, 0 : 2 * F_TILES])
         nc.vector.tensor_copy(
             out=stacked[:, :, :, DIST:ONE],
@@ -117,20 +234,12 @@ def tile_graphmessagelayer_pa_kernel(tc, node_state, positions, We1, be1, We2, b
             out=stacked[:, :, :, ONE : ONE + 1],
             in_=vecs[:, 0, :].unsqueeze(2).unsqueeze(3).to_broadcast([P, F_TILES, GRAPHS, 1]),
         )
-
-        sel = keep.tile([P, HALVES, P], BF16)
-        for h in range(HALVES):
-            nc.vector.tensor_tensor(
-                out=sel[:, h, :].rearrange("p (i j) -> p i j", j=NODES),
-                in0=ident_bf[:, h * HALF : (h + 1) * HALF].unsqueeze(2).to_broadcast([P, HALF, NODES]),
-                in1=ident_bf[:, 0:NODES].unsqueeze(1).to_broadcast([P, HALF, NODES]),
-                op=ALU.subtract,
-            )
-        rel = psum_pre.tile([P, HALVES, 64], F32, tag="pre")
-        for h in range(HALVES):
-            nc.tensor.matmul(out=rel[:, h, :], lhsT=sel[:, h, :], rhs=pos_nodes[:], start=True, stop=True)
         rel_sq = keep.tile([P, HALVES, 64], F32)
         nc.scalar.activation(out=rel_sq[:], in_=rel[:], func=ACT.Square)
+
+        regroup_weight(1)
+        load_weight(RAW_BUFS + 1)
+        nc.sync.dma_start(out=be2_all[:], in_=be2.partition_broadcast(P))
         sq = keep.tile([P, HALVES, GRAPHS], F32)
         nc.vector.tensor_reduce(
             out=sq[:],
@@ -142,6 +251,11 @@ def tile_graphmessagelayer_pa_kernel(tc, node_state, positions, We1, be1, We2, b
         nc.vector.tensor_scalar_max(out=sq_floor[:], in0=sq[:], scalar1=TINY)
         root = keep.tile([P, HALVES, GRAPHS], F32)
         nc.scalar.activation(out=root[:], in_=sq_floor[:], func=ACT.Sqrt)
+        quantise_weight(0)
+
+        regroup_weight(2)
+        quantise_weight(1)
+        node_products(0)
         dist = keep.tile([P, HALVES, GRAPHS], F32)
         nc.vector.scalar_tensor_tensor(
             out=dist[:].rearrange("p h b -> p (h b)"),
@@ -158,36 +272,6 @@ def tile_graphmessagelayer_pa_kernel(tc, node_state, positions, We1, be1, We2, b
         nc.vector.tensor_tensor(
             out=dist_cols[:, :, :, DIST + 2], in0=rest[:], in1=dist_cols[:, :, :, DIST + 1], op=ALU.subtract
         )
-
-        pick = keep.tile([P, 2 * NODES], BF16)
-        nc.vector.tensor_tensor(
-            out=pick[:], in0=ident_bf[:, HI : HI + 2 * NODES], in1=ident_bf[:, LO : LO + 2 * NODES], op=ALU.add
-        )
-        pick_pairs = keep.tile([P, NODES, NODES], BF16)
-        nc.vector.tensor_tensor(
-            out=pick_pairs[:],
-            in0=pick[:, 0:NODES].unsqueeze(2).to_broadcast([P, NODES, NODES]),
-            in1=pick[:, NODES : 2 * NODES].unsqueeze(1).to_broadcast([P, NODES, NODES]),
-            op=ALU.add,
-        )
-        spread = keep.tile([P, GRAPHS, PAIRS], BF16)
-        nc.vector.tensor_copy(
-            out=spread[0:DIST, :, :],
-            in_=pick_pairs[0:DIST, :, :].rearrange("p i j -> p (i j)").unsqueeze(1).to_broadcast([DIST, GRAPHS, PAIRS]),
-        )
-        per_bank = 2 * BANK // P
-        for q in range(GRAPHS * HALVES // per_bank):
-            dist_t = psum_flip.tile([P, per_bank // HALVES, HALVES, P], BF16, tag="flip")
-            for k in range(per_bank // HALVES):
-                for h in range(HALVES):
-                    b = q * (per_bank // HALVES) + k
-                    nc.tensor.transpose(dist_t[:, k, h, :], dist_cols[:, h, b, :], ident_bf[:])
-            b0 = q * (per_bank // HALVES)
-            nc.scalar.copy(
-                out=spread[DIST:P, b0 : b0 + per_bank // HALVES, :].rearrange("p b q -> p (b q)"),
-                in_=dist_t[DIST:P, :, :, :].rearrange("p k h n -> p (k h n)"),
-            )
-
         dist_rep = keep.tile([P, VECTOR_GRAPHS, HALVES, P], F32)
         nc.vector.tensor_copy(
             out=dist_rep[:],
@@ -195,74 +279,25 @@ def tile_graphmessagelayer_pa_kernel(tc, node_state, positions, We1, be1, We2, b
                 [P, VECTOR_GRAPHS, HALVES, P]
             ),
         )
-        dist_flip = psum_pre.tile([P, VECTOR_GRAPHS, HALVES, P], F32, tag="pre")
+        for q in range(3):
+            flip_spread(q)
+        dist_flip = psum_flip.tile([P, VECTOR_GRAPHS, HALVES, P], F32, tag="flip")
         for v in range(VECTOR_GRAPHS):
             for h in range(HALVES):
                 nc.tensor.transpose(dist_flip[:, v, h, :], dist_rep[:, v, h, :], ident_f[:])
+
+        regroup_weight(3)
+        quantise_weight(2)
+        quantise_weight(3)
+        split_products(0)
+        node_products(1)
+        for q in range(3):
+            copy_spread(q)
         dist_all = keep.tile([P, VECTOR_GRAPHS, PAIRS], F32)
         nc.scalar.copy(out=dist_all[:].rearrange("p v q -> p (v q)"), in_=dist_flip[:].rearrange("p v h n -> p (v h n)"))
-
-        w_codes = keep.tile([P, 3 * PASSES, WIDTH], U32, align_bytes=64)
-        w_scales = keep.tile([P, 3 * PASSES, WIDTH], U8, align_bytes=64)
-        a_last = keep.tile([P, 2, F_TILES, VECTOR_GRAPHS * NODES], F32)
-        weight_rows = [We1[0:WIDTH, :], We1[WIDTH : 2 * WIDTH, :], We2]
-        def quantise_weight(w):
-            for g in range(PASSES):
-                raw = raw_pool.tile([P, PACK, WIDTH], BF16)
-                nc.sync.dma_start(
-                    out=raw[:],
-                    in_=weight_rows[w][g * K_PASS : (g + 1) * K_PASS, :].rearrange("(t p) n -> p t n", p=P),
-                )
-                grouped = grouped_pool.tile([P, WIDTH, PACK], BF16, align_bytes=64)
-                mid = WIDTH // 2
-                nc.vector.tensor_copy(
-                    out=grouped[:, 0:mid, :].rearrange("p (c i) t -> p c t i", i=RUN),
-                    in_=raw[:, :, 0:mid].rearrange("p t (c i) -> p c t i", i=RUN),
-                )
-                nc.scalar.copy(
-                    out=grouped[:, mid:WIDTH, :].rearrange("p (c i) t -> p c t i", i=RUN),
-                    in_=raw[:, :, mid:WIDTH].rearrange("p t (c i) -> p c t i", i=RUN),
-                )
-                nc.vector.quantize_mx(
-                    out=w_codes[:, w * PASSES + g, :].bitcast(FP8X4),
-                    scales=w_scales[:, w * PASSES + g, :],
-                    in_=grouped[:].rearrange("p n t -> p (n t)"),
-                )
-
-        def node_products(w):
-            for pair in range(F_TILES // 2):
-                a_ps = psum_pre.tile([P, 2, ALL_NODES], F32, tag="pre")
-                for e in range(2):
-                    f = 2 * pair + e
-                    for g in range(PASSES):
-                        nc.tensor.matmul_mx(
-                            out=a_ps[:, e, :],
-                            lhsT=w_codes[:, w * PASSES + g, f * P : (f + 1) * P].bitcast(FP8X4),
-                            lhsT_scale=w_scales[:, w * PASSES + g, f * P : (f + 1) * P],
-                            rhs=x_codes[:, g, :].bitcast(FP8X4),
-                            rhs_scale=x_scales[:, g, :],
-                            start=(g == 0),
-                            stop=(g == PASSES - 1),
-                        )
-                f_pair = slice(2 * pair, 2 * pair + 2)
-                by_graph = a_ps[:].rearrange("p e (b n) -> p e b n", n=NODES)
-                high = stacked[:, f_pair, :, HI + w * NODES : HI + (w + 1) * NODES]
-                nc.scalar.copy(out=high, in_=by_graph)
-                nc.vector.tensor_tensor(
-                    out=stacked[:, f_pair, :, LO + w * NODES : LO + (w + 1) * NODES],
-                    in0=by_graph,
-                    in1=high,
-                    op=ALU.subtract,
-                )
-                nc.scalar.copy(out=a_last[:, w, f_pair, :], in_=a_ps[:, :, TENSOR_GRAPHS * NODES : ALL_NODES])
-
-        quantise_weight(0)
-        node_products(0)
-        quantise_weight(1)
-        node_products(1)
-        quantise_weight(2)
-        be2_all = keep.tile([P, WIDTH], BF16)
-        nc.sync.dma_start(out=be2_all[:], in_=be2.partition_broadcast(P))
+        flip_spread(3)
+        split_products(1)
+        copy_spread(3)
 
         sums = keep.tile([P, VECTOR_GRAPHS, F_TILES, PAIRS], F32)
         flipped = {}
@@ -295,23 +330,28 @@ def tile_graphmessagelayer_pa_kernel(tc, node_state, positions, We1, be1, We2, b
                     )
                 pre[u].append(pre_ps[:])
 
-        def vector_sums(v, f):
+        def side_sums(v, f):
             nodes = slice(v * NODES, (v + 1) * NODES)
-            nc.vector.scalar_tensor_tensor(
-                out=sums[:, v, f, :].rearrange("p (i j) -> p i j", j=NODES),
-                in0=a_last[:, 0, f, nodes].unsqueeze(2).to_broadcast([P, NODES, NODES]),
-                scalar=vecs[:, 0, f : f + 1],
-                in1=a_last[:, 1, f, nodes].unsqueeze(1).to_broadcast([P, NODES, NODES]),
-                op0=ALU.add,
-                op1=ALU.add,
-            )
-            nc.vector.scalar_tensor_tensor(
+            by_pair = sums[:, v, f, :].rearrange("p (i j) -> p i j", j=NODES)
+            nc.gpsimd.tensor_scalar(
                 out=sums[:, v, f, :],
                 in0=dist_all[:, v, :],
-                scalar=vecs[:, 1, f : f + 1],
-                in1=sums[:, v, f, :],
+                scalar1=vecs[:, 1, f : f + 1],
+                scalar2=vecs[:, 0, f : f + 1],
                 op0=ALU.mult,
                 op1=ALU.add,
+            )
+            nc.gpsimd.tensor_tensor(
+                out=by_pair,
+                in0=by_pair,
+                in1=a_last[:, 0, f, nodes].unsqueeze(2).to_broadcast([P, NODES, NODES]),
+                op=ALU.add,
+            )
+            nc.gpsimd.tensor_tensor(
+                out=by_pair,
+                in0=by_pair,
+                in1=a_last[:, 1, f, nodes].unsqueeze(1).to_broadcast([P, NODES, NODES]),
+                op=ALU.add,
             )
 
         def activate(u):
@@ -358,23 +398,29 @@ def tile_graphmessagelayer_pa_kernel(tc, node_state, positions, We1, be1, We2, b
                 )
             nc.sync.dma_start(out=out_rows[u * P : (u + 1) * P, :], in_=msg[:])
 
-        with tc.manual_schedule():
-            flip_terms(0)
-            copy_terms(0)
-            form_pre(0)
-            flip_terms(1)
-            for u in range(UNITS + 2):
-                if u % HALVES == 0 and u // HALVES + 1 < TENSOR_GRAPHS:
-                    copy_terms(u // HALVES + 1)
-                if u < UNITS:
-                    h_grouped[u] = activate(u)
-                if u + 1 < TENSOR_UNITS:
-                    form_pre(u + 1)
-                if 1 <= u <= UNITS:
-                    h_words[u - 1] = quantise(h_grouped[u - 1])
-                if u < VECTOR_GRAPHS * F_TILES:
-                    vector_sums(u // F_TILES, u % F_TILES)
-                if u >= 2:
-                    multiply(u - 2, h_words[u - 2])
-                if u % HALVES == 1 and (u + 3) // HALVES < TENSOR_GRAPHS:
-                    flip_terms((u + 3) // HALVES)
+        flip_terms(0)
+        copy_terms(0)
+        form_pre(0)
+        flip_terms(1)
+        copy_terms(1)
+        regroup_weight(4)
+        regroup_weight(5)
+        quantise_weight(4)
+        quantise_weight(5)
+        for v in range(VECTOR_GRAPHS):
+            for f in range(F_TILES):
+                side_sums(v, f)
+
+        for u in range(UNITS + 2):
+            if u < UNITS:
+                h_grouped[u] = activate(u)
+            if u % HALVES == 1 and (u + 3) // HALVES < TENSOR_GRAPHS:
+                copy_terms((u + 3) // HALVES)
+            if u + 1 < TENSOR_UNITS:
+                form_pre(u + 1)
+            if 1 <= u <= UNITS:
+                h_words[u - 1] = quantise(h_grouped[u - 1])
+            if u >= 2:
+                multiply(u - 2, h_words[u - 2])
+            if u % HALVES == 0 and u // HALVES + 2 < TENSOR_GRAPHS:
+                flip_terms(u // HALVES + 2)

@@ -27,8 +27,8 @@ HALVES = PAIRS // P
 HALF = NODES // HALVES
 BANK = 512
 RUN = 4
+VECTOR_COLUMNS = 640
 RAW_BUFS = 4
-TINY = 1e-30
 
 HI = 0
 LO = 32
@@ -90,7 +90,7 @@ def tile_graphmessagelayer_pa_kernel(tc, node_state, positions, We1, be1, We2, b
 
         def regroup_weight(k):
             grouped[k] = grouped_pool.tile([P, WIDTH, PACK], BF16, align_bytes=64, tag="grouped", name="grouped")
-            mid = WIDTH // 2
+            mid = VECTOR_COLUMNS
             nc.vector.tensor_copy(
                 out=grouped[k][:, 0:mid, :].rearrange("p (c i) t -> p c t i", i=RUN),
                 in_=raw[k][:, :, 0:mid].rearrange("p t (c i) -> p c t i", i=RUN),
@@ -126,12 +126,12 @@ def tile_graphmessagelayer_pa_kernel(tc, node_state, positions, We1, be1, We2, b
         def split_products(w):
             for pair in range(F_TILES // 2):
                 f_pair = slice(2 * pair, 2 * pair + 2)
-                by_graph = a_ps[w, pair][:].rearrange("p e (b n) -> p e b n", n=NODES)
-                high = stacked[:, f_pair, :, HI + w * NODES : HI + (w + 1) * NODES]
+                by_graph = a_ps[w, pair][:, :, 0 : TENSOR_GRAPHS * NODES].rearrange("p e (b n) -> p e b n", n=NODES)
+                high = stacked[:, f_pair, 0:TENSOR_GRAPHS, HI + w * NODES : HI + (w + 1) * NODES]
                 nc.scalar.copy(out=high, in_=by_graph)
                 nc.scalar.copy(out=a_last[:, w, f_pair, :], in_=a_ps[w, pair][:, :, TENSOR_GRAPHS * NODES : ALL_NODES])
                 nc.vector.tensor_tensor(
-                    out=stacked[:, f_pair, :, LO + w * NODES : LO + (w + 1) * NODES],
+                    out=stacked[:, f_pair, 0:TENSOR_GRAPHS, LO + w * NODES : LO + (w + 1) * NODES],
                     in0=by_graph,
                     in1=high,
                     op=ALU.subtract,
@@ -148,12 +148,14 @@ def tile_graphmessagelayer_pa_kernel(tc, node_state, positions, We1, be1, We2, b
 
         def copy_spread(q):
             nc.scalar.copy(
-                out=spread[DIST:P, q * per_bank : (q + 1) * per_bank, :].rearrange("p b q -> p (b q)"),
-                in_=dist_t[q][DIST:P, :, :, :].rearrange("p k h n -> p (k h n)"),
+                out=spread[:, q * per_bank : (q + 1) * per_bank, :].rearrange("p b q -> p (b q)"),
+                in_=dist_t[q][:].rearrange("p k h n -> p (k h n)"),
             )
 
         warm = keep.tile([P, 2], F32)
         nc.vector.memset(warm[:], 1.0)
+        halves = keep.tile([P, HALVES, GRAPHS], F32)
+        nc.vector.memset(halves[:], 0.5)
         nc.vector.memset(vec_rows[:], 0.0)
         nc.vector.memset(pos_nodes[:], 0.0)
         nc.scalar.dma_start(out=vec_rows[0:F_TILES, :], in_=be1.rearrange("(r c) -> r c", c=P))
@@ -166,41 +168,48 @@ def tile_graphmessagelayer_pa_kernel(tc, node_state, positions, We1, be1, We2, b
                 out=pos_nodes[0:NODES, 0 : GRAPHS * COORDS].rearrange("n (b c) -> n b c", c=COORDS),
                 in_=positions.rearrange("b n c -> n b c"),
             )
-        nc.scalar.activation(out=warm[:, 1:2], in_=warm[:, 0:1], func=ACT.Sqrt)
+        nc.scalar.activation(out=warm[:, 1:2], in_=warm[:, 0:1], func=ACT.Silu)
+        load_weight(0)
         nc.sync.dma_start(
             out=x_rows[:], in_=node_state.rearrange("b n h -> (b n) h").rearrange("(a p) h -> p a h", p=P)
         )
-        for k in range(RAW_BUFS):
+        for k in range(1, RAW_BUFS):
             load_weight(k)
         make_identity(nc, ident_bf[:])
         make_identity(nc, ident_f[:])
 
         stacked_words = stacked[:].rearrange("p f b c -> p (f b c)").bitcast(I32).rearrange("p (r c) -> p r c", c=P // 2)
-        nc.vector.memset(stacked_words[:, :, USED // 2 : P // 2], 0)
-        nc.vector.memset(dist_cols[:].rearrange("p h b c -> p (h b c)").bitcast(I32), 0)
+        nc.vector.memset(stacked_words[:, :, DIST // 2 : P // 2], 0)
+        dist_words = dist_cols[:].rearrange("p h b c -> p (h b c)").bitcast(I32).rearrange("p (r c) -> p r c", c=P // 2)
+        nc.vector.memset(dist_words[:, :, DIST // 2 : P // 2], 0)
         nc.vector.memset(dist_cols[:, :, :, ONE : ONE + 1], 1.0)
         sel = keep.tile([P, HALVES, P], BF16)
         for h in range(HALVES):
-            nc.vector.tensor_tensor(
+            nc.gpsimd.tensor_tensor(
                 out=sel[:, h, :].rearrange("p (i j) -> p i j", j=NODES),
                 in0=ident_bf[:, h * HALF : (h + 1) * HALF].unsqueeze(2).to_broadcast([P, HALF, NODES]),
                 in1=ident_bf[:, 0:NODES].unsqueeze(1).to_broadcast([P, HALF, NODES]),
                 op=ALU.subtract,
             )
         pick = keep.tile([P, 2 * NODES], BF16)
-        nc.vector.tensor_tensor(
+        nc.gpsimd.tensor_tensor(
             out=pick[:], in0=ident_bf[:, HI : HI + 2 * NODES], in1=ident_bf[:, LO : LO + 2 * NODES], op=ALU.add
         )
         pick_pairs = keep.tile([P, NODES, NODES], BF16)
-        nc.vector.tensor_tensor(
+        nc.gpsimd.tensor_tensor(
             out=pick_pairs[:],
             in0=pick[:, 0:NODES].unsqueeze(2).to_broadcast([P, NODES, NODES]),
             in1=pick[:, NODES : 2 * NODES].unsqueeze(1).to_broadcast([P, NODES, NODES]),
             op=ALU.add,
         )
-        nc.vector.tensor_copy(
-            out=spread[0:DIST, :, :],
-            in_=pick_pairs[0:DIST, :, :].rearrange("p i j -> p (i j)").unsqueeze(1).to_broadcast([DIST, GRAPHS, PAIRS]),
+        pick_t = psum_acc.tile([P, HALVES, P], BF16, tag="acc")
+        for h in range(HALVES):
+            nc.tensor.transpose(
+                pick_t[:, h, :], pick_pairs[:, h * HALF : (h + 1) * HALF, :].rearrange("p i j -> p (i j)"), ident_bf[:]
+            )
+        nc.scalar.copy(
+            out=dist_cols[:, :, :, 0:DIST],
+            in_=pick_t[:, :, 0:DIST].unsqueeze(2).to_broadcast([P, HALVES, GRAPHS, DIST]),
         )
 
         for a in range(2):
@@ -209,9 +218,7 @@ def tile_graphmessagelayer_pa_kernel(tc, node_state, positions, We1, be1, We2, b
                 for t in range(PACK):
                     k0 = g * K_PASS + t * P
                     nc.tensor.transpose(x_t[:, t, :], x_rows[:, a, k0 : k0 + P], ident_bf[:])
-                nc.vector.tensor_copy(
-                    out=x_grouped[:, g, a * P : (a + 1) * P, :], in_=x_t[:].rearrange("p t r -> p r t")
-                )
+                nc.scalar.copy(out=x_grouped[:, g, a * P : (a + 1) * P, :], in_=x_t[:].rearrange("p t r -> p r t"))
         vec_t = psum_acc.tile([P, P], BF16, tag="acc")
         nc.tensor.transpose(vec_t[:], vec_rows[:], ident_bf[:])
         rel = psum_acc.tile([P, HALVES, 64], F32, tag="acc")
@@ -226,11 +233,11 @@ def tile_graphmessagelayer_pa_kernel(tc, node_state, positions, We1, be1, We2, b
             in_=x_grouped[:].rearrange("p g r t -> p (g r t)"),
         )
         nc.vector.tensor_copy(out=vecs[:].rearrange("p v f -> p (v f)"), in_=vec_t[:, 0 : 2 * F_TILES])
-        nc.vector.tensor_copy(
+        nc.gpsimd.tensor_copy(
             out=stacked[:, :, :, DIST:ONE],
             in_=vecs[:, 1, :].unsqueeze(2).unsqueeze(3).to_broadcast([P, F_TILES, GRAPHS, ONE - DIST]),
         )
-        nc.vector.tensor_copy(
+        nc.gpsimd.tensor_copy(
             out=stacked[:, :, :, ONE : ONE + 1],
             in_=vecs[:, 0, :].unsqueeze(2).unsqueeze(3).to_broadcast([P, F_TILES, GRAPHS, 1]),
         )
@@ -247,24 +254,16 @@ def tile_graphmessagelayer_pa_kernel(tc, node_state, positions, We1, be1, We2, b
             axis=mybir.AxisListType.X,
             op=ALU.add,
         )
-        sq_floor = keep.tile([P, HALVES, GRAPHS], F32)
-        nc.vector.tensor_scalar_max(out=sq_floor[:], in0=sq[:], scalar1=TINY)
-        root = keep.tile([P, HALVES, GRAPHS], F32)
-        nc.scalar.activation(out=root[:], in_=sq_floor[:], func=ACT.Sqrt)
+        dist = keep.tile([P, HALVES, GRAPHS], F32)
+        nc.gpsimd.tensor_tensor(out=dist[:], in0=sq[:], in1=halves[:], op=ALU.pow)
         quantise_weight(0)
 
         regroup_weight(2)
         quantise_weight(1)
         node_products(0)
-        dist = keep.tile([P, HALVES, GRAPHS], F32)
-        nc.vector.scalar_tensor_tensor(
-            out=dist[:].rearrange("p h b -> p (h b)"),
-            in0=sq[:].rearrange("p h b -> p (h b)"),
-            scalar=0.0,
-            in1=root[:].rearrange("p h b -> p (h b)"),
-            op0=ALU.is_gt,
-            op1=ALU.mult,
-        )
+        regroup_weight(3)
+        quantise_weight(2)
+        quantise_weight(3)
         rest = keep.tile([P, HALVES, GRAPHS], F32)
         nc.vector.tensor_copy(out=dist_cols[:, :, :, DIST], in_=dist[:])
         nc.vector.tensor_tensor(out=rest[:], in0=dist[:], in1=dist_cols[:, :, :, DIST], op=ALU.subtract)
@@ -273,7 +272,7 @@ def tile_graphmessagelayer_pa_kernel(tc, node_state, positions, We1, be1, We2, b
             out=dist_cols[:, :, :, DIST + 2], in0=rest[:], in1=dist_cols[:, :, :, DIST + 1], op=ALU.subtract
         )
         dist_rep = keep.tile([P, VECTOR_GRAPHS, HALVES, P], F32)
-        nc.vector.tensor_copy(
+        nc.gpsimd.tensor_copy(
             out=dist_rep[:],
             in_=dist[:, :, TENSOR_GRAPHS:GRAPHS].rearrange("p h b -> p b h").unsqueeze(3).to_broadcast(
                 [P, VECTOR_GRAPHS, HALVES, P]
@@ -281,23 +280,19 @@ def tile_graphmessagelayer_pa_kernel(tc, node_state, positions, We1, be1, We2, b
         )
         for q in range(3):
             flip_spread(q)
-        dist_flip = psum_flip.tile([P, VECTOR_GRAPHS, HALVES, P], F32, tag="flip")
+        split_products(0)
+        node_products(1)
+        regroup_weight(4)
+        for q in range(3):
+            copy_spread(q)
+        flip_spread(3)
+        dist_flip = psum_acc.tile([P, VECTOR_GRAPHS, HALVES, P], F32, tag="acc")
         for v in range(VECTOR_GRAPHS):
             for h in range(HALVES):
                 nc.tensor.transpose(dist_flip[:, v, h, :], dist_rep[:, v, h, :], ident_f[:])
-
-        regroup_weight(3)
-        quantise_weight(2)
-        quantise_weight(3)
-        split_products(0)
-        node_products(1)
-        for q in range(3):
-            copy_spread(q)
-        dist_all = keep.tile([P, VECTOR_GRAPHS, PAIRS], F32)
-        nc.scalar.copy(out=dist_all[:].rearrange("p v q -> p (v q)"), in_=dist_flip[:].rearrange("p v h n -> p (v h n)"))
-        flip_spread(3)
         split_products(1)
-        copy_spread(3)
+        regroup_weight(5)
+        quantise_weight(4)
 
         sums = keep.tile([P, VECTOR_GRAPHS, F_TILES, PAIRS], F32)
         flipped = {}
@@ -402,10 +397,10 @@ def tile_graphmessagelayer_pa_kernel(tc, node_state, positions, We1, be1, We2, b
         copy_terms(0)
         form_pre(0)
         flip_terms(1)
+        copy_spread(3)
+        dist_all = keep.tile([P, VECTOR_GRAPHS, PAIRS], F32)
+        nc.scalar.copy(out=dist_all[:].rearrange("p v q -> p (v q)"), in_=dist_flip[:].rearrange("p v h n -> p (v h n)"))
         copy_terms(1)
-        regroup_weight(4)
-        regroup_weight(5)
-        quantise_weight(4)
         quantise_weight(5)
         for v in range(VECTOR_GRAPHS):
             for f in range(F_TILES):
@@ -416,11 +411,11 @@ def tile_graphmessagelayer_pa_kernel(tc, node_state, positions, We1, be1, We2, b
                 h_grouped[u] = activate(u)
             if u % HALVES == 1 and (u + 3) // HALVES < TENSOR_GRAPHS:
                 copy_terms((u + 3) // HALVES)
-            if u + 1 < TENSOR_UNITS:
-                form_pre(u + 1)
             if 1 <= u <= UNITS:
                 h_words[u - 1] = quantise(h_grouped[u - 1])
             if u >= 2:
                 multiply(u - 2, h_words[u - 2])
+            if u + 1 < TENSOR_UNITS:
+                form_pre(u + 1)
             if u % HALVES == 0 and u // HALVES + 2 < TENSOR_GRAPHS:
                 flip_terms(u // HALVES + 2)

@@ -15,6 +15,7 @@ ACT = mybir.ActivationFunctionType
 P = 128
 PACK = 4
 K_PASS = P * PACK
+BANK = 512
 GRAPHS = 16
 NODES = 16
 COORDS = 3
@@ -22,23 +23,32 @@ WIDTH = 1024
 PASSES = WIDTH // K_PASS
 F_TILES = WIDTH // P
 ALL_NODES = GRAPHS * NODES
+NODE_TILES = ALL_NODES // P
+F_PER_BANK = BANK // ALL_NODES
 PAIRS = NODES * NODES
 HALVES = PAIRS // P
 HALF = NODES // HALVES
-BANK = 512
-RUN = 4
-VECTOR_COLUMNS = 640
-RAW_BUFS = 4
+POS_COLUMNS = 64
+TINY = 1e-30
 
 HI = 0
 LO = 32
 DIST = 64
 ONE = 67
-USED = 68
-VECTOR_GRAPHS = 2
-TENSOR_GRAPHS = GRAPHS - VECTOR_GRAPHS
+
+SIDE_GRAPHS = 2
+TENSOR_GRAPHS = GRAPHS - SIDE_GRAPHS
 UNITS = GRAPHS * HALVES
 TENSOR_UNITS = TENSOR_GRAPHS * HALVES
+
+RUN = 4
+VECTOR_COLUMNS = 640
+RAW_BUFS = 4
+PRE_BANKS = 4
+ACC_BANKS = 3
+SPREAD_GRAPHS = 2 * BANK // PAIRS
+
+assert GRAPHS // SPREAD_GRAPHS == ACC_BANKS + 1
 
 FLOPS = 2 * ALL_NODES * WIDTH * 2 * WIDTH + 2 * GRAPHS * PAIRS * WIDTH * WIDTH
 
@@ -46,6 +56,7 @@ FLOPS = 2 * ALL_NODES * WIDTH * 2 * WIDTH + 2 * GRAPHS * PAIRS * WIDTH * WIDTH
 def tile_graphmessagelayer_pa_kernel(tc, node_state, positions, We1, be1, We2, be2, out):
     nc = tc.nc
     out_rows = out.rearrange("b i j m -> (b i j) m")
+    weight_rows = [We1[0:WIDTH, :], We1[WIDTH : 2 * WIDTH, :], We2]
 
     with ExitStack() as ctx:
         keep = ctx.enter_context(tc.tile_pool(name="keep", bufs=1))
@@ -54,16 +65,16 @@ def tile_graphmessagelayer_pa_kernel(tc, node_state, positions, We1, be1, We2, b
         work = ctx.enter_context(tc.tile_pool(name="work", bufs=4))
         store_pool = ctx.enter_context(tc.tile_pool(name="store", bufs=6))
         psum_flip = ctx.enter_context(tc.psum_pool(name="psum_flip", bufs=1))
-        psum_pre = ctx.enter_context(tc.psum_pool(name="psum_pre", bufs=4))
-        psum_acc = ctx.enter_context(tc.psum_pool(name="psum_acc", bufs=3))
-
+        psum_pre = ctx.enter_context(tc.psum_pool(name="psum_pre", bufs=PRE_BANKS))
+        psum_acc = ctx.enter_context(tc.psum_pool(name="psum_acc", bufs=ACC_BANKS))
         ctx.enter_context(tc.manual_schedule())
 
         vec_rows = keep.tile([P, P], BF16)
-        pos_nodes = keep.tile([P, 64], BF16)
+        pos_nodes = keep.tile([P, POS_COLUMNS], BF16)
         stacked = keep.tile([P, F_TILES, GRAPHS, P], BF16)
-        dist_cols = keep.tile([P, HALVES, GRAPHS, P], BF16)
-        x_rows = keep.tile([P, 2, WIDTH], BF16)
+        spread_t = keep.tile([P, HALVES, GRAPHS, P], BF16)
+        spread = keep.tile([P, GRAPHS, PAIRS], BF16)
+        x_rows = keep.tile([P, NODE_TILES, WIDTH], BF16)
         ident_bf = keep.tile([P, P], BF16)
         ident_f = keep.tile([P, P], F32)
         x_grouped = keep.tile([P, PASSES, ALL_NODES, PACK], BF16, align_bytes=64)
@@ -72,13 +83,19 @@ def tile_graphmessagelayer_pa_kernel(tc, node_state, positions, We1, be1, We2, b
         vecs = keep.tile([P, 2, F_TILES], F32)
         w_codes = keep.tile([P, 3 * PASSES, WIDTH], U32, align_bytes=64)
         w_scales = keep.tile([P, 3 * PASSES, WIDTH], U8, align_bytes=64)
-        a_last = keep.tile([P, 2, F_TILES, VECTOR_GRAPHS * NODES], F32)
+        a_side = keep.tile([P, 2, F_TILES, SIDE_GRAPHS * NODES], F32)
+        dist_all = keep.tile([P, SIDE_GRAPHS, PAIRS], F32)
+        sums = keep.tile([P, SIDE_GRAPHS, F_TILES, PAIRS], F32)
         be2_all = keep.tile([P, WIDTH], BF16)
-        spread = keep.tile([P, GRAPHS, PAIRS], BF16)
-        weight_rows = [We1[0:WIDTH, :], We1[WIDTH : 2 * WIDTH, :], We2]
         raw = {}
-        grouped = {}
+        w_grouped = {}
         a_ps = {}
+        spread_ps = {}
+        flipped = {}
+        terms = {}
+        pre = {}
+        h_grouped = {}
+        h_words = {}
 
         def load_weight(k):
             w, g = divmod(k, PASSES)
@@ -89,32 +106,32 @@ def tile_graphmessagelayer_pa_kernel(tc, node_state, positions, We1, be1, We2, b
             )
 
         def regroup_weight(k):
-            grouped[k] = grouped_pool.tile([P, WIDTH, PACK], BF16, align_bytes=64, tag="grouped", name="grouped")
-            mid = VECTOR_COLUMNS
+            w_grouped[k] = grouped_pool.tile([P, WIDTH, PACK], BF16, align_bytes=64, tag="grouped", name="grouped")
+            cut = VECTOR_COLUMNS
             nc.vector.tensor_copy(
-                out=grouped[k][:, 0:mid, :].rearrange("p (c i) t -> p c t i", i=RUN),
-                in_=raw[k][:, :, 0:mid].rearrange("p t (c i) -> p c t i", i=RUN),
+                out=w_grouped[k][:, 0:cut, :].rearrange("p (c i) t -> p c t i", i=RUN),
+                in_=raw[k][:, :, 0:cut].rearrange("p t (c i) -> p c t i", i=RUN),
             )
             nc.scalar.copy(
-                out=grouped[k][:, mid:WIDTH, :].rearrange("p (c i) t -> p c t i", i=RUN),
-                in_=raw[k][:, :, mid:WIDTH].rearrange("p t (c i) -> p c t i", i=RUN),
+                out=w_grouped[k][:, cut:WIDTH, :].rearrange("p (c i) t -> p c t i", i=RUN),
+                in_=raw[k][:, :, cut:WIDTH].rearrange("p t (c i) -> p c t i", i=RUN),
             )
 
         def quantise_weight(k):
             nc.vector.quantize_mx(
                 out=w_codes[:, k, :].bitcast(FP8X4),
                 scales=w_scales[:, k, :],
-                in_=grouped[k][:].rearrange("p n t -> p (n t)"),
+                in_=w_grouped[k][:].rearrange("p n t -> p (n t)"),
             )
 
         def node_products(w):
-            for pair in range(F_TILES // 2):
-                a_ps[w, pair] = psum_pre.tile([P, 2, ALL_NODES], F32, tag="pre", name="a_ps")
-                for e in range(2):
-                    f = 2 * pair + e
+            for bank in range(F_TILES // F_PER_BANK):
+                a_ps[w, bank] = psum_pre.tile([P, F_PER_BANK, ALL_NODES], F32, tag="pre", name="a_ps")
+                for e in range(F_PER_BANK):
+                    f = bank * F_PER_BANK + e
                     for g in range(PASSES):
                         nc.tensor.matmul_mx(
-                            out=a_ps[w, pair][:, e, :],
+                            out=a_ps[w, bank][:, e, :],
                             lhsT=w_codes[:, w * PASSES + g, f * P : (f + 1) * P].bitcast(FP8X4),
                             lhsT_scale=w_scales[:, w * PASSES + g, f * P : (f + 1) * P],
                             rhs=x_codes[:, g, :].bitcast(FP8X4),
@@ -124,182 +141,30 @@ def tile_graphmessagelayer_pa_kernel(tc, node_state, positions, We1, be1, We2, b
                         )
 
         def split_products(w):
-            for pair in range(F_TILES // 2):
-                f_pair = slice(2 * pair, 2 * pair + 2)
-                by_graph = a_ps[w, pair][:, :, 0 : TENSOR_GRAPHS * NODES].rearrange("p e (b n) -> p e b n", n=NODES)
-                high = stacked[:, f_pair, 0:TENSOR_GRAPHS, HI + w * NODES : HI + (w + 1) * NODES]
+            for bank in range(F_TILES // F_PER_BANK):
+                f_range = slice(bank * F_PER_BANK, (bank + 1) * F_PER_BANK)
+                by_graph = a_ps[w, bank][:, :, 0 : TENSOR_GRAPHS * NODES].rearrange("p e (b n) -> p e b n", n=NODES)
+                high = stacked[:, f_range, 0:TENSOR_GRAPHS, HI + w * NODES : HI + (w + 1) * NODES]
                 nc.scalar.copy(out=high, in_=by_graph)
-                nc.scalar.copy(out=a_last[:, w, f_pair, :], in_=a_ps[w, pair][:, :, TENSOR_GRAPHS * NODES : ALL_NODES])
+                nc.scalar.copy(out=a_side[:, w, f_range, :], in_=a_ps[w, bank][:, :, TENSOR_GRAPHS * NODES : ALL_NODES])
                 nc.vector.tensor_tensor(
-                    out=stacked[:, f_pair, 0:TENSOR_GRAPHS, LO + w * NODES : LO + (w + 1) * NODES],
+                    out=stacked[:, f_range, 0:TENSOR_GRAPHS, LO + w * NODES : LO + (w + 1) * NODES],
                     in0=by_graph,
                     in1=high,
                     op=ALU.subtract,
                 )
 
-        per_bank = 2 * BANK // P // HALVES
-        dist_t = {}
-
         def flip_spread(q):
-            dist_t[q] = psum_acc.tile([P, per_bank, HALVES, P], BF16, tag="acc", name="dist_t")
-            for k in range(per_bank):
+            spread_ps[q] = psum_acc.tile([P, SPREAD_GRAPHS, HALVES, P], BF16, tag="acc", name="spread_ps")
+            for k in range(SPREAD_GRAPHS):
                 for h in range(HALVES):
-                    nc.tensor.transpose(dist_t[q][:, k, h, :], dist_cols[:, h, q * per_bank + k, :], ident_bf[:])
+                    nc.tensor.transpose(spread_ps[q][:, k, h, :], spread_t[:, h, q * SPREAD_GRAPHS + k, :], ident_bf[:])
 
         def copy_spread(q):
             nc.scalar.copy(
-                out=spread[:, q * per_bank : (q + 1) * per_bank, :].rearrange("p b q -> p (b q)"),
-                in_=dist_t[q][:].rearrange("p k h n -> p (k h n)"),
+                out=spread[:, q * SPREAD_GRAPHS : (q + 1) * SPREAD_GRAPHS, :].rearrange("p b q -> p (b q)"),
+                in_=spread_ps[q][:].rearrange("p k h n -> p (k h n)"),
             )
-
-        warm = keep.tile([P, 2], F32)
-        nc.vector.memset(warm[:], 1.0)
-        halves = keep.tile([P, HALVES, GRAPHS], F32)
-        nc.vector.memset(halves[:], 0.5)
-        nc.vector.memset(vec_rows[:], 0.0)
-        nc.vector.memset(pos_nodes[:], 0.0)
-        nc.scalar.dma_start(out=vec_rows[0:F_TILES, :], in_=be1.rearrange("(r c) -> r c", c=P))
-        nc.scalar.dma_start(
-            out=vec_rows[F_TILES : 2 * F_TILES, :],
-            in_=We1[2 * WIDTH : 2 * WIDTH + 1, :].rearrange("o (r c) -> (o r) c", c=P),
-        )
-        with nc.allow_non_contiguous_dma(reason="768 small values, once"):
-            nc.scalar.dma_start(
-                out=pos_nodes[0:NODES, 0 : GRAPHS * COORDS].rearrange("n (b c) -> n b c", c=COORDS),
-                in_=positions.rearrange("b n c -> n b c"),
-            )
-        nc.scalar.activation(out=warm[:, 1:2], in_=warm[:, 0:1], func=ACT.Silu)
-        load_weight(0)
-        nc.sync.dma_start(
-            out=x_rows[:], in_=node_state.rearrange("b n h -> (b n) h").rearrange("(a p) h -> p a h", p=P)
-        )
-        for k in range(1, RAW_BUFS):
-            load_weight(k)
-        make_identity(nc, ident_bf[:])
-        make_identity(nc, ident_f[:])
-
-        stacked_words = stacked[:].rearrange("p f b c -> p (f b c)").bitcast(I32).rearrange("p (r c) -> p r c", c=P // 2)
-        nc.vector.memset(stacked_words[:, :, DIST // 2 : P // 2], 0)
-        dist_words = dist_cols[:].rearrange("p h b c -> p (h b c)").bitcast(I32).rearrange("p (r c) -> p r c", c=P // 2)
-        nc.vector.memset(dist_words[:, :, DIST // 2 : P // 2], 0)
-        nc.vector.memset(dist_cols[:, :, :, ONE : ONE + 1], 1.0)
-        sel = keep.tile([P, HALVES, P], BF16)
-        for h in range(HALVES):
-            nc.gpsimd.tensor_tensor(
-                out=sel[:, h, :].rearrange("p (i j) -> p i j", j=NODES),
-                in0=ident_bf[:, h * HALF : (h + 1) * HALF].unsqueeze(2).to_broadcast([P, HALF, NODES]),
-                in1=ident_bf[:, 0:NODES].unsqueeze(1).to_broadcast([P, HALF, NODES]),
-                op=ALU.subtract,
-            )
-        pick = keep.tile([P, 2 * NODES], BF16)
-        nc.gpsimd.tensor_tensor(
-            out=pick[:], in0=ident_bf[:, HI : HI + 2 * NODES], in1=ident_bf[:, LO : LO + 2 * NODES], op=ALU.add
-        )
-        pick_pairs = keep.tile([P, NODES, NODES], BF16)
-        nc.gpsimd.tensor_tensor(
-            out=pick_pairs[:],
-            in0=pick[:, 0:NODES].unsqueeze(2).to_broadcast([P, NODES, NODES]),
-            in1=pick[:, NODES : 2 * NODES].unsqueeze(1).to_broadcast([P, NODES, NODES]),
-            op=ALU.add,
-        )
-        pick_t = psum_acc.tile([P, HALVES, P], BF16, tag="acc")
-        for h in range(HALVES):
-            nc.tensor.transpose(
-                pick_t[:, h, :], pick_pairs[:, h * HALF : (h + 1) * HALF, :].rearrange("p i j -> p (i j)"), ident_bf[:]
-            )
-        nc.scalar.copy(
-            out=dist_cols[:, :, :, 0:DIST],
-            in_=pick_t[:, :, 0:DIST].unsqueeze(2).to_broadcast([P, HALVES, GRAPHS, DIST]),
-        )
-
-        for a in range(2):
-            for g in range(PASSES):
-                x_t = psum_pre.tile([P, PACK, P], BF16, tag="pre")
-                for t in range(PACK):
-                    k0 = g * K_PASS + t * P
-                    nc.tensor.transpose(x_t[:, t, :], x_rows[:, a, k0 : k0 + P], ident_bf[:])
-                nc.scalar.copy(out=x_grouped[:, g, a * P : (a + 1) * P, :], in_=x_t[:].rearrange("p t r -> p r t"))
-        vec_t = psum_acc.tile([P, P], BF16, tag="acc")
-        nc.tensor.transpose(vec_t[:], vec_rows[:], ident_bf[:])
-        rel = psum_acc.tile([P, HALVES, 64], F32, tag="acc")
-        for h in range(HALVES):
-            nc.tensor.matmul(out=rel[:, h, :], lhsT=sel[:, h, :], rhs=pos_nodes[:], start=True, stop=True)
-
-        regroup_weight(0)
-        load_weight(RAW_BUFS)
-        nc.vector.quantize_mx(
-            out=x_codes[:].rearrange("p g r -> p (g r)").bitcast(FP8X4),
-            scales=x_scales[:].rearrange("p g r -> p (g r)"),
-            in_=x_grouped[:].rearrange("p g r t -> p (g r t)"),
-        )
-        nc.vector.tensor_copy(out=vecs[:].rearrange("p v f -> p (v f)"), in_=vec_t[:, 0 : 2 * F_TILES])
-        nc.gpsimd.tensor_copy(
-            out=stacked[:, :, :, DIST:ONE],
-            in_=vecs[:, 1, :].unsqueeze(2).unsqueeze(3).to_broadcast([P, F_TILES, GRAPHS, ONE - DIST]),
-        )
-        nc.gpsimd.tensor_copy(
-            out=stacked[:, :, :, ONE : ONE + 1],
-            in_=vecs[:, 0, :].unsqueeze(2).unsqueeze(3).to_broadcast([P, F_TILES, GRAPHS, 1]),
-        )
-        rel_sq = keep.tile([P, HALVES, 64], F32)
-        nc.scalar.activation(out=rel_sq[:], in_=rel[:], func=ACT.Square)
-
-        regroup_weight(1)
-        load_weight(RAW_BUFS + 1)
-        nc.sync.dma_start(out=be2_all[:], in_=be2.partition_broadcast(P))
-        sq = keep.tile([P, HALVES, GRAPHS], F32)
-        nc.vector.tensor_reduce(
-            out=sq[:],
-            in_=rel_sq[:, :, 0 : GRAPHS * COORDS].rearrange("p h (b c) -> p h b c", c=COORDS),
-            axis=mybir.AxisListType.X,
-            op=ALU.add,
-        )
-        dist = keep.tile([P, HALVES, GRAPHS], F32)
-        nc.gpsimd.tensor_tensor(out=dist[:], in0=sq[:], in1=halves[:], op=ALU.pow)
-        quantise_weight(0)
-
-        regroup_weight(2)
-        quantise_weight(1)
-        node_products(0)
-        regroup_weight(3)
-        quantise_weight(2)
-        quantise_weight(3)
-        rest = keep.tile([P, HALVES, GRAPHS], F32)
-        nc.vector.tensor_copy(out=dist_cols[:, :, :, DIST], in_=dist[:])
-        nc.vector.tensor_tensor(out=rest[:], in0=dist[:], in1=dist_cols[:, :, :, DIST], op=ALU.subtract)
-        nc.vector.tensor_copy(out=dist_cols[:, :, :, DIST + 1], in_=rest[:])
-        nc.vector.tensor_tensor(
-            out=dist_cols[:, :, :, DIST + 2], in0=rest[:], in1=dist_cols[:, :, :, DIST + 1], op=ALU.subtract
-        )
-        dist_rep = keep.tile([P, VECTOR_GRAPHS, HALVES, P], F32)
-        nc.gpsimd.tensor_copy(
-            out=dist_rep[:],
-            in_=dist[:, :, TENSOR_GRAPHS:GRAPHS].rearrange("p h b -> p b h").unsqueeze(3).to_broadcast(
-                [P, VECTOR_GRAPHS, HALVES, P]
-            ),
-        )
-        for q in range(3):
-            flip_spread(q)
-        split_products(0)
-        node_products(1)
-        regroup_weight(4)
-        for q in range(3):
-            copy_spread(q)
-        flip_spread(3)
-        dist_flip = psum_acc.tile([P, VECTOR_GRAPHS, HALVES, P], F32, tag="acc")
-        for v in range(VECTOR_GRAPHS):
-            for h in range(HALVES):
-                nc.tensor.transpose(dist_flip[:, v, h, :], dist_rep[:, v, h, :], ident_f[:])
-        split_products(1)
-        regroup_weight(5)
-        quantise_weight(4)
-
-        sums = keep.tile([P, VECTOR_GRAPHS, F_TILES, PAIRS], F32)
-        flipped = {}
-        terms = {}
-        pre = {}
-        h_grouped = {}
-        h_words = {}
 
         def flip_terms(b):
             flipped[b] = psum_flip.tile([P, F_TILES, P], BF16, tag="flip", name="flipped")
@@ -339,13 +204,13 @@ def tile_graphmessagelayer_pa_kernel(tc, node_state, positions, We1, be1, We2, b
             nc.gpsimd.tensor_tensor(
                 out=by_pair,
                 in0=by_pair,
-                in1=a_last[:, 0, f, nodes].unsqueeze(2).to_broadcast([P, NODES, NODES]),
+                in1=a_side[:, 0, f, nodes].unsqueeze(2).to_broadcast([P, NODES, NODES]),
                 op=ALU.add,
             )
             nc.gpsimd.tensor_tensor(
                 out=by_pair,
                 in0=by_pair,
-                in1=a_last[:, 1, f, nodes].unsqueeze(1).to_broadcast([P, NODES, NODES]),
+                in1=a_side[:, 1, f, nodes].unsqueeze(1).to_broadcast([P, NODES, NODES]),
                 op=ALU.add,
             )
 
@@ -353,25 +218,24 @@ def tile_graphmessagelayer_pa_kernel(tc, node_state, positions, We1, be1, We2, b
             if u >= TENSOR_UNITS:
                 v, h = divmod(u - TENSOR_UNITS, HALVES)
                 pre[u] = [sums[:, v, g * PACK : (g + 1) * PACK, h * P : (h + 1) * P] for g in range(PASSES)]
-            grouped = work.tile([P, PASSES, P, PACK], BF16, align_bytes=64, tag="h_grouped")
+            h_grouped[u] = work.tile([P, PASSES, P, PACK], BF16, align_bytes=64, tag="h_grouped", name="h_grouped")
             for g in range(PASSES):
                 nc.scalar.activation(
-                    out=grouped[:, g, :, :], in_=pre[u][g].rearrange("p t r -> p r t"), func=ACT.Silu
+                    out=h_grouped[u][:, g, :, :], in_=pre[u][g].rearrange("p t r -> p r t"), func=ACT.Silu
                 )
-            return grouped
 
-        def quantise(grouped):
+        def quantise(u):
             h_codes = work.tile([P, PASSES, P], U32, align_bytes=64)
             h_scales = work.tile([P, PASSES, P], U8, align_bytes=64)
             nc.vector.quantize_mx(
                 out=h_codes[:].rearrange("p g r -> p (g r)").bitcast(FP8X4),
                 scales=h_scales[:].rearrange("p g r -> p (g r)"),
-                in_=grouped[:].rearrange("p g r t -> p (g r t)"),
+                in_=h_grouped[u][:].rearrange("p g r t -> p (g r t)"),
             )
-            return h_codes, h_scales
+            h_words[u] = (h_codes, h_scales)
 
-        def multiply(u, words):
-            h_codes, h_scales = words
+        def multiply(u):
+            h_codes, h_scales = h_words[u]
             msg = store_pool.tile([P, WIDTH], F32)
             for m in range(WIDTH // BANK):
                 acc = psum_acc.tile([P, BANK], F32, tag="acc")
@@ -393,28 +257,180 @@ def tile_graphmessagelayer_pa_kernel(tc, node_state, positions, We1, be1, We2, b
                 )
             nc.sync.dma_start(out=out_rows[u * P : (u + 1) * P, :], in_=msg[:])
 
+        warm = keep.tile([P, 2], F32)
+        nc.vector.memset(warm[:], 1.0)
+        nc.vector.memset(vec_rows[:], 0.0)
+        nc.vector.memset(pos_nodes[:], 0.0)
+        nc.scalar.dma_start(out=vec_rows[0:F_TILES, :], in_=be1.rearrange("(r c) -> r c", c=P))
+        nc.scalar.dma_start(
+            out=vec_rows[F_TILES : 2 * F_TILES, :],
+            in_=We1[2 * WIDTH : 2 * WIDTH + 1, :].rearrange("o (r c) -> (o r) c", c=P),
+        )
+        with nc.allow_non_contiguous_dma(reason="768 values in runs of 3, once"):
+            nc.scalar.dma_start(
+                out=pos_nodes[0:NODES, 0 : GRAPHS * COORDS].rearrange("n (b c) -> n b c", c=COORDS),
+                in_=positions.rearrange("b n c -> n b c"),
+            )
+        nc.scalar.activation(out=warm[:, 1:2], in_=warm[:, 0:1], func=ACT.Sqrt)
+        load_weight(0)
+        nc.sync.dma_start(
+            out=x_rows[:], in_=node_state.rearrange("b n h -> (b n) h").rearrange("(a p) h -> p a h", p=P)
+        )
+        for k in range(1, RAW_BUFS):
+            load_weight(k)
+        make_identity(nc, ident_bf[:])
+        make_identity(nc, ident_f[:])
+
+        stacked_words = stacked[:].rearrange("p f b c -> p (f b c)").bitcast(I32).rearrange("p (r c) -> p r c", c=P // 2)
+        nc.vector.memset(stacked_words[:, :, DIST // 2 : P // 2], 0)
+        spread_words = spread_t[:].rearrange("p h b c -> p (h b c)").bitcast(I32).rearrange("p (r c) -> p r c", c=P // 2)
+        nc.vector.memset(spread_words[:, :, DIST // 2 : P // 2], 0)
+        nc.vector.memset(spread_t[:, :, :, ONE : ONE + 1], 1.0)
+
+        sel = keep.tile([P, HALVES, P], BF16)
+        for h in range(HALVES):
+            nc.gpsimd.tensor_tensor(
+                out=sel[:, h, :].rearrange("p (i j) -> p i j", j=NODES),
+                in0=ident_bf[:, h * HALF : (h + 1) * HALF].unsqueeze(2).to_broadcast([P, HALF, NODES]),
+                in1=ident_bf[:, 0:NODES].unsqueeze(1).to_broadcast([P, HALF, NODES]),
+                op=ALU.subtract,
+            )
+        pick = keep.tile([P, 2 * NODES], BF16)
+        nc.gpsimd.tensor_tensor(
+            out=pick[:], in0=ident_bf[:, HI : HI + 2 * NODES], in1=ident_bf[:, LO : LO + 2 * NODES], op=ALU.add
+        )
+        pick_pairs = keep.tile([P, NODES, NODES], BF16)
+        nc.gpsimd.tensor_tensor(
+            out=pick_pairs[:],
+            in0=pick[:, 0:NODES].unsqueeze(2).to_broadcast([P, NODES, NODES]),
+            in1=pick[:, NODES : 2 * NODES].unsqueeze(1).to_broadcast([P, NODES, NODES]),
+            op=ALU.add,
+        )
+        pick_t = psum_acc.tile([P, HALVES, P], BF16, tag="acc")
+        for h in range(HALVES):
+            nc.tensor.transpose(
+                pick_t[:, h, :], pick_pairs[:, h * HALF : (h + 1) * HALF, :].rearrange("p i j -> p (i j)"), ident_bf[:]
+            )
+        nc.scalar.copy(
+            out=spread_t[:, :, :, 0:DIST],
+            in_=pick_t[:, :, 0:DIST].unsqueeze(2).to_broadcast([P, HALVES, GRAPHS, DIST]),
+        )
+
+        for a in range(NODE_TILES):
+            for g in range(PASSES):
+                x_t = psum_pre.tile([P, PACK, P], BF16, tag="pre")
+                for t in range(PACK):
+                    k0 = g * K_PASS + t * P
+                    nc.tensor.transpose(x_t[:, t, :], x_rows[:, a, k0 : k0 + P], ident_bf[:])
+                nc.scalar.copy(out=x_grouped[:, g, a * P : (a + 1) * P, :], in_=x_t[:].rearrange("p t r -> p r t"))
+        vec_t = psum_acc.tile([P, P], BF16, tag="acc")
+        nc.tensor.transpose(vec_t[:], vec_rows[:], ident_bf[:])
+        rel = psum_acc.tile([P, HALVES, POS_COLUMNS], F32, tag="acc")
+        for h in range(HALVES):
+            nc.tensor.matmul(out=rel[:, h, :], lhsT=sel[:, h, :], rhs=pos_nodes[:], start=True, stop=True)
+
+        regroup_weight(0)
+        load_weight(RAW_BUFS)
+        nc.vector.quantize_mx(
+            out=x_codes[:].rearrange("p g r -> p (g r)").bitcast(FP8X4),
+            scales=x_scales[:].rearrange("p g r -> p (g r)"),
+            in_=x_grouped[:].rearrange("p g r t -> p (g r t)"),
+        )
+        nc.vector.tensor_copy(out=vecs[:].rearrange("p v f -> p (v f)"), in_=vec_t[:, 0 : 2 * F_TILES])
+        nc.gpsimd.tensor_copy(
+            out=stacked[:, :, :, DIST:ONE],
+            in_=vecs[:, 1, :].unsqueeze(2).unsqueeze(3).to_broadcast([P, F_TILES, GRAPHS, ONE - DIST]),
+        )
+        nc.gpsimd.tensor_copy(
+            out=stacked[:, :, :, ONE : ONE + 1],
+            in_=vecs[:, 0, :].unsqueeze(2).unsqueeze(3).to_broadcast([P, F_TILES, GRAPHS, 1]),
+        )
+        rel_sq = keep.tile([P, HALVES, POS_COLUMNS], F32)
+        nc.scalar.activation(out=rel_sq[:], in_=rel[:], func=ACT.Square)
+
+        regroup_weight(1)
+        load_weight(RAW_BUFS + 1)
+        nc.sync.dma_start(out=be2_all[:], in_=be2.partition_broadcast(P))
+        sq = keep.tile([P, HALVES, GRAPHS], F32)
+        nc.vector.tensor_reduce(
+            out=sq[:],
+            in_=rel_sq[:, :, 0 : GRAPHS * COORDS].rearrange("p h (b c) -> p h b c", c=COORDS),
+            axis=mybir.AxisListType.X,
+            op=ALU.add,
+        )
+        sq_floor = keep.tile([P, HALVES, GRAPHS], F32)
+        nc.vector.tensor_scalar_max(out=sq_floor[:], in0=sq[:], scalar1=TINY)
+        root = keep.tile([P, HALVES, GRAPHS], F32)
+        nc.scalar.activation(out=root[:], in_=sq_floor[:], func=ACT.Sqrt)
+        quantise_weight(0)
+
+        regroup_weight(2)
+        quantise_weight(1)
+        node_products(0)
+        dist = keep.tile([P, HALVES, GRAPHS], F32)
+        nc.vector.scalar_tensor_tensor(
+            out=dist[:].rearrange("p h b -> p (h b)"),
+            in0=sq[:].rearrange("p h b -> p (h b)"),
+            scalar=0.0,
+            in1=root[:].rearrange("p h b -> p (h b)"),
+            op0=ALU.is_gt,
+            op1=ALU.mult,
+        )
+        rest = keep.tile([P, HALVES, GRAPHS], F32)
+        nc.vector.tensor_copy(out=spread_t[:, :, :, DIST], in_=dist[:])
+        nc.vector.tensor_tensor(out=rest[:], in0=dist[:], in1=spread_t[:, :, :, DIST], op=ALU.subtract)
+        nc.vector.tensor_copy(out=spread_t[:, :, :, DIST + 1], in_=rest[:])
+        nc.vector.tensor_tensor(
+            out=spread_t[:, :, :, DIST + 2], in0=rest[:], in1=spread_t[:, :, :, DIST + 1], op=ALU.subtract
+        )
+        dist_rep = keep.tile([P, SIDE_GRAPHS, HALVES, P], F32)
+        nc.gpsimd.tensor_copy(
+            out=dist_rep[:],
+            in_=dist[:, :, TENSOR_GRAPHS:GRAPHS].rearrange("p h b -> p b h").unsqueeze(3).to_broadcast(
+                [P, SIDE_GRAPHS, HALVES, P]
+            ),
+        )
+        for q in range(ACC_BANKS):
+            flip_spread(q)
+
+        regroup_weight(3)
+        quantise_weight(2)
+        quantise_weight(3)
+        split_products(0)
+        node_products(1)
+        regroup_weight(4)
+        for q in range(ACC_BANKS):
+            copy_spread(q)
+        flip_spread(ACC_BANKS)
+        dist_ps = psum_acc.tile([P, SIDE_GRAPHS, HALVES, P], F32, tag="acc")
+        for v in range(SIDE_GRAPHS):
+            for h in range(HALVES):
+                nc.tensor.transpose(dist_ps[:, v, h, :], dist_rep[:, v, h, :], ident_f[:])
+        split_products(1)
+        regroup_weight(5)
+        quantise_weight(4)
+
         flip_terms(0)
         copy_terms(0)
         form_pre(0)
         flip_terms(1)
-        copy_spread(3)
-        dist_all = keep.tile([P, VECTOR_GRAPHS, PAIRS], F32)
-        nc.scalar.copy(out=dist_all[:].rearrange("p v q -> p (v q)"), in_=dist_flip[:].rearrange("p v h n -> p (v h n)"))
+        copy_spread(ACC_BANKS)
+        nc.scalar.copy(out=dist_all[:].rearrange("p v q -> p (v q)"), in_=dist_ps[:].rearrange("p v h n -> p (v h n)"))
         copy_terms(1)
         quantise_weight(5)
-        for v in range(VECTOR_GRAPHS):
+        for v in range(SIDE_GRAPHS):
             for f in range(F_TILES):
                 side_sums(v, f)
 
         for u in range(UNITS + 2):
             if u < UNITS:
-                h_grouped[u] = activate(u)
+                activate(u)
             if u % HALVES == 1 and (u + 3) // HALVES < TENSOR_GRAPHS:
                 copy_terms((u + 3) // HALVES)
             if 1 <= u <= UNITS:
-                h_words[u - 1] = quantise(h_grouped[u - 1])
+                quantise(u - 1)
             if u >= 2:
-                multiply(u - 2, h_words[u - 2])
+                multiply(u - 2)
             if u + 1 < TENSOR_UNITS:
                 form_pre(u + 1)
             if u % HALVES == 0 and u // HALVES + 2 < TENSOR_GRAPHS:

@@ -24,7 +24,7 @@ PASSES = WIDTH // K_PASS
 F_TILES = WIDTH // P
 ALL_NODES = GRAPHS * NODES
 NODE_TILES = ALL_NODES // P
-F_PER_BANK = BANK // ALL_NODES
+TILE_GRAPHS = P // NODES
 PAIRS = NODES * NODES
 HALVES = PAIRS // P
 HALF = NODES // HALVES
@@ -41,14 +41,14 @@ TENSOR_GRAPHS = GRAPHS - SIDE_GRAPHS
 UNITS = GRAPHS * HALVES
 TENSOR_UNITS = TENSOR_GRAPHS * HALVES
 
+SIDES = WIDTH // BANK
+PIECE_F = BANK // P
 RUN = 4
-VECTOR_COLUMNS = 640
-RAW_BUFS = 4
-PRE_BANKS = 4
-ACC_BANKS = 3
+VECTOR_COLUMNS = 256
+LEAD = 6
 SPREAD_GRAPHS = 2 * BANK // PAIRS
-
-assert GRAPHS // SPREAD_GRAPHS == ACC_BANKS + 1
+EARLY_GRAPHS = (LEAD + HALVES) // HALVES
+MEMSET_GRAPHS = 6
 
 FLOPS = 2 * ALL_NODES * WIDTH * 2 * WIDTH + 2 * GRAPHS * PAIRS * WIDTH * WIDTH
 
@@ -57,21 +57,24 @@ def tile_graphmessagelayer_pa_kernel(tc, node_state, positions, We1, be1, We2, b
     nc = tc.nc
     out_rows = out.rearrange("b i j m -> (b i j) m")
     weight_rows = [We1[0:WIDTH, :], We1[WIDTH : 2 * WIDTH, :], We2]
+    pieces = [(w, g, c) for c in range(SIDES) for w in range(2) for g in range(PASSES)]
+    pieces += [(2, g, c) for c in range(SIDES) for g in range(PASSES)]
 
     with ExitStack() as ctx:
         keep = ctx.enter_context(tc.tile_pool(name="keep", bufs=1))
-        raw_pool = ctx.enter_context(tc.tile_pool(name="raw", bufs=RAW_BUFS))
-        grouped_pool = ctx.enter_context(tc.tile_pool(name="grouped", bufs=2))
+        raw_pool = ctx.enter_context(tc.tile_pool(name="raw", bufs=8))
+        grouped_pool = ctx.enter_context(tc.tile_pool(name="grouped", bufs=3))
+        unit_pool = ctx.enter_context(tc.tile_pool(name="unit", bufs=LEAD + 4))
         work = ctx.enter_context(tc.tile_pool(name="work", bufs=4))
         store_pool = ctx.enter_context(tc.tile_pool(name="store", bufs=6))
-        psum_flip = ctx.enter_context(tc.psum_pool(name="psum_flip", bufs=1))
-        psum_pre = ctx.enter_context(tc.psum_pool(name="psum_pre", bufs=PRE_BANKS))
-        psum_acc = ctx.enter_context(tc.psum_pool(name="psum_acc", bufs=ACC_BANKS))
+        psum_pre = ctx.enter_context(tc.psum_pool(name="psum_pre", bufs=4))
+        psum_acc = ctx.enter_context(tc.psum_pool(name="psum_acc", bufs=4))
         ctx.enter_context(tc.manual_schedule())
 
         vec_rows = keep.tile([P, P], BF16)
         pos_nodes = keep.tile([P, POS_COLUMNS], BF16)
-        stacked = keep.tile([P, F_TILES, GRAPHS, P], BF16)
+        parts = keep.tile([P, NODE_TILES, 2, 2, WIDTH], BF16)
+        terms = keep.tile([P, TENSOR_GRAPHS, WIDTH], BF16)
         spread_t = keep.tile([P, HALVES, GRAPHS, P], BF16)
         spread = keep.tile([P, GRAPHS, PAIRS], BF16)
         x_rows = keep.tile([P, NODE_TILES, WIDTH], BF16)
@@ -81,78 +84,99 @@ def tile_graphmessagelayer_pa_kernel(tc, node_state, positions, We1, be1, We2, b
         x_codes = keep.tile([P, PASSES, ALL_NODES], U32, align_bytes=64)
         x_scales = keep.tile([P, PASSES, ALL_NODES], U8, align_bytes=64)
         vecs = keep.tile([P, 2, F_TILES], F32)
-        w_codes = keep.tile([P, 3 * PASSES, WIDTH], U32, align_bytes=64)
-        w_scales = keep.tile([P, 3 * PASSES, WIDTH], U8, align_bytes=64)
+        w_codes = keep.tile([P, 3, PASSES, WIDTH], U32, align_bytes=64)
+        w_scales = keep.tile([P, 3, PASSES, WIDTH], U8, align_bytes=64)
         a_side = keep.tile([P, 2, F_TILES, SIDE_GRAPHS * NODES], F32)
         dist_all = keep.tile([P, SIDE_GRAPHS, PAIRS], F32)
         sums = keep.tile([P, SIDE_GRAPHS, F_TILES, PAIRS], F32)
         be2_all = keep.tile([P, WIDTH], BF16)
         raw = {}
-        w_grouped = {}
+        grouped = {}
         a_ps = {}
+        side_ps = {}
         spread_ps = {}
-        flipped = {}
-        terms = {}
         pre = {}
         h_grouped = {}
         h_words = {}
 
-        def load_weight(k):
-            w, g = divmod(k, PASSES)
-            raw[k] = raw_pool.tile([P, PACK, WIDTH], BF16, tag="raw", name="raw")
+        def load_piece(k):
+            w, g, c = pieces[k]
+            raw[k] = raw_pool.tile([P, PACK, BANK], BF16, tag="raw", name="raw")
             nc.sync.dma_start(
                 out=raw[k][:],
-                in_=weight_rows[w][g * K_PASS : (g + 1) * K_PASS, :].rearrange("(t p) n -> p t n", p=P),
+                in_=weight_rows[w][g * K_PASS : (g + 1) * K_PASS, c * BANK : (c + 1) * BANK].rearrange(
+                    "(t p) n -> p t n", p=P
+                ),
             )
 
-        def regroup_weight(k):
-            w_grouped[k] = grouped_pool.tile([P, WIDTH, PACK], BF16, align_bytes=64, tag="grouped", name="grouped")
+        def regroup(k):
+            grouped[k] = grouped_pool.tile([P, BANK, PACK], BF16, align_bytes=64, tag="grouped", name="grouped")
             cut = VECTOR_COLUMNS
             nc.vector.tensor_copy(
-                out=w_grouped[k][:, 0:cut, :].rearrange("p (c i) t -> p c t i", i=RUN),
+                out=grouped[k][:, 0:cut, :].rearrange("p (c i) t -> p c t i", i=RUN),
                 in_=raw[k][:, :, 0:cut].rearrange("p t (c i) -> p c t i", i=RUN),
             )
             nc.scalar.copy(
-                out=w_grouped[k][:, cut:WIDTH, :].rearrange("p (c i) t -> p c t i", i=RUN),
-                in_=raw[k][:, :, cut:WIDTH].rearrange("p t (c i) -> p c t i", i=RUN),
+                out=grouped[k][:, cut:BANK, :].rearrange("p (c i) t -> p c t i", i=RUN),
+                in_=raw[k][:, :, cut:BANK].rearrange("p t (c i) -> p c t i", i=RUN),
             )
 
-        def quantise_weight(k):
+        def quantise_piece(k):
+            w, g, c = pieces[k]
             nc.vector.quantize_mx(
-                out=w_codes[:, k, :].bitcast(FP8X4),
-                scales=w_scales[:, k, :],
-                in_=w_grouped[k][:].rearrange("p n t -> p (n t)"),
+                out=w_codes[:, w, g, c * BANK : (c + 1) * BANK].bitcast(FP8X4),
+                scales=w_scales[:, w, g, c * BANK : (c + 1) * BANK],
+                in_=grouped[k][:].rearrange("p n t -> p (n t)"),
             )
 
-        def node_products(w):
-            for bank in range(F_TILES // F_PER_BANK):
-                a_ps[w, bank] = psum_pre.tile([P, F_PER_BANK, ALL_NODES], F32, tag="pre", name="a_ps")
-                for e in range(F_PER_BANK):
-                    f = bank * F_PER_BANK + e
-                    for g in range(PASSES):
-                        nc.tensor.matmul_mx(
-                            out=a_ps[w, bank][:, e, :],
-                            lhsT=w_codes[:, w * PASSES + g, f * P : (f + 1) * P].bitcast(FP8X4),
-                            lhsT_scale=w_scales[:, w * PASSES + g, f * P : (f + 1) * P],
-                            rhs=x_codes[:, g, :].bitcast(FP8X4),
-                            rhs_scale=x_scales[:, g, :],
-                            start=(g == 0),
-                            stop=(g == PASSES - 1),
-                        )
-
-        def split_products(w):
-            for bank in range(F_TILES // F_PER_BANK):
-                f_range = slice(bank * F_PER_BANK, (bank + 1) * F_PER_BANK)
-                by_graph = a_ps[w, bank][:, :, 0 : TENSOR_GRAPHS * NODES].rearrange("p e (b n) -> p e b n", n=NODES)
-                high = stacked[:, f_range, 0:TENSOR_GRAPHS, HI + w * NODES : HI + (w + 1) * NODES]
-                nc.scalar.copy(out=high, in_=by_graph)
-                nc.scalar.copy(out=a_side[:, w, f_range, :], in_=a_ps[w, bank][:, :, TENSOR_GRAPHS * NODES : ALL_NODES])
-                nc.vector.tensor_tensor(
-                    out=stacked[:, f_range, 0:TENSOR_GRAPHS, LO + w * NODES : LO + (w + 1) * NODES],
-                    in0=by_graph,
-                    in1=high,
-                    op=ALU.subtract,
+        def product(c, w, a):
+            a_ps[w, a] = psum_pre.tile([P, BANK], F32, tag="pre", name="a_ps")
+            for g in range(PASSES):
+                nc.tensor.matmul_mx(
+                    out=a_ps[w, a][:],
+                    lhsT=x_codes[:, g, a * P : (a + 1) * P].bitcast(FP8X4),
+                    lhsT_scale=x_scales[:, g, a * P : (a + 1) * P],
+                    rhs=w_codes[:, w, g, c * BANK : (c + 1) * BANK].bitcast(FP8X4),
+                    rhs_scale=w_scales[:, w, g, c * BANK : (c + 1) * BANK],
+                    start=(g == 0),
+                    stop=(g == PASSES - 1),
                 )
+
+        def split_product(c, w, a):
+            columns = slice(c * BANK, (c + 1) * BANK)
+            nc.scalar.copy(out=parts[:, a, w, 0, columns], in_=a_ps[w, a][:])
+            nc.vector.tensor_tensor(
+                out=parts[:, a, w, 1, columns], in0=a_ps[w, a][:], in1=parts[:, a, w, 0, columns], op=ALU.subtract
+            )
+
+        def place_terms(b, columns):
+            a, n0 = divmod(b * NODES, P)
+            for s in range(2):
+                for w in range(2):
+                    row = (2 * s + w) * NODES
+                    nc.sync.dma_start(
+                        out=terms[row : row + NODES, b, columns], in_=parts[n0 : n0 + NODES, a, w, s, columns]
+                    )
+
+        def side_product(c, w):
+            side_ps[w] = psum_acc.tile([P, PIECE_F, P], F32, tag="acc", name="side_ps")
+            for e in range(PIECE_F):
+                f0 = c * BANK + e * P
+                for g in range(PASSES):
+                    nc.tensor.matmul_mx(
+                        out=side_ps[w][:, e, :],
+                        lhsT=w_codes[:, w, g, f0 : f0 + P].bitcast(FP8X4),
+                        lhsT_scale=w_scales[:, w, g, f0 : f0 + P],
+                        rhs=x_codes[:, g, ALL_NODES - P : ALL_NODES].bitcast(FP8X4),
+                        rhs_scale=x_scales[:, g, ALL_NODES - P : ALL_NODES],
+                        start=(g == 0),
+                        stop=(g == PASSES - 1),
+                    )
+
+        def copy_side(c, w):
+            nc.scalar.copy(
+                out=a_side[:, w, c * PIECE_F : (c + 1) * PIECE_F, :], in_=side_ps[w][:, :, P - SIDE_GRAPHS * NODES : P]
+            )
 
         def flip_spread(q):
             spread_ps[q] = psum_acc.tile([P, SPREAD_GRAPHS, HALVES, P], BF16, tag="acc", name="spread_ps")
@@ -166,29 +190,18 @@ def tile_graphmessagelayer_pa_kernel(tc, node_state, positions, We1, be1, We2, b
                 in_=spread_ps[q][:].rearrange("p k h n -> p (k h n)"),
             )
 
-        def flip_terms(b):
-            flipped[b] = psum_flip.tile([P, F_TILES, P], BF16, tag="flip", name="flipped")
-            for f in range(F_TILES):
-                nc.tensor.transpose(flipped[b][:, f, :], stacked[:, f, b, :], ident_bf[:])
-
-        def copy_terms(b):
-            terms[b] = work.tile([P, F_TILES, P], BF16, tag="terms", name="terms")
-            nc.scalar.copy(out=terms[b][:], in_=flipped[b][:])
-
-        def form_pre(u):
+        def form_pre(u, c):
             b, h = divmod(u, HALVES)
-            pre[u] = []
-            for g in range(PASSES):
-                pre_ps = psum_pre.tile([P, PACK, P], F32, tag="pre")
-                for t in range(PACK):
-                    nc.tensor.matmul(
-                        out=pre_ps[:, t, :],
-                        lhsT=terms[b][:, g * PACK + t, :],
-                        rhs=spread[:, b, h * P : (h + 1) * P],
-                        start=True,
-                        stop=True,
-                    )
-                pre[u].append(pre_ps[:])
+            pre[u, c] = psum_pre.tile([P, PACK, P], F32, tag="pre", name="pre_ps")
+            for t in range(PACK):
+                f = c * PIECE_F + t
+                nc.tensor.matmul(
+                    out=pre[u, c][:, t, :],
+                    lhsT=terms[:, b, f * P : (f + 1) * P],
+                    rhs=spread[:, b, h * P : (h + 1) * P],
+                    start=True,
+                    stop=True,
+                )
 
         def side_sums(v, f):
             nodes = slice(v * NODES, (v + 1) * NODES)
@@ -214,15 +227,15 @@ def tile_graphmessagelayer_pa_kernel(tc, node_state, positions, We1, be1, We2, b
                 op=ALU.add,
             )
 
-        def activate(u):
-            if u >= TENSOR_UNITS:
+        def activate(u, c):
+            if c == 0:
+                h_grouped[u] = unit_pool.tile([P, PASSES, P, PACK], BF16, align_bytes=64, tag="h", name="h_grouped")
+            if u < TENSOR_UNITS:
+                source = pre[u, c][:]
+            else:
                 v, h = divmod(u - TENSOR_UNITS, HALVES)
-                pre[u] = [sums[:, v, g * PACK : (g + 1) * PACK, h * P : (h + 1) * P] for g in range(PASSES)]
-            h_grouped[u] = work.tile([P, PASSES, P, PACK], BF16, align_bytes=64, tag="h_grouped", name="h_grouped")
-            for g in range(PASSES):
-                nc.scalar.activation(
-                    out=h_grouped[u][:, g, :, :], in_=pre[u][g].rearrange("p t r -> p r t"), func=ACT.Silu
-                )
+                source = sums[:, v, c * PACK : (c + 1) * PACK, h * P : (h + 1) * P]
+            nc.scalar.activation(out=h_grouped[u][:, c, :, :], in_=source.rearrange("p t r -> p r t"), func=ACT.Silu)
 
         def quantise(u):
             h_codes = work.tile([P, PASSES, P], U32, align_bytes=64)
@@ -237,15 +250,15 @@ def tile_graphmessagelayer_pa_kernel(tc, node_state, positions, We1, be1, We2, b
         def multiply(u):
             h_codes, h_scales = h_words[u]
             msg = store_pool.tile([P, WIDTH], F32)
-            for m in range(WIDTH // BANK):
+            for m in range(SIDES):
                 acc = psum_acc.tile([P, BANK], F32, tag="acc")
                 for g in range(PASSES):
                     nc.tensor.matmul_mx(
                         out=acc[:],
                         lhsT=h_codes[:, g, :].bitcast(FP8X4),
                         lhsT_scale=h_scales[:, g, :],
-                        rhs=w_codes[:, 2 * PASSES + g, m * BANK : (m + 1) * BANK].bitcast(FP8X4),
-                        rhs_scale=w_scales[:, 2 * PASSES + g, m * BANK : (m + 1) * BANK],
+                        rhs=w_codes[:, 2, g, m * BANK : (m + 1) * BANK].bitcast(FP8X4),
+                        rhs_scale=w_scales[:, 2, g, m * BANK : (m + 1) * BANK],
                         start=(g == 0),
                         stop=(g == PASSES - 1),
                     )
@@ -272,20 +285,20 @@ def tile_graphmessagelayer_pa_kernel(tc, node_state, positions, We1, be1, We2, b
                 in_=positions.rearrange("b n c -> n b c"),
             )
         nc.scalar.activation(out=warm[:, 1:2], in_=warm[:, 0:1], func=ACT.Sqrt)
-        load_weight(0)
+        load_piece(0)
         nc.sync.dma_start(
             out=x_rows[:], in_=node_state.rearrange("b n h -> (b n) h").rearrange("(a p) h -> p a h", p=P)
         )
-        for k in range(1, RAW_BUFS):
-            load_weight(k)
+        for k in range(1, 8):
+            load_piece(k)
         make_identity(nc, ident_bf[:])
-        make_identity(nc, ident_f[:])
 
-        stacked_words = stacked[:].rearrange("p f b c -> p (f b c)").bitcast(I32).rearrange("p (r c) -> p r c", c=P // 2)
-        nc.vector.memset(stacked_words[:, :, DIST // 2 : P // 2], 0)
         spread_words = spread_t[:].rearrange("p h b c -> p (h b c)").bitcast(I32).rearrange("p (r c) -> p r c", c=P // 2)
         nc.vector.memset(spread_words[:, :, DIST // 2 : P // 2], 0)
         nc.vector.memset(spread_t[:, :, :, ONE : ONE + 1], 1.0)
+        term_words = terms[:].rearrange("p b f -> p (b f)").bitcast(I32)
+        cut = MEMSET_GRAPHS * WIDTH // 2
+        nc.vector.memset(term_words[DIST:P, 0:cut], 0)
 
         sel = keep.tile([P, HALVES, P], BF16)
         for h in range(HALVES):
@@ -306,6 +319,8 @@ def tile_graphmessagelayer_pa_kernel(tc, node_state, positions, We1, be1, We2, b
             in1=pick[:, NODES : 2 * NODES].unsqueeze(1).to_broadcast([P, NODES, NODES]),
             op=ALU.add,
         )
+        nc.gpsimd.memset(term_words[DIST:P, cut:], 0)
+        make_identity(nc, ident_f[:])
         pick_t = psum_acc.tile([P, HALVES, P], BF16, tag="acc")
         for h in range(HALVES):
             nc.tensor.transpose(
@@ -315,42 +330,15 @@ def tile_graphmessagelayer_pa_kernel(tc, node_state, positions, We1, be1, We2, b
             out=spread_t[:, :, :, 0:DIST],
             in_=pick_t[:, :, 0:DIST].unsqueeze(2).to_broadcast([P, HALVES, GRAPHS, DIST]),
         )
-
-        for a in range(NODE_TILES):
-            for g in range(PASSES):
-                x_t = psum_pre.tile([P, PACK, P], BF16, tag="pre")
-                for t in range(PACK):
-                    k0 = g * K_PASS + t * P
-                    nc.tensor.transpose(x_t[:, t, :], x_rows[:, a, k0 : k0 + P], ident_bf[:])
-                nc.scalar.copy(out=x_grouped[:, g, a * P : (a + 1) * P, :], in_=x_t[:].rearrange("p t r -> p r t"))
-        vec_t = psum_acc.tile([P, P], BF16, tag="acc")
-        nc.tensor.transpose(vec_t[:], vec_rows[:], ident_bf[:])
         rel = psum_acc.tile([P, HALVES, POS_COLUMNS], F32, tag="acc")
         for h in range(HALVES):
             nc.tensor.matmul(out=rel[:, h, :], lhsT=sel[:, h, :], rhs=pos_nodes[:], start=True, stop=True)
-
-        regroup_weight(0)
-        load_weight(RAW_BUFS)
-        nc.vector.quantize_mx(
-            out=x_codes[:].rearrange("p g r -> p (g r)").bitcast(FP8X4),
-            scales=x_scales[:].rearrange("p g r -> p (g r)"),
-            in_=x_grouped[:].rearrange("p g r t -> p (g r t)"),
-        )
-        nc.vector.tensor_copy(out=vecs[:].rearrange("p v f -> p (v f)"), in_=vec_t[:, 0 : 2 * F_TILES])
-        nc.gpsimd.tensor_copy(
-            out=stacked[:, :, :, DIST:ONE],
-            in_=vecs[:, 1, :].unsqueeze(2).unsqueeze(3).to_broadcast([P, F_TILES, GRAPHS, ONE - DIST]),
-        )
-        nc.gpsimd.tensor_copy(
-            out=stacked[:, :, :, ONE : ONE + 1],
-            in_=vecs[:, 0, :].unsqueeze(2).unsqueeze(3).to_broadcast([P, F_TILES, GRAPHS, 1]),
-        )
+        vec_t = psum_acc.tile([P, P], BF16, tag="acc")
+        nc.tensor.transpose(vec_t[:], vec_rows[:], ident_bf[:])
         rel_sq = keep.tile([P, HALVES, POS_COLUMNS], F32)
         nc.scalar.activation(out=rel_sq[:], in_=rel[:], func=ACT.Square)
 
-        regroup_weight(1)
-        load_weight(RAW_BUFS + 1)
-        nc.sync.dma_start(out=be2_all[:], in_=be2.partition_broadcast(P))
+        regroup(0)
         sq = keep.tile([P, HALVES, GRAPHS], F32)
         nc.vector.tensor_reduce(
             out=sq[:],
@@ -362,11 +350,18 @@ def tile_graphmessagelayer_pa_kernel(tc, node_state, positions, We1, be1, We2, b
         nc.vector.tensor_scalar_max(out=sq_floor[:], in0=sq[:], scalar1=TINY)
         root = keep.tile([P, HALVES, GRAPHS], F32)
         nc.scalar.activation(out=root[:], in_=sq_floor[:], func=ACT.Sqrt)
-        quantise_weight(0)
+        quantise_piece(0)
 
-        regroup_weight(2)
-        quantise_weight(1)
-        node_products(0)
+        for a in range(NODE_TILES):
+            for g in range(PASSES):
+                x_t = psum_pre.tile([P, PACK, P], BF16, tag="pre")
+                for t in range(PACK):
+                    k0 = g * K_PASS + t * P
+                    nc.tensor.transpose(x_t[:, t, :], x_rows[:, a, k0 : k0 + P], ident_bf[:])
+                nc.scalar.copy(out=x_grouped[:, g, a * P : (a + 1) * P, :], in_=x_t[:].rearrange("p t r -> p r t"))
+
+        regroup(1)
+        load_piece(8)
         dist = keep.tile([P, HALVES, GRAPHS], F32)
         nc.vector.scalar_tensor_tensor(
             out=dist[:].rearrange("p h b -> p (h b)"),
@@ -376,13 +371,43 @@ def tile_graphmessagelayer_pa_kernel(tc, node_state, positions, We1, be1, We2, b
             op0=ALU.is_gt,
             op1=ALU.mult,
         )
+        nc.vector.quantize_mx(
+            out=x_codes[:].rearrange("p g r -> p (g r)").bitcast(FP8X4),
+            scales=x_scales[:].rearrange("p g r -> p (g r)"),
+            in_=x_grouped[:].rearrange("p g r t -> p (g r t)"),
+        )
         rest = keep.tile([P, HALVES, GRAPHS], F32)
         nc.vector.tensor_copy(out=spread_t[:, :, :, DIST], in_=dist[:])
+        quantise_piece(1)
         nc.vector.tensor_tensor(out=rest[:], in0=dist[:], in1=spread_t[:, :, :, DIST], op=ALU.subtract)
+
+        regroup(2)
+        load_piece(9)
         nc.vector.tensor_copy(out=spread_t[:, :, :, DIST + 1], in_=rest[:])
+        product(0, 0, 0)
+        product(0, 0, 1)
+        regroup(3)
+        load_piece(10)
         nc.vector.tensor_tensor(
             out=spread_t[:, :, :, DIST + 2], in0=rest[:], in1=spread_t[:, :, :, DIST + 1], op=ALU.subtract
         )
+        quantise_piece(2)
+        load_piece(11)
+        nc.sync.dma_start(
+            out=terms[DIST:ONE, :, :],
+            in_=We1[2 * WIDTH : 2 * WIDTH + 1, :]
+            .rearrange("o f -> (o f)")
+            .partition_broadcast(ONE - DIST)
+            .unsqueeze(1)
+            .to_broadcast([ONE - DIST, TENSOR_GRAPHS, WIDTH]),
+        )
+        nc.sync.dma_start(
+            out=terms[ONE : ONE + 1, :, :],
+            in_=be1.partition_broadcast(1).unsqueeze(1).to_broadcast([1, TENSOR_GRAPHS, WIDTH]),
+        )
+        nc.sync.dma_start(out=be2_all[:], in_=be2.partition_broadcast(P))
+        nc.vector.tensor_copy(out=vecs[:].rearrange("p v f -> p (v f)"), in_=vec_t[:, 0 : 2 * F_TILES])
+        quantise_piece(3)
         dist_rep = keep.tile([P, SIDE_GRAPHS, HALVES, P], F32)
         nc.gpsimd.tensor_copy(
             out=dist_rep[:],
@@ -390,48 +415,90 @@ def tile_graphmessagelayer_pa_kernel(tc, node_state, positions, We1, be1, We2, b
                 [P, SIDE_GRAPHS, HALVES, P]
             ),
         )
-        for q in range(ACC_BANKS):
-            flip_spread(q)
+        flip_spread(0)
+        flip_spread(1)
+        product(0, 1, 0)
+        product(0, 1, 1)
+        for w in range(2):
+            for a in range(NODE_TILES):
+                split_product(0, w, a)
+        for b in range(EARLY_GRAPHS):
+            place_terms(b, slice(0, BANK))
+        side_product(0, 0)
+        side_product(0, 1)
+        copy_spread(0)
+        copy_side(0, 0)
+        copy_side(0, 1)
+        nc.scalar.activation(out=warm[:, 1:2], in_=warm[:, 0:1], func=ACT.Silu)
 
-        regroup_weight(3)
-        quantise_weight(2)
-        quantise_weight(3)
-        split_products(0)
-        node_products(1)
-        regroup_weight(4)
-        for q in range(ACC_BANKS):
-            copy_spread(q)
-        flip_spread(ACC_BANKS)
+        regroup(4)
+        regroup(5)
+        quantise_piece(4)
+        regroup(6)
+        quantise_piece(5)
+        copy_spread(1)
+        flip_spread(2)
+        flip_spread(3)
         dist_ps = psum_acc.tile([P, SIDE_GRAPHS, HALVES, P], F32, tag="acc")
         for v in range(SIDE_GRAPHS):
             for h in range(HALVES):
                 nc.tensor.transpose(dist_ps[:, v, h, :], dist_rep[:, v, h, :], ident_f[:])
-        split_products(1)
-        regroup_weight(5)
-        quantise_weight(4)
-
-        flip_terms(0)
-        copy_terms(0)
-        form_pre(0)
-        flip_terms(1)
-        copy_spread(ACC_BANKS)
         nc.scalar.copy(out=dist_all[:].rearrange("p v q -> p (v q)"), in_=dist_ps[:].rearrange("p v h n -> p (v h n)"))
-        copy_terms(1)
-        quantise_weight(5)
+        regroup(7)
+        quantise_piece(6)
+        product(1, 0, 0)
+        product(1, 0, 1)
+        copy_spread(2)
+        copy_spread(3)
+        quantise_piece(7)
+        product(1, 1, 0)
+        product(1, 1, 1)
+        regroup(8)
+        for w in range(2):
+            for a in range(NODE_TILES):
+                split_product(1, w, a)
+        for b in range(EARLY_GRAPHS):
+            place_terms(b, slice(BANK, WIDTH))
+        side_product(1, 0)
+        side_product(1, 1)
+        copy_side(1, 0)
+        copy_side(1, 1)
         for v in range(SIDE_GRAPHS):
             for f in range(F_TILES):
                 side_sums(v, f)
+        form_pre(0, 0)
+        regroup(9)
+        quantise_piece(8)
+        form_pre(1, 0)
+        activate(0, 0)
+        regroup(10)
+        quantise_piece(9)
+        form_pre(2, 0)
+        activate(1, 0)
+        regroup(11)
+        quantise_piece(10)
+        form_pre(3, 0)
+        activate(2, 0)
+        quantise_piece(11)
+        for u in range(4, LEAD):
+            form_pre(u, 0)
+            activate(u - 1, 0)
+        form_pre(LEAD, 0)
+        activate(LEAD - 1, 0)
+        form_pre(0, 1)
 
         for u in range(UNITS + 2):
             if u < UNITS:
-                activate(u)
-            if u % HALVES == 1 and (u + 3) // HALVES < TENSOR_GRAPHS:
-                copy_terms((u + 3) // HALVES)
+                activate(u, 1)
+            if u + LEAD < UNITS:
+                activate(u + LEAD, 0)
+            if EARLY_GRAPHS + u < TENSOR_GRAPHS:
+                place_terms(EARLY_GRAPHS + u, slice(0, WIDTH))
             if 1 <= u <= UNITS:
                 quantise(u - 1)
             if u >= 2:
                 multiply(u - 2)
             if u + 1 < TENSOR_UNITS:
-                form_pre(u + 1)
-            if u % HALVES == 0 and u // HALVES + 2 < TENSOR_GRAPHS:
-                flip_terms(u // HALVES + 2)
+                form_pre(u + 1, 1)
+            if u + LEAD + 1 < TENSOR_UNITS:
+                form_pre(u + LEAD + 1, 0)

@@ -33,8 +33,9 @@ TINY = 1e-30
 
 HI = 0
 LO = 32
-DIST = 64
-ONE = 67
+ONE = 64
+DIST = 65
+DIST_PARTS = 3
 
 SIDE_GRAPHS = 2
 TENSOR_GRAPHS = GRAPHS - SIDE_GRAPHS
@@ -44,11 +45,9 @@ TENSOR_UNITS = TENSOR_GRAPHS * HALVES
 SIDES = WIDTH // BANK
 PIECE_F = BANK // P
 RUN = 4
-VECTOR_COLUMNS = 256
+VECTOR_COLUMNS = 320
 LEAD = 6
-SPREAD_GRAPHS = 2 * BANK // PAIRS
 EARLY_GRAPHS = (LEAD + HALVES) // HALVES
-MEMSET_GRAPHS = 6
 
 FLOPS = 2 * ALL_NODES * WIDTH * 2 * WIDTH + 2 * GRAPHS * PAIRS * WIDTH * WIDTH
 
@@ -62,7 +61,7 @@ def tile_graphmessagelayer_pa_kernel(tc, node_state, positions, We1, be1, We2, b
 
     with ExitStack() as ctx:
         keep = ctx.enter_context(tc.tile_pool(name="keep", bufs=1))
-        raw_pool = ctx.enter_context(tc.tile_pool(name="raw", bufs=8))
+        raw_pool = ctx.enter_context(tc.tile_pool(name="raw", bufs=12))
         grouped_pool = ctx.enter_context(tc.tile_pool(name="grouped", bufs=3))
         unit_pool = ctx.enter_context(tc.tile_pool(name="unit", bufs=LEAD + 4))
         work = ctx.enter_context(tc.tile_pool(name="work", bufs=4))
@@ -75,11 +74,9 @@ def tile_graphmessagelayer_pa_kernel(tc, node_state, positions, We1, be1, We2, b
         pos_nodes = keep.tile([P, POS_COLUMNS], BF16)
         parts = keep.tile([P, NODE_TILES, 2, 2, WIDTH], BF16)
         terms = keep.tile([P, TENSOR_GRAPHS, WIDTH], BF16)
-        spread_t = keep.tile([P, HALVES, GRAPHS, P], BF16)
         spread = keep.tile([P, GRAPHS, PAIRS], BF16)
         x_rows = keep.tile([P, NODE_TILES, WIDTH], BF16)
         ident_bf = keep.tile([P, P], BF16)
-        ident_f = keep.tile([P, P], F32)
         x_grouped = keep.tile([P, PASSES, ALL_NODES, PACK], BF16, align_bytes=64)
         x_codes = keep.tile([P, PASSES, ALL_NODES], U32, align_bytes=64)
         x_scales = keep.tile([P, PASSES, ALL_NODES], U8, align_bytes=64)
@@ -94,7 +91,6 @@ def tile_graphmessagelayer_pa_kernel(tc, node_state, positions, We1, be1, We2, b
         grouped = {}
         a_ps = {}
         side_ps = {}
-        spread_ps = {}
         pre = {}
         h_grouped = {}
         h_words = {}
@@ -176,18 +172,6 @@ def tile_graphmessagelayer_pa_kernel(tc, node_state, positions, We1, be1, We2, b
         def copy_side(c, w):
             nc.scalar.copy(
                 out=a_side[:, w, c * PIECE_F : (c + 1) * PIECE_F, :], in_=side_ps[w][:, :, P - SIDE_GRAPHS * NODES : P]
-            )
-
-        def flip_spread(q):
-            spread_ps[q] = psum_acc.tile([P, SPREAD_GRAPHS, HALVES, P], BF16, tag="acc", name="spread_ps")
-            for k in range(SPREAD_GRAPHS):
-                for h in range(HALVES):
-                    nc.tensor.transpose(spread_ps[q][:, k, h, :], spread_t[:, h, q * SPREAD_GRAPHS + k, :], ident_bf[:])
-
-        def copy_spread(q):
-            nc.scalar.copy(
-                out=spread[:, q * SPREAD_GRAPHS : (q + 1) * SPREAD_GRAPHS, :].rearrange("p b q -> p (b q)"),
-                in_=spread_ps[q][:].rearrange("p k h n -> p (k h n)"),
             )
 
         def form_pre(u, c):
@@ -272,18 +256,24 @@ def tile_graphmessagelayer_pa_kernel(tc, node_state, positions, We1, be1, We2, b
 
         warm = keep.tile([P, 2], F32)
         nc.vector.memset(warm[:], 1.0)
-        nc.vector.memset(vec_rows[:], 0.0)
         nc.vector.memset(pos_nodes[:], 0.0)
-        nc.scalar.dma_start(out=vec_rows[0:F_TILES, :], in_=be1.rearrange("(r c) -> r c", c=P))
-        nc.scalar.dma_start(
-            out=vec_rows[F_TILES : 2 * F_TILES, :],
-            in_=We1[2 * WIDTH : 2 * WIDTH + 1, :].rearrange("o (r c) -> (o r) c", c=P),
-        )
         with nc.allow_non_contiguous_dma(reason="768 values in runs of 3, once"):
             nc.scalar.dma_start(
                 out=pos_nodes[0:NODES, 0 : GRAPHS * COORDS].rearrange("n (b c) -> n b c", c=COORDS),
                 in_=positions.rearrange("b n c -> n b c"),
             )
+        nc.vector.memset(vec_rows[:], 0.0)
+        nc.scalar.dma_start(out=vec_rows[0:F_TILES, :], in_=be1.rearrange("(r c) -> r c", c=P))
+        nc.scalar.dma_start(
+            out=vec_rows[F_TILES : 2 * F_TILES, :],
+            in_=We1[2 * WIDTH : 2 * WIDTH + 1, :].rearrange("o (r c) -> (o r) c", c=P),
+        )
+        nc.vector.memset(terms[ONE:P, 0, :].bitcast(I32), 0)
+        nc.scalar.dma_start(out=terms[ONE : ONE + 1, 0, :], in_=be1.partition_broadcast(1))
+        nc.scalar.dma_start(
+            out=terms[DIST : DIST + DIST_PARTS, 0, :],
+            in_=We1[2 * WIDTH : 2 * WIDTH + 1, :].rearrange("o f -> (o f)").partition_broadcast(DIST_PARTS),
+        )
         nc.scalar.activation(out=warm[:, 1:2], in_=warm[:, 0:1], func=ACT.Sqrt)
         load_piece(0)
         nc.sync.dma_start(
@@ -291,14 +281,15 @@ def tile_graphmessagelayer_pa_kernel(tc, node_state, positions, We1, be1, We2, b
         )
         for k in range(1, 8):
             load_piece(k)
+        nc.sync.dma_start(
+            out=terms[ONE:P, 1:EARLY_GRAPHS, :],
+            in_=terms[ONE:P, 0:1, :].to_broadcast([P - ONE, EARLY_GRAPHS - 1, WIDTH]),
+        )
+        for k in range(8, 12):
+            load_piece(k)
         make_identity(nc, ident_bf[:])
-
-        spread_words = spread_t[:].rearrange("p h b c -> p (h b c)").bitcast(I32).rearrange("p (r c) -> p r c", c=P // 2)
-        nc.vector.memset(spread_words[:, :, DIST // 2 : P // 2], 0)
-        nc.vector.memset(spread_t[:, :, :, ONE : ONE + 1], 1.0)
-        term_words = terms[:].rearrange("p b f -> p (b f)").bitcast(I32)
-        cut = MEMSET_GRAPHS * WIDTH // 2
-        nc.vector.memset(term_words[DIST:P, 0:cut], 0)
+        dist_columns = keep.tile([P, P], BF16)
+        nc.vector.memset(dist_columns[:], 0.0)
 
         sel = keep.tile([P, HALVES, P], BF16)
         for h in range(HALVES):
@@ -312,6 +303,12 @@ def tile_graphmessagelayer_pa_kernel(tc, node_state, positions, We1, be1, We2, b
         nc.gpsimd.tensor_tensor(
             out=pick[:], in0=ident_bf[:, HI : HI + 2 * NODES], in1=ident_bf[:, LO : LO + 2 * NODES], op=ALU.add
         )
+        nc.gpsimd.tensor_tensor(
+            out=pick[:, 0:NODES],
+            in0=pick[:, 0:NODES],
+            in1=ident_bf[:, ONE : ONE + 1].to_broadcast([P, NODES]),
+            op=ALU.add,
+        )
         pick_pairs = keep.tile([P, NODES, NODES], BF16)
         nc.gpsimd.tensor_tensor(
             out=pick_pairs[:],
@@ -319,26 +316,22 @@ def tile_graphmessagelayer_pa_kernel(tc, node_state, positions, We1, be1, We2, b
             in1=pick[:, NODES : 2 * NODES].unsqueeze(1).to_broadcast([P, NODES, NODES]),
             op=ALU.add,
         )
-        nc.gpsimd.memset(term_words[DIST:P, cut:], 0)
-        make_identity(nc, ident_f[:])
-        pick_t = psum_acc.tile([P, HALVES, P], BF16, tag="acc")
-        for h in range(HALVES):
-            nc.tensor.transpose(
-                pick_t[:, h, :], pick_pairs[:, h * HALF : (h + 1) * HALF, :].rearrange("p i j -> p (i j)"), ident_bf[:]
-            )
-        nc.scalar.copy(
-            out=spread_t[:, :, :, 0:DIST],
-            in_=pick_t[:, :, 0:DIST].unsqueeze(2).to_broadcast([P, HALVES, GRAPHS, DIST]),
+        dist_ones = keep.tile([P, 1], BF16)
+        nc.gpsimd.tensor_tensor(
+            out=dist_ones[:], in0=ident_bf[:, DIST : DIST + 1], in1=ident_bf[:, DIST + 1 : DIST + 2], op=ALU.add
+        )
+        nc.gpsimd.tensor_tensor(
+            out=dist_ones[:], in0=dist_ones[:], in1=ident_bf[:, DIST + 2 : DIST + 3], op=ALU.add
+        )
+        nc.vector.tensor_copy(
+            out=spread[:],
+            in_=pick_pairs[:].rearrange("p i j -> p (i j)").unsqueeze(1).to_broadcast([P, GRAPHS, PAIRS]),
         )
         rel = psum_acc.tile([P, HALVES, POS_COLUMNS], F32, tag="acc")
         for h in range(HALVES):
             nc.tensor.matmul(out=rel[:, h, :], lhsT=sel[:, h, :], rhs=pos_nodes[:], start=True, stop=True)
-        vec_t = psum_acc.tile([P, P], BF16, tag="acc")
-        nc.tensor.transpose(vec_t[:], vec_rows[:], ident_bf[:])
         rel_sq = keep.tile([P, HALVES, POS_COLUMNS], F32)
         nc.scalar.activation(out=rel_sq[:], in_=rel[:], func=ACT.Square)
-
-        regroup(0)
         sq = keep.tile([P, HALVES, GRAPHS], F32)
         nc.vector.tensor_reduce(
             out=sq[:],
@@ -350,18 +343,8 @@ def tile_graphmessagelayer_pa_kernel(tc, node_state, positions, We1, be1, We2, b
         nc.vector.tensor_scalar_max(out=sq_floor[:], in0=sq[:], scalar1=TINY)
         root = keep.tile([P, HALVES, GRAPHS], F32)
         nc.scalar.activation(out=root[:], in_=sq_floor[:], func=ACT.Sqrt)
-        quantise_piece(0)
 
-        for a in range(NODE_TILES):
-            for g in range(PASSES):
-                x_t = psum_pre.tile([P, PACK, P], BF16, tag="pre")
-                for t in range(PACK):
-                    k0 = g * K_PASS + t * P
-                    nc.tensor.transpose(x_t[:, t, :], x_rows[:, a, k0 : k0 + P], ident_bf[:])
-                nc.scalar.copy(out=x_grouped[:, g, a * P : (a + 1) * P, :], in_=x_t[:].rearrange("p t r -> p r t"))
-
-        regroup(1)
-        load_piece(8)
+        regroup(0)
         dist = keep.tile([P, HALVES, GRAPHS], F32)
         nc.vector.scalar_tensor_tensor(
             out=dist[:].rearrange("p h b -> p (h b)"),
@@ -371,121 +354,125 @@ def tile_graphmessagelayer_pa_kernel(tc, node_state, positions, We1, be1, We2, b
             op0=ALU.is_gt,
             op1=ALU.mult,
         )
+        part = [
+            dist_columns[:, k * HALVES * GRAPHS : (k + 1) * HALVES * GRAPHS].rearrange("p (b h) -> p h b", h=HALVES)
+            for k in range(DIST_PARTS)
+        ]
+        for a in range(NODE_TILES):
+            for g in range(PASSES):
+                x_t = psum_pre.tile([P, PACK, P], BF16, tag="pre")
+                for t in range(PACK):
+                    k0 = g * K_PASS + t * P
+                    nc.tensor.transpose(x_t[:, t, :], x_rows[:, a, k0 : k0 + P], ident_bf[:])
+                nc.scalar.copy(out=x_grouped[:, g, a * P : (a + 1) * P, :], in_=x_t[:].rearrange("p t r -> p r t"))
+        vec_t = psum_acc.tile([P, P], BF16, tag="acc")
+        nc.tensor.transpose(vec_t[:], vec_rows[:], ident_bf[:])
+        rest = keep.tile([P, HALVES, GRAPHS], F32)
+        nc.vector.tensor_copy(out=part[0], in_=dist[:])
+        regroup(1)
+        nc.vector.tensor_tensor(out=rest[:], in0=dist[:], in1=part[0], op=ALU.subtract)
+        quantise_piece(0)
+        nc.vector.tensor_copy(out=part[1], in_=rest[:])
         nc.vector.quantize_mx(
             out=x_codes[:].rearrange("p g r -> p (g r)").bitcast(FP8X4),
             scales=x_scales[:].rearrange("p g r -> p (g r)"),
             in_=x_grouped[:].rearrange("p g r t -> p (g r t)"),
         )
-        rest = keep.tile([P, HALVES, GRAPHS], F32)
-        nc.vector.tensor_copy(out=spread_t[:, :, :, DIST], in_=dist[:])
-        quantise_piece(1)
-        nc.vector.tensor_tensor(out=rest[:], in0=dist[:], in1=spread_t[:, :, :, DIST], op=ALU.subtract)
-
+        nc.vector.tensor_tensor(out=part[2], in0=rest[:], in1=part[1], op=ALU.subtract)
+        dist_rows_ps = psum_acc.tile([P, P], BF16, tag="acc")
+        nc.tensor.transpose(dist_rows_ps[:], dist_columns[:], ident_bf[:])
         regroup(2)
-        load_piece(9)
-        nc.vector.tensor_copy(out=spread_t[:, :, :, DIST + 1], in_=rest[:])
+        quantise_piece(1)
         product(0, 0, 0)
         product(0, 0, 1)
-        regroup(3)
-        load_piece(10)
-        nc.vector.tensor_tensor(
-            out=spread_t[:, :, :, DIST + 2], in0=rest[:], in1=spread_t[:, :, :, DIST + 1], op=ALU.subtract
-        )
-        quantise_piece(2)
-        load_piece(11)
-        nc.sync.dma_start(
-            out=terms[DIST:ONE, :, :],
-            in_=We1[2 * WIDTH : 2 * WIDTH + 1, :]
-            .rearrange("o f -> (o f)")
-            .partition_broadcast(ONE - DIST)
-            .unsqueeze(1)
-            .to_broadcast([ONE - DIST, TENSOR_GRAPHS, WIDTH]),
-        )
-        nc.sync.dma_start(
-            out=terms[ONE : ONE + 1, :, :],
-            in_=be1.partition_broadcast(1).unsqueeze(1).to_broadcast([1, TENSOR_GRAPHS, WIDTH]),
-        )
-        nc.sync.dma_start(out=be2_all[:], in_=be2.partition_broadcast(P))
         nc.vector.tensor_copy(out=vecs[:].rearrange("p v f -> p (v f)"), in_=vec_t[:, 0 : 2 * F_TILES])
+        regroup(3)
+        quantise_piece(2)
+        dist_rows = keep.tile([P, P], BF16)
+        nc.scalar.copy(out=dist_rows[:], in_=dist_rows_ps[:])
+        for k in range(DIST_PARTS):
+            rows = slice(k * HALVES * GRAPHS, (k + 1) * HALVES * GRAPHS)
+            nc.sync.dma_start(
+                out=spread[DIST + k : DIST + k + 1, :, :].rearrange("o b q -> o (b q)"), in_=dist_rows[rows, :]
+            )
+        nc.sync.dma_start(out=be2_all[:], in_=be2.partition_broadcast(P))
+        nc.scalar.activation(out=warm[:, 1:2], in_=warm[:, 0:1], func=ACT.Silu)
+        split_product(0, 0, 0)
+        split_product(0, 0, 1)
+        regroup(4)
         quantise_piece(3)
-        dist_rep = keep.tile([P, SIDE_GRAPHS, HALVES, P], F32)
-        nc.gpsimd.tensor_copy(
-            out=dist_rep[:],
-            in_=dist[:, :, TENSOR_GRAPHS:GRAPHS].rearrange("p h b -> p b h").unsqueeze(3).to_broadcast(
-                [P, SIDE_GRAPHS, HALVES, P]
-            ),
-        )
-        flip_spread(0)
-        flip_spread(1)
         product(0, 1, 0)
         product(0, 1, 1)
-        for w in range(2):
-            for a in range(NODE_TILES):
-                split_product(0, w, a)
-        for b in range(EARLY_GRAPHS):
-            place_terms(b, slice(0, BANK))
-        side_product(0, 0)
-        side_product(0, 1)
-        copy_spread(0)
-        copy_side(0, 0)
-        copy_side(0, 1)
-        nc.scalar.activation(out=warm[:, 1:2], in_=warm[:, 0:1], func=ACT.Silu)
-
-        regroup(4)
         regroup(5)
         quantise_piece(4)
-        regroup(6)
-        quantise_piece(5)
-        copy_spread(1)
-        flip_spread(2)
-        flip_spread(3)
-        dist_ps = psum_acc.tile([P, SIDE_GRAPHS, HALVES, P], F32, tag="acc")
+        split_product(0, 1, 0)
+        split_product(0, 1, 1)
+        for b in range(EARLY_GRAPHS):
+            place_terms(b, slice(0, BANK))
+        nc.sync.dma_start(
+            out=terms[ONE:P, EARLY_GRAPHS:TENSOR_GRAPHS, :],
+            in_=terms[ONE:P, 0:1, :].to_broadcast([P - ONE, TENSOR_GRAPHS - EARLY_GRAPHS, WIDTH]),
+        )
+        dist_ps = psum_acc.tile([P, SIDE_GRAPHS, PAIRS], F32, tag="acc")
         for v in range(SIDE_GRAPHS):
-            for h in range(HALVES):
-                nc.tensor.transpose(dist_ps[:, v, h, :], dist_rep[:, v, h, :], ident_f[:])
-        nc.scalar.copy(out=dist_all[:].rearrange("p v q -> p (v q)"), in_=dist_ps[:].rearrange("p v h n -> p (v h n)"))
-        regroup(7)
-        quantise_piece(6)
+            nc.tensor.matmul(
+                out=dist_ps[:, v, :],
+                lhsT=dist_ones[:].to_broadcast([P, P]),
+                rhs=spread[:, TENSOR_GRAPHS + v, :],
+                start=True,
+                stop=True,
+            )
+        side_product(0, 0)
+        side_product(0, 1)
+        regroup(6)
+        nc.scalar.copy(out=dist_all[:], in_=dist_ps[:])
+        copy_side(0, 0)
+        copy_side(0, 1)
+        quantise_piece(5)
         product(1, 0, 0)
         product(1, 0, 1)
-        copy_spread(2)
-        copy_spread(3)
+        for v in range(SIDE_GRAPHS):
+            for f in range(PIECE_F):
+                side_sums(v, f)
+        regroup(7)
+        quantise_piece(6)
+        form_pre(0, 0)
+        form_pre(1, 0)
+        split_product(1, 0, 0)
+        split_product(1, 0, 1)
+        regroup(8)
         quantise_piece(7)
         product(1, 1, 0)
         product(1, 1, 1)
-        regroup(8)
-        for w in range(2):
-            for a in range(NODE_TILES):
-                split_product(1, w, a)
+        activate(0, 0)
+        regroup(9)
+        quantise_piece(8)
+        activate(1, 0)
+        split_product(1, 1, 0)
+        split_product(1, 1, 1)
         for b in range(EARLY_GRAPHS):
             place_terms(b, slice(BANK, WIDTH))
         side_product(1, 0)
         side_product(1, 1)
+        form_pre(2, 0)
+        form_pre(3, 0)
+        regroup(10)
+        quantise_piece(9)
+        activate(2, 0)
+        regroup(11)
+        quantise_piece(10)
         copy_side(1, 0)
         copy_side(1, 1)
         for v in range(SIDE_GRAPHS):
-            for f in range(F_TILES):
+            for f in range(PIECE_F, F_TILES):
                 side_sums(v, f)
-        form_pre(0, 0)
-        regroup(9)
-        quantise_piece(8)
-        form_pre(1, 0)
-        activate(0, 0)
-        regroup(10)
-        quantise_piece(9)
-        form_pre(2, 0)
-        activate(1, 0)
-        regroup(11)
-        quantise_piece(10)
-        form_pre(3, 0)
-        activate(2, 0)
+        activate(3, 0)
         quantise_piece(11)
         for u in range(4, LEAD):
             form_pre(u, 0)
-            activate(u - 1, 0)
-        form_pre(LEAD, 0)
-        activate(LEAD - 1, 0)
+            activate(u, 0)
         form_pre(0, 1)
+        form_pre(LEAD, 0)
 
         for u in range(UNITS + 2):
             if u < UNITS:

@@ -39,14 +39,15 @@ DIST_PARTS = 3
 
 SIDE_GRAPHS = 2
 TENSOR_GRAPHS = GRAPHS - SIDE_GRAPHS
+SIDE_EVERY = 4
 UNITS = GRAPHS * HALVES
-TENSOR_UNITS = TENSOR_GRAPHS * HALVES
+
 
 SIDES = WIDTH // BANK
 PIECE_F = BANK // P
 RUN = 4
 VECTOR_COLUMNS = 320
-LEAD = 6
+LEAD = 4
 EARLY_GRAPHS = (LEAD + HALVES) // HALVES
 
 FLOPS = 2 * ALL_NODES * WIDTH * 2 * WIDTH + 2 * GRAPHS * PAIRS * WIDTH * WIDTH
@@ -58,6 +59,10 @@ def tile_graphmessagelayer_pa_kernel(tc, node_state, positions, We1, be1, We2, b
     weight_rows = [We1[0:WIDTH, :], We1[WIDTH : 2 * WIDTH, :], We2]
     pieces = [(w, g, c) for c in range(SIDES) for w in range(2) for g in range(PASSES)]
     pieces += [(2, g, c) for c in range(SIDES) for g in range(PASSES)]
+    side_places = [GRAPHS - 1 - SIDE_EVERY * v for v in reversed(range(SIDE_GRAPHS))]
+    order = list(range(TENSOR_GRAPHS))
+    for v, place in enumerate(side_places):
+        order.insert(place, TENSOR_GRAPHS + v)
 
     with ExitStack() as ctx:
         keep = ctx.enter_context(tc.tile_pool(name="keep", bufs=1))
@@ -175,7 +180,9 @@ def tile_graphmessagelayer_pa_kernel(tc, node_state, positions, We1, be1, We2, b
             )
 
         def form_pre(u, c):
-            b, h = divmod(u, HALVES)
+            b, h = order[u // HALVES], u % HALVES
+            if b >= TENSOR_GRAPHS:
+                return
             pre[u, c] = psum_pre.tile([P, PACK, P], F32, tag="pre", name="pre_ps")
             for t in range(PACK):
                 f = c * PIECE_F + t
@@ -214,10 +221,11 @@ def tile_graphmessagelayer_pa_kernel(tc, node_state, positions, We1, be1, We2, b
         def activate(u, c):
             if c == 0:
                 h_grouped[u] = unit_pool.tile([P, PASSES, P, PACK], BF16, align_bytes=64, tag="h", name="h_grouped")
-            if u < TENSOR_UNITS:
+            b, h = order[u // HALVES], u % HALVES
+            if b < TENSOR_GRAPHS:
                 source = pre[u, c][:]
             else:
-                v, h = divmod(u - TENSOR_UNITS, HALVES)
+                v = b - TENSOR_GRAPHS
                 source = sums[:, v, c * PACK : (c + 1) * PACK, h * P : (h + 1) * P]
             nc.scalar.activation(out=h_grouped[u][:, c, :, :], in_=source.rearrange("p t r -> p r t"), func=ACT.Silu)
 
@@ -252,7 +260,8 @@ def tile_graphmessagelayer_pa_kernel(tc, node_state, positions, We1, be1, We2, b
                     in1=be2_all[:, m * BANK : (m + 1) * BANK],
                     op=ALU.add,
                 )
-            nc.sync.dma_start(out=out_rows[u * P : (u + 1) * P, :], in_=msg[:])
+            r0 = order[u // HALVES] * PAIRS + u % HALVES * P
+            nc.sync.dma_start(out=out_rows[r0 : r0 + P, :], in_=msg[:])
 
         warm = keep.tile([P, 2], F32)
         nc.vector.memset(warm[:], 1.0)
@@ -413,27 +422,14 @@ def tile_graphmessagelayer_pa_kernel(tc, node_state, positions, We1, be1, We2, b
             out=terms[ONE:P, EARLY_GRAPHS:TENSOR_GRAPHS, :],
             in_=terms[ONE:P, 0:1, :].to_broadcast([P - ONE, TENSOR_GRAPHS - EARLY_GRAPHS, WIDTH]),
         )
-        dist_ps = psum_acc.tile([P, SIDE_GRAPHS, PAIRS], F32, tag="acc")
-        for v in range(SIDE_GRAPHS):
-            nc.tensor.matmul(
-                out=dist_ps[:, v, :],
-                lhsT=dist_ones[:].to_broadcast([P, P]),
-                rhs=spread[:, TENSOR_GRAPHS + v, :],
-                start=True,
-                stop=True,
-            )
         side_product(0, 0)
         side_product(0, 1)
         regroup(6)
-        nc.scalar.copy(out=dist_all[:], in_=dist_ps[:])
         copy_side(0, 0)
         copy_side(0, 1)
         quantise_piece(5)
         product(1, 0, 0)
         product(1, 0, 1)
-        for v in range(SIDE_GRAPHS):
-            for f in range(PIECE_F):
-                side_sums(v, f)
         regroup(7)
         quantise_piece(6)
         form_pre(0, 0)
@@ -463,11 +459,24 @@ def tile_graphmessagelayer_pa_kernel(tc, node_state, positions, We1, be1, We2, b
         quantise_piece(10)
         copy_side(1, 0)
         copy_side(1, 1)
-        for v in range(SIDE_GRAPHS):
-            for f in range(PIECE_F, F_TILES):
-                side_sums(v, f)
+        dist_ps = []
+        for v in range(0, SIDE_GRAPHS, 2):
+            n = min(2, SIDE_GRAPHS - v)
+            dist_ps.append(psum_acc.tile([P, n, PAIRS], F32, tag="acc", name="dist_ps"))
+            nc.tensor.matmul(
+                out=dist_ps[-1][:].rearrange("p v q -> p (v q)"),
+                lhsT=dist_ones[:].to_broadcast([P, P]),
+                rhs=spread[:, TENSOR_GRAPHS + v : TENSOR_GRAPHS + v + n, :].rearrange("p v q -> p (v q)"),
+                start=True,
+                stop=True,
+            )
         activate(3, 0)
         quantise_piece(11)
+        for k, d in enumerate(dist_ps):
+            nc.scalar.copy(out=dist_all[:, 2 * k : min(2 * k + 2, SIDE_GRAPHS), :], in_=d[:])
+        for v in range(SIDE_GRAPHS):
+            for f in range(F_TILES):
+                side_sums(v, f)
         for u in range(4, LEAD):
             form_pre(u, 0)
             activate(u, 0)
@@ -485,7 +494,7 @@ def tile_graphmessagelayer_pa_kernel(tc, node_state, positions, We1, be1, We2, b
                 quantise(u - 1)
             if u >= 2:
                 multiply(u - 2)
-            if u + 1 < TENSOR_UNITS:
+            if u + 1 < UNITS:
                 form_pre(u + 1, 1)
-            if u + LEAD + 1 < TENSOR_UNITS:
+            if u + LEAD + 1 < UNITS:
                 form_pre(u + LEAD + 1, 0)

@@ -57,8 +57,8 @@ def tile_graphmessagelayer_pa_kernel(tc, node_state, positions, We1, be1, We2, b
     nc = tc.nc
     out_rows = out.rearrange("b i j m -> (b i j) m")
     weight_rows = [We1[0:WIDTH, :], We1[WIDTH : 2 * WIDTH, :], We2]
-    pieces = [(w, g, c) for c in range(SIDES) for w in range(2) for g in range(PASSES)]
-    pieces += [(2, g, c) for c in range(SIDES) for g in range(PASSES)]
+    pieces = [(0, g, c) for g in range(PASSES) for c in range(SIDES)]
+    pieces += [(w, g, c) for w in (1, 2) for c in range(SIDES) for g in range(PASSES)]
     side_places = [GRAPHS - 1 - SIDE_EVERY * v for v in reversed(range(SIDE_GRAPHS))]
     order = list(range(TENSOR_GRAPHS))
     for v, place in enumerate(side_places):
@@ -66,7 +66,7 @@ def tile_graphmessagelayer_pa_kernel(tc, node_state, positions, We1, be1, We2, b
 
     with ExitStack() as ctx:
         keep = ctx.enter_context(tc.tile_pool(name="keep", bufs=1))
-        raw_pool = ctx.enter_context(tc.tile_pool(name="raw", bufs=12))
+        raw_pool = ctx.enter_context(tc.tile_pool(name="raw", bufs=6))
         grouped_pool = ctx.enter_context(tc.tile_pool(name="grouped", bufs=3))
         unit_pool = ctx.enter_context(tc.tile_pool(name="unit", bufs=LEAD + 4))
         work = ctx.enter_context(tc.tile_pool(name="work", bufs=4))
@@ -100,26 +100,25 @@ def tile_graphmessagelayer_pa_kernel(tc, node_state, positions, We1, be1, We2, b
         h_grouped = {}
         h_words = {}
 
-        def load_piece(k):
-            w, g, c = pieces[k]
-            raw[k] = raw_pool.tile([P, PACK, BANK], BF16, tag="raw", name="raw")
-            nc.sync.dma_start(
-                out=raw[k][:],
-                in_=weight_rows[w][g * K_PASS : (g + 1) * K_PASS, c * BANK : (c + 1) * BANK].rearrange(
-                    "(t p) n -> p t n", p=P
-                ),
-            )
+        def load_weight(w, g, columns=slice(0, WIDTH)):
+            if (w, g) not in raw:
+                raw[w, g] = raw_pool.tile([P, PACK, WIDTH], BF16, tag="raw", name="raw")
+            words = "(p t) n -> p t n" if w < 2 else "(t p) n -> p t n"
+            source = weight_rows[w][g * K_PASS : (g + 1) * K_PASS, :].rearrange(words, p=P)
+            nc.sync.dma_start(out=raw[w, g][:, :, columns], in_=source[:, :, columns])
 
         def regroup(k):
+            w, g, c = pieces[k]
             grouped[k] = grouped_pool.tile([P, BANK, PACK], BF16, align_bytes=64, tag="grouped", name="grouped")
+            source = raw[w, g][:, :, c * BANK : (c + 1) * BANK]
             cut = VECTOR_COLUMNS
             nc.vector.tensor_copy(
                 out=grouped[k][:, 0:cut, :].rearrange("p (c i) t -> p c t i", i=RUN),
-                in_=raw[k][:, :, 0:cut].rearrange("p t (c i) -> p c t i", i=RUN),
+                in_=source[:, :, 0:cut].rearrange("p t (c i) -> p c t i", i=RUN),
             )
             nc.scalar.copy(
                 out=grouped[k][:, cut:BANK, :].rearrange("p (c i) t -> p c t i", i=RUN),
-                in_=raw[k][:, :, cut:BANK].rearrange("p t (c i) -> p c t i", i=RUN),
+                in_=source[:, :, cut:BANK].rearrange("p t (c i) -> p c t i", i=RUN),
             )
 
         def quantise_piece(k):
@@ -131,10 +130,10 @@ def tile_graphmessagelayer_pa_kernel(tc, node_state, positions, We1, be1, We2, b
             )
 
         def product(c, w, a):
-            a_ps[w, a] = psum_pre.tile([P, BANK], F32, tag="pre", name="a_ps")
+            a_ps[c, w, a] = psum_pre.tile([P, BANK], F32, tag="pre", name="a_ps")
             for g in range(PASSES):
                 nc.tensor.matmul_mx(
-                    out=a_ps[w, a][:],
+                    out=a_ps[c, w, a][:],
                     lhsT=x_codes[:, g, a * P : (a + 1) * P].bitcast(FP8X4),
                     lhsT_scale=x_scales[:, g, a * P : (a + 1) * P],
                     rhs=w_codes[:, w, g, c * BANK : (c + 1) * BANK].bitcast(FP8X4),
@@ -145,27 +144,26 @@ def tile_graphmessagelayer_pa_kernel(tc, node_state, positions, We1, be1, We2, b
 
         def split_product(c, w, a):
             columns = slice(c * BANK, (c + 1) * BANK)
-            nc.scalar.copy(out=parts[:, a, w, 0, columns], in_=a_ps[w, a][:])
+            nc.scalar.copy(out=parts[:, a, w, 0, columns], in_=a_ps[c, w, a][:])
             nc.vector.tensor_tensor(
-                out=parts[:, a, w, 1, columns], in0=a_ps[w, a][:], in1=parts[:, a, w, 0, columns], op=ALU.subtract
+                out=parts[:, a, w, 1, columns], in0=a_ps[c, w, a][:], in1=parts[:, a, w, 0, columns], op=ALU.subtract
             )
 
-        def place_terms(b, columns):
+        def place_terms(b, w, columns):
             a, n0 = divmod(b * NODES, P)
             for s in range(2):
-                for w in range(2):
-                    row = (2 * s + w) * NODES
-                    nc.sync.dma_start(
-                        out=terms[row : row + NODES, b, columns], in_=parts[n0 : n0 + NODES, a, w, s, columns]
-                    )
+                row = (2 * s + w) * NODES
+                nc.sync.dma_start(
+                    out=terms[row : row + NODES, b, columns], in_=parts[n0 : n0 + NODES, a, w, s, columns]
+                )
 
         def side_product(c, w):
-            side_ps[w] = psum_acc.tile([P, PIECE_F, P], F32, tag="acc", name="side_ps")
+            side_ps[c, w] = psum_acc.tile([P, PIECE_F, P], F32, tag="acc", name="side_ps")
             for e in range(PIECE_F):
                 f0 = c * BANK + e * P
                 for g in range(PASSES):
                     nc.tensor.matmul_mx(
-                        out=side_ps[w][:, e, :],
+                        out=side_ps[c, w][:, e, :],
                         lhsT=w_codes[:, w, g, f0 : f0 + P].bitcast(FP8X4),
                         lhsT_scale=w_scales[:, w, g, f0 : f0 + P],
                         rhs=x_codes[:, g, ALL_NODES - P : ALL_NODES].bitcast(FP8X4),
@@ -176,7 +174,7 @@ def tile_graphmessagelayer_pa_kernel(tc, node_state, positions, We1, be1, We2, b
 
         def copy_side(c, w):
             nc.scalar.copy(
-                out=a_side[:, w, c * PIECE_F : (c + 1) * PIECE_F, :], in_=side_ps[w][:, :, P - SIDE_GRAPHS * NODES : P]
+                out=a_side[:, w, c * PIECE_F : (c + 1) * PIECE_F, :], in_=side_ps[c, w][:, :, P - SIDE_GRAPHS * NODES : P]
             )
 
         def form_pre(u, c):
@@ -284,18 +282,24 @@ def tile_graphmessagelayer_pa_kernel(tc, node_state, positions, We1, be1, We2, b
             in_=We1[2 * WIDTH : 2 * WIDTH + 1, :].rearrange("o f -> (o f)").partition_broadcast(DIST_PARTS),
         )
         nc.scalar.activation(out=warm[:, 1:2], in_=warm[:, 0:1], func=ACT.Sqrt)
-        load_piece(0)
+        load_weight(0, 0, slice(0, BANK))
         nc.sync.dma_start(
             out=x_rows[:], in_=node_state.rearrange("b n h -> (b n) h").rearrange("(a p) h -> p a h", p=P)
         )
-        for k in range(1, 8):
-            load_piece(k)
+        load_weight(0, 0, slice(BANK, WIDTH))
+        load_weight(0, 1)
+        load_weight(1, 0)
+        load_weight(1, 1)
         nc.sync.dma_start(
             out=terms[ONE:P, 1:EARLY_GRAPHS, :],
             in_=terms[ONE:P, 0:1, :].to_broadcast([P - ONE, EARLY_GRAPHS - 1, WIDTH]),
         )
-        for k in range(8, 12):
-            load_piece(k)
+        load_weight(2, 0)
+        load_weight(2, 1)
+        nc.sync.dma_start(
+            out=terms[ONE:P, EARLY_GRAPHS:TENSOR_GRAPHS, :],
+            in_=terms[ONE:P, 0:1, :].to_broadcast([P - ONE, TENSOR_GRAPHS - EARLY_GRAPHS, WIDTH]),
+        )
         make_identity(nc, ident_bf[:])
         dist_columns = keep.tile([P, P], BF16)
         nc.vector.memset(dist_columns[:], 0.0)
@@ -371,8 +375,8 @@ def tile_graphmessagelayer_pa_kernel(tc, node_state, positions, We1, be1, We2, b
             for g in range(PASSES):
                 x_t = psum_pre.tile([P, PACK, P], BF16, tag="pre")
                 for t in range(PACK):
-                    k0 = g * K_PASS + t * P
-                    nc.tensor.transpose(x_t[:, t, :], x_rows[:, a, k0 : k0 + P], ident_bf[:])
+                    columns = slice(g * K_PASS + t, (g + 1) * K_PASS, PACK)
+                    nc.tensor.transpose(x_t[:, t, :], x_rows[:, a, columns], ident_bf[:])
                 nc.scalar.copy(out=x_grouped[:, g, a * P : (a + 1) * P, :], in_=x_t[:].rearrange("p t r -> p r t"))
         vec_t = psum_acc.tile([P, P], BF16, tag="acc")
         nc.tensor.transpose(vec_t[:], vec_rows[:], ident_bf[:])
@@ -392,11 +396,11 @@ def tile_graphmessagelayer_pa_kernel(tc, node_state, positions, We1, be1, We2, b
         nc.tensor.transpose(dist_rows_ps[:], dist_columns[:], ident_bf[:])
         regroup(2)
         quantise_piece(1)
-        product(0, 0, 0)
-        product(0, 0, 1)
         nc.vector.tensor_copy(out=vecs[:].rearrange("p v f -> p (v f)"), in_=vec_t[:, 0 : 2 * F_TILES])
         regroup(3)
         quantise_piece(2)
+        product(0, 0, 0)
+        product(0, 0, 1)
         dist_rows = keep.tile([P, P], BF16)
         nc.scalar.copy(out=dist_rows[:], in_=dist_rows_ps[:])
         for k in range(DIST_PARTS):
@@ -406,59 +410,57 @@ def tile_graphmessagelayer_pa_kernel(tc, node_state, positions, We1, be1, We2, b
             )
         nc.sync.dma_start(out=be2_all[:], in_=be2.partition_broadcast(P))
         nc.scalar.activation(out=warm[:, 1:2], in_=warm[:, 0:1], func=ACT.Silu)
-        split_product(0, 0, 0)
-        split_product(0, 0, 1)
         regroup(4)
         quantise_piece(3)
-        product(0, 1, 0)
-        product(0, 1, 1)
+        product(1, 0, 0)
+        product(1, 0, 1)
+        split_product(0, 0, 0)
+        split_product(0, 0, 1)
         regroup(5)
         quantise_piece(4)
+        split_product(1, 0, 0)
+        split_product(1, 0, 1)
+        for b in range(EARLY_GRAPHS):
+            place_terms(b, 0, slice(0, WIDTH))
+        side_product(0, 0)
+        side_product(1, 0)
+        regroup(6)
+        quantise_piece(5)
+        product(0, 1, 0)
+        product(0, 1, 1)
+        copy_side(0, 0)
+        copy_side(1, 0)
+        regroup(7)
+        quantise_piece(6)
         split_product(0, 1, 0)
         split_product(0, 1, 1)
         for b in range(EARLY_GRAPHS):
-            place_terms(b, slice(0, BANK))
-        nc.sync.dma_start(
-            out=terms[ONE:P, EARLY_GRAPHS:TENSOR_GRAPHS, :],
-            in_=terms[ONE:P, 0:1, :].to_broadcast([P - ONE, TENSOR_GRAPHS - EARLY_GRAPHS, WIDTH]),
-        )
-        side_product(0, 0)
-        side_product(0, 1)
-        regroup(6)
-        copy_side(0, 0)
-        copy_side(0, 1)
-        quantise_piece(5)
-        product(1, 0, 0)
-        product(1, 0, 1)
-        regroup(7)
-        quantise_piece(6)
-        form_pre(0, 0)
-        form_pre(1, 0)
-        split_product(1, 0, 0)
-        split_product(1, 0, 1)
+            place_terms(b, 1, slice(0, BANK))
         regroup(8)
         quantise_piece(7)
         product(1, 1, 0)
         product(1, 1, 1)
-        activate(0, 0)
         regroup(9)
         quantise_piece(8)
-        activate(1, 0)
         split_product(1, 1, 0)
         split_product(1, 1, 1)
         for b in range(EARLY_GRAPHS):
-            place_terms(b, slice(BANK, WIDTH))
-        side_product(1, 0)
+            place_terms(b, 1, slice(BANK, WIDTH))
+        side_product(0, 1)
         side_product(1, 1)
-        form_pre(2, 0)
-        form_pre(3, 0)
+        form_pre(0, 0)
+        form_pre(1, 0)
         regroup(10)
         quantise_piece(9)
-        activate(2, 0)
         regroup(11)
+        activate(0, 0)
+        form_pre(2, 0)
         quantise_piece(10)
-        copy_side(1, 0)
+        activate(1, 0)
+        form_pre(3, 0)
+        copy_side(0, 1)
         copy_side(1, 1)
+        activate(2, 0)
         dist_ps = []
         for v in range(0, SIDE_GRAPHS, 2):
             n = min(2, SIDE_GRAPHS - v)
@@ -477,9 +479,6 @@ def tile_graphmessagelayer_pa_kernel(tc, node_state, positions, We1, be1, We2, b
         for v in range(SIDE_GRAPHS):
             for f in range(F_TILES):
                 side_sums(v, f)
-        for u in range(4, LEAD):
-            form_pre(u, 0)
-            activate(u, 0)
         form_pre(0, 1)
         form_pre(LEAD, 0)
 
@@ -489,7 +488,8 @@ def tile_graphmessagelayer_pa_kernel(tc, node_state, positions, We1, be1, We2, b
             if u + LEAD < UNITS:
                 activate(u + LEAD, 0)
             if EARLY_GRAPHS + u < TENSOR_GRAPHS:
-                place_terms(EARLY_GRAPHS + u, slice(0, WIDTH))
+                place_terms(EARLY_GRAPHS + u, 0, slice(0, WIDTH))
+                place_terms(EARLY_GRAPHS + u, 1, slice(0, WIDTH))
             if 1 <= u <= UNITS:
                 quantise(u - 1)
             if u >= 2:

@@ -49,6 +49,7 @@ RUN = 4
 VECTOR_COLUMNS = 320
 LEAD = 4
 EARLY_GRAPHS = (LEAD + HALVES) // HALVES
+SLOTS = 5
 
 FLOPS = 2 * ALL_NODES * WIDTH * 2 * WIDTH + 2 * GRAPHS * PAIRS * WIDTH * WIDTH
 
@@ -78,7 +79,7 @@ def tile_graphmessagelayer_pa_kernel(tc, node_state, positions, We1, be1, We2, b
         vec_rows = keep.tile([P, P], BF16)
         pos_nodes = keep.tile([P, POS_COLUMNS], BF16)
         parts = keep.tile([P, NODE_TILES, 2, 2, WIDTH], BF16)
-        terms = keep.tile([P, TENSOR_GRAPHS, WIDTH], BF16)
+        terms = keep.tile([P, SLOTS, WIDTH], BF16)
         spread = keep.tile([P, GRAPHS, PAIRS], BF16)
         x_rows = keep.tile([P, NODE_TILES, WIDTH], BF16)
         ident_bf = keep.tile([P, P], BF16)
@@ -154,7 +155,7 @@ def tile_graphmessagelayer_pa_kernel(tc, node_state, positions, We1, be1, We2, b
             for s in range(2):
                 row = (2 * s + w) * NODES
                 nc.sync.dma_start(
-                    out=terms[row : row + NODES, b, columns], in_=parts[n0 : n0 + NODES, a, w, s, columns]
+                    out=terms[row : row + NODES, b % SLOTS, columns], in_=parts[n0 : n0 + NODES, a, w, s, columns]
                 )
 
         def side_product(c, w):
@@ -186,7 +187,7 @@ def tile_graphmessagelayer_pa_kernel(tc, node_state, positions, We1, be1, We2, b
                 f = c * PIECE_F + t
                 nc.tensor.matmul(
                     out=pre[u, c][:, t, :],
-                    lhsT=terms[:, b, f * P : (f + 1) * P],
+                    lhsT=terms[:, b % SLOTS, f * P : (f + 1) * P],
                     rhs=spread[:, b, h * P : (h + 1) * P],
                     start=True,
                     stop=True,
@@ -264,25 +265,22 @@ def tile_graphmessagelayer_pa_kernel(tc, node_state, positions, We1, be1, We2, b
         warm = keep.tile([P, 2], F32)
         nc.vector.memset(warm[:], 1.0)
         nc.vector.memset(pos_nodes[:], 0.0)
-        with nc.allow_non_contiguous_dma(reason="768 values in runs of 3, once"):
-            nc.scalar.dma_start(
-                out=pos_nodes[0:NODES, 0 : GRAPHS * COORDS].rearrange("n (b c) -> n b c", c=COORDS),
-                in_=positions.rearrange("b n c -> n b c"),
-            )
         nc.vector.memset(vec_rows[:], 0.0)
+        dist_columns = keep.tile([P, P], BF16)
+        nc.vector.memset(dist_columns[:], 0.0)
+        nc.vector.memset(terms[ONE:P, :, :].rearrange("p s f -> p (s f)").bitcast(I32), 0)
         nc.scalar.dma_start(out=vec_rows[0:F_TILES, :], in_=be1.rearrange("(r c) -> r c", c=P))
         nc.scalar.dma_start(
             out=vec_rows[F_TILES : 2 * F_TILES, :],
             in_=We1[2 * WIDTH : 2 * WIDTH + 1, :].rearrange("o (r c) -> (o r) c", c=P),
         )
-        nc.vector.memset(terms[ONE:P, 0, :].bitcast(I32), 0)
-        nc.scalar.dma_start(out=terms[ONE : ONE + 1, 0, :], in_=be1.partition_broadcast(1))
-        nc.scalar.dma_start(
-            out=terms[DIST : DIST + DIST_PARTS, 0, :],
-            in_=We1[2 * WIDTH : 2 * WIDTH + 1, :].rearrange("o f -> (o f)").partition_broadcast(DIST_PARTS),
-        )
         nc.scalar.activation(out=warm[:, 1:2], in_=warm[:, 0:1], func=ACT.Sqrt)
         load_weight(0, 0, slice(0, BANK))
+        with nc.allow_non_contiguous_dma(reason="768 values in runs of 3, once"):
+            nc.sync.dma_start(
+                out=pos_nodes[0:NODES, 0 : GRAPHS * COORDS].rearrange("n (b c) -> n b c", c=COORDS),
+                in_=positions.rearrange("b n c -> n b c"),
+            )
         nc.sync.dma_start(
             out=x_rows[:], in_=node_state.rearrange("b n h -> (b n) h").rearrange("(a p) h -> p a h", p=P)
         )
@@ -290,19 +288,21 @@ def tile_graphmessagelayer_pa_kernel(tc, node_state, positions, We1, be1, We2, b
         load_weight(0, 1)
         load_weight(1, 0)
         load_weight(1, 1)
-        nc.sync.dma_start(
-            out=terms[ONE:P, 1:EARLY_GRAPHS, :],
-            in_=terms[ONE:P, 0:1, :].to_broadcast([P - ONE, EARLY_GRAPHS - 1, WIDTH]),
-        )
         load_weight(2, 0)
         load_weight(2, 1)
         nc.sync.dma_start(
-            out=terms[ONE:P, EARLY_GRAPHS:TENSOR_GRAPHS, :],
-            in_=terms[ONE:P, 0:1, :].to_broadcast([P - ONE, TENSOR_GRAPHS - EARLY_GRAPHS, WIDTH]),
+            out=terms[ONE : ONE + 1, :, :],
+            in_=be1.partition_broadcast(1).unsqueeze(1).to_broadcast([1, SLOTS, WIDTH]),
+        )
+        nc.sync.dma_start(
+            out=terms[DIST : DIST + DIST_PARTS, :, :],
+            in_=We1[2 * WIDTH : 2 * WIDTH + 1, :]
+            .rearrange("o f -> (o f)")
+            .partition_broadcast(DIST_PARTS)
+            .unsqueeze(1)
+            .to_broadcast([DIST_PARTS, SLOTS, WIDTH]),
         )
         make_identity(nc, ident_bf[:])
-        dist_columns = keep.tile([P, P], BF16)
-        nc.vector.memset(dist_columns[:], 0.0)
 
         sel = keep.tile([P, HALVES, P], BF16)
         for h in range(HALVES):
@@ -446,6 +446,9 @@ def tile_graphmessagelayer_pa_kernel(tc, node_state, positions, We1, be1, We2, b
         split_product(1, 1, 1)
         for b in range(EARLY_GRAPHS):
             place_terms(b, 1, slice(BANK, WIDTH))
+        for b in range(EARLY_GRAPHS, SLOTS):
+            for w in range(2):
+                place_terms(b, w, slice(0, WIDTH))
         side_product(0, 1)
         side_product(1, 1)
         form_pre(0, 0)
@@ -487,9 +490,10 @@ def tile_graphmessagelayer_pa_kernel(tc, node_state, positions, We1, be1, We2, b
                 activate(u, 1)
             if u + LEAD < UNITS:
                 activate(u + LEAD, 0)
-            if EARLY_GRAPHS + u < TENSOR_GRAPHS:
-                place_terms(EARLY_GRAPHS + u, 0, slice(0, WIDTH))
-                place_terms(EARLY_GRAPHS + u, 1, slice(0, WIDTH))
+            k, h = divmod(u, HALVES)
+            if h == HALVES - 1 and k < GRAPHS and order[k] + SLOTS < TENSOR_GRAPHS:
+                for w in range(2):
+                    place_terms(order[k] + SLOTS, w, slice(0, WIDTH))
             if 1 <= u <= UNITS:
                 quantise(u - 1)
             if u >= 2:

@@ -37,7 +37,7 @@ ONE = 64
 DIST = 65
 DIST_PARTS = 3
 
-SIDE_GRAPHS = 2
+SIDE_GRAPHS = 3
 TENSOR_GRAPHS = GRAPHS - SIDE_GRAPHS
 SIDE_EVERY = 4
 UNITS = GRAPHS * HALVES
@@ -47,7 +47,8 @@ SIDES = WIDTH // BANK
 PIECE_F = BANK // P
 RUN = 4
 VECTOR_COLUMNS = 320
-LEAD = 4
+SIDE_RATE = 1
+LEAD = 2
 EARLY_GRAPHS = (LEAD + HALVES) // HALVES
 SLOTS = 5
 
@@ -108,19 +109,17 @@ def tile_graphmessagelayer_pa_kernel(tc, node_state, positions, We1, be1, We2, b
             source = weight_rows[w][g * K_PASS : (g + 1) * K_PASS, :].rearrange(words, p=P)
             nc.sync.dma_start(out=raw[w, g][:, :, columns], in_=source[:, :, columns])
 
-        def regroup(k):
+        def regroup_columns(k, engine_copy, columns):
             w, g, c = pieces[k]
+            engine_copy(
+                out=grouped[k][:, columns, :].rearrange("p (c i) t -> p c t i", i=RUN),
+                in_=raw[w, g][:, :, c * BANK : (c + 1) * BANK][:, :, columns].rearrange("p t (c i) -> p c t i", i=RUN),
+            )
+
+        def regroup(k):
             grouped[k] = grouped_pool.tile([P, BANK, PACK], BF16, align_bytes=64, tag="grouped", name="grouped")
-            source = raw[w, g][:, :, c * BANK : (c + 1) * BANK]
-            cut = VECTOR_COLUMNS
-            nc.vector.tensor_copy(
-                out=grouped[k][:, 0:cut, :].rearrange("p (c i) t -> p c t i", i=RUN),
-                in_=source[:, :, 0:cut].rearrange("p t (c i) -> p c t i", i=RUN),
-            )
-            nc.scalar.copy(
-                out=grouped[k][:, cut:BANK, :].rearrange("p (c i) t -> p c t i", i=RUN),
-                in_=source[:, :, cut:BANK].rearrange("p t (c i) -> p c t i", i=RUN),
-            )
+            regroup_columns(k, nc.vector.tensor_copy, slice(0, VECTOR_COLUMNS))
+            regroup_columns(k, nc.scalar.copy, slice(VECTOR_COLUMNS, BANK))
 
         def quantise_piece(k):
             w, g, c = pieces[k]
@@ -130,9 +129,10 @@ def tile_graphmessagelayer_pa_kernel(tc, node_state, positions, We1, be1, We2, b
                 in_=grouped[k][:].rearrange("p n t -> p (n t)"),
             )
 
-        def product(c, w, a):
-            a_ps[c, w, a] = psum_pre.tile([P, BANK], F32, tag="pre", name="a_ps")
-            for g in range(PASSES):
+        def product(c, w, g):
+            for a in range(NODE_TILES):
+                if g == 0:
+                    a_ps[c, w, a] = psum_pre.tile([P, BANK], F32, tag="pre", name="a_ps")
                 nc.tensor.matmul_mx(
                     out=a_ps[c, w, a][:],
                     lhsT=x_codes[:, g, a * P : (a + 1) * P].bitcast(FP8X4),
@@ -142,6 +142,10 @@ def tile_graphmessagelayer_pa_kernel(tc, node_state, positions, We1, be1, We2, b
                     start=(g == 0),
                     stop=(g == PASSES - 1),
                 )
+
+        def split_products(c, w):
+            for a in range(NODE_TILES):
+                split_product(c, w, a)
 
         def split_product(c, w, a):
             columns = slice(c * BANK, (c + 1) * BANK)
@@ -196,13 +200,12 @@ def tile_graphmessagelayer_pa_kernel(tc, node_state, positions, We1, be1, We2, b
         def side_sums(v, f):
             nodes = slice(v * NODES, (v + 1) * NODES)
             by_pair = sums[:, v, f, :].rearrange("p (i j) -> p i j", j=NODES)
-            nc.gpsimd.tensor_scalar(
+            nc.scalar.activation(
                 out=sums[:, v, f, :],
-                in0=dist_all[:, v, :],
-                scalar1=vecs[:, 1, f : f + 1],
-                scalar2=vecs[:, 0, f : f + 1],
-                op0=ALU.mult,
-                op1=ALU.add,
+                in_=dist_all[:, v, :],
+                func=ACT.Identity,
+                scale=vecs[:, 1, f : f + 1],
+                bias=vecs[:, 0, f : f + 1],
             )
             nc.gpsimd.tensor_tensor(
                 out=by_pair,
@@ -397,9 +400,10 @@ def tile_graphmessagelayer_pa_kernel(tc, node_state, positions, We1, be1, We2, b
         regroup(2)
         quantise_piece(1)
         nc.vector.tensor_copy(out=vecs[:].rearrange("p v f -> p (v f)"), in_=vec_t[:, 0 : 2 * F_TILES])
+        product(0, 0, 0)
+        product(1, 0, 0)
         regroup(3)
         quantise_piece(2)
-        product(0, 0, 0)
         product(0, 0, 1)
         dist_rows = keep.tile([P, P], BF16)
         nc.scalar.copy(out=dist_rows[:], in_=dist_rows_ps[:])
@@ -412,78 +416,53 @@ def tile_graphmessagelayer_pa_kernel(tc, node_state, positions, We1, be1, We2, b
         nc.scalar.activation(out=warm[:, 1:2], in_=warm[:, 0:1], func=ACT.Silu)
         regroup(4)
         quantise_piece(3)
-        product(1, 0, 0)
         product(1, 0, 1)
-        split_product(0, 0, 0)
-        split_product(0, 0, 1)
+        split_products(0, 0)
         regroup(5)
         quantise_piece(4)
-        split_product(1, 0, 0)
-        split_product(1, 0, 1)
+        product(0, 1, 0)
+        split_products(1, 0)
         for b in range(EARLY_GRAPHS):
             place_terms(b, 0, slice(0, WIDTH))
         side_product(0, 0)
         side_product(1, 0)
         regroup(6)
         quantise_piece(5)
-        product(0, 1, 0)
         product(0, 1, 1)
-        copy_side(0, 0)
-        copy_side(1, 0)
         regroup(7)
         quantise_piece(6)
-        split_product(0, 1, 0)
-        split_product(0, 1, 1)
+        product(1, 1, 0)
+        split_products(0, 1)
         for b in range(EARLY_GRAPHS):
             place_terms(b, 1, slice(0, BANK))
+        copy_side(0, 0)
+        copy_side(1, 0)
         regroup(8)
         quantise_piece(7)
-        product(1, 1, 0)
         product(1, 1, 1)
         regroup(9)
-        quantise_piece(8)
-        split_product(1, 1, 0)
-        split_product(1, 1, 1)
+        split_products(1, 1)
         for b in range(EARLY_GRAPHS):
             place_terms(b, 1, slice(BANK, WIDTH))
         for b in range(EARLY_GRAPHS, SLOTS):
             for w in range(2):
                 place_terms(b, w, slice(0, WIDTH))
-        side_product(0, 1)
-        side_product(1, 1)
         form_pre(0, 0)
         form_pre(1, 0)
+        side_product(0, 1)
+        side_product(1, 1)
+        quantise_piece(8)
         regroup(10)
         quantise_piece(9)
-        regroup(11)
         activate(0, 0)
-        form_pre(2, 0)
-        quantise_piece(10)
+        regroup(11)
         activate(1, 0)
-        form_pre(3, 0)
-        copy_side(0, 1)
-        copy_side(1, 1)
-        activate(2, 0)
-        dist_ps = []
-        for v in range(0, SIDE_GRAPHS, 2):
-            n = min(2, SIDE_GRAPHS - v)
-            dist_ps.append(psum_acc.tile([P, n, PAIRS], F32, tag="acc", name="dist_ps"))
-            nc.tensor.matmul(
-                out=dist_ps[-1][:].rearrange("p v q -> p (v q)"),
-                lhsT=dist_ones[:].to_broadcast([P, P]),
-                rhs=spread[:, TENSOR_GRAPHS + v : TENSOR_GRAPHS + v + n, :].rearrange("p v q -> p (v q)"),
-                start=True,
-                stop=True,
-            )
-        activate(3, 0)
-        quantise_piece(11)
-        for k, d in enumerate(dist_ps):
-            nc.scalar.copy(out=dist_all[:, 2 * k : min(2 * k + 2, SIDE_GRAPHS), :], in_=d[:])
-        for v in range(SIDE_GRAPHS):
-            for f in range(F_TILES):
-                side_sums(v, f)
         form_pre(0, 1)
         form_pre(LEAD, 0)
+        quantise_piece(10)
+        copy_side(0, 1)
+        copy_side(1, 1)
+        quantise_piece(11)
 
         for u in range(UNITS + 2):
             if u < UNITS:
@@ -494,8 +473,25 @@ def tile_graphmessagelayer_pa_kernel(tc, node_state, positions, We1, be1, We2, b
             if h == HALVES - 1 and k < GRAPHS and order[k] + SLOTS < TENSOR_GRAPHS:
                 for w in range(2):
                     place_terms(order[k] + SLOTS, w, slice(0, WIDTH))
+            if u == 1:
+                dist_ps = []
+                for v in range(0, SIDE_GRAPHS, 2):
+                    n = min(2, SIDE_GRAPHS - v)
+                    dist_ps.append(psum_acc.tile([P, n, PAIRS], F32, tag="acc", name="dist_ps"))
+                    nc.tensor.matmul(
+                        out=dist_ps[-1][:].rearrange("p v q -> p (v q)"),
+                        lhsT=dist_ones[:].to_broadcast([P, P]),
+                        rhs=spread[:, TENSOR_GRAPHS + v : TENSOR_GRAPHS + v + n, :].rearrange("p v q -> p (v q)"),
+                        start=True,
+                        stop=True,
+                    )
+                for k, d in enumerate(dist_ps):
+                    nc.scalar.copy(out=dist_all[:, 2 * k : min(2 * k + 2, SIDE_GRAPHS), :], in_=d[:])
             if 1 <= u <= UNITS:
                 quantise(u - 1)
+            for n in range(SIDE_RATE * (u - 1), SIDE_RATE * u):
+                if 0 <= n < SIDE_GRAPHS * F_TILES:
+                    side_sums(*divmod(n, F_TILES))
             if u >= 2:
                 multiply(u - 2)
             if u + 1 < UNITS:

@@ -101,6 +101,7 @@ def tile_graphmessagelayer_pa_kernel(tc, node_state, positions, We1, be1, We2, b
         pre = {}
         h_grouped = {}
         h_words = {}
+        msgs = {}
 
         def load_weight(w, g, columns=slice(0, WIDTH)):
             if (w, g) not in raw:
@@ -241,29 +242,28 @@ def tile_graphmessagelayer_pa_kernel(tc, node_state, positions, We1, be1, We2, b
             )
             h_words[u] = (h_codes, h_scales)
 
-        def multiply(u):
+        def multiply(u, m):
             h_codes, h_scales = h_words[u]
-            msg = store_pool.tile([P, WIDTH], F32)
-            for m in range(SIDES):
-                acc = psum_acc.tile([P, BANK], F32, tag="acc")
-                for g in range(PASSES):
-                    nc.tensor.matmul_mx(
-                        out=acc[:],
-                        lhsT=h_codes[:, g, :].bitcast(FP8X4),
-                        lhsT_scale=h_scales[:, g, :],
-                        rhs=w_codes[:, 2, g, m * BANK : (m + 1) * BANK].bitcast(FP8X4),
-                        rhs_scale=w_scales[:, 2, g, m * BANK : (m + 1) * BANK],
-                        start=(g == 0),
-                        stop=(g == PASSES - 1),
-                    )
-                nc.vector.tensor_tensor(
-                    out=msg[:, m * BANK : (m + 1) * BANK],
-                    in0=acc[:],
-                    in1=be2_all[:, m * BANK : (m + 1) * BANK],
-                    op=ALU.add,
+            if m == 0:
+                msgs[u] = store_pool.tile([P, WIDTH], F32, tag="msg", name="msg")
+            columns = slice(m * BANK, (m + 1) * BANK)
+            acc = psum_acc.tile([P, BANK], F32, tag="acc")
+            for g in range(PASSES):
+                nc.tensor.matmul_mx(
+                    out=acc[:],
+                    lhsT=h_codes[:, g, :].bitcast(FP8X4),
+                    lhsT_scale=h_scales[:, g, :],
+                    rhs=w_codes[:, 2, g, columns].bitcast(FP8X4),
+                    rhs_scale=w_scales[:, 2, g, columns],
+                    start=(g == 0),
+                    stop=(g == PASSES - 1),
                 )
+            nc.vector.tensor_tensor(out=msgs[u][:, columns], in0=acc[:], in1=be2_all[:, columns], op=ALU.add)
             r0 = order[u // HALVES] * PAIRS + u % HALVES * P
-            nc.sync.dma_start(out=out_rows[r0 : r0 + P, :], in_=msg[:])
+            if u == UNITS - 1:
+                nc.sync.dma_start(out=out_rows[r0 : r0 + P, columns], in_=msgs[u][:, columns])
+            elif m == SIDES - 1:
+                nc.sync.dma_start(out=out_rows[r0 : r0 + P, :], in_=msgs[u][:])
 
         warm = keep.tile([P, 2], F32)
         nc.vector.memset(warm[:], 1.0)
@@ -348,6 +348,7 @@ def tile_graphmessagelayer_pa_kernel(tc, node_state, positions, We1, be1, We2, b
             nc.tensor.matmul(out=rel[:, h, :], lhsT=sel[:, h, :], rhs=pos_nodes[:], start=True, stop=True)
         rel_sq = keep.tile([P, HALVES, POS_COLUMNS], F32)
         nc.scalar.activation(out=rel_sq[:], in_=rel[:], func=ACT.Square)
+        regroup(0)
         sq = keep.tile([P, HALVES, GRAPHS], F32)
         nc.vector.tensor_reduce(
             out=sq[:],
@@ -360,7 +361,6 @@ def tile_graphmessagelayer_pa_kernel(tc, node_state, positions, We1, be1, We2, b
         root = keep.tile([P, HALVES, GRAPHS], F32)
         nc.scalar.activation(out=root[:], in_=sq_floor[:], func=ACT.Sqrt)
 
-        regroup(0)
         dist = keep.tile([P, HALVES, GRAPHS], F32)
         nc.vector.scalar_tensor_tensor(
             out=dist[:].rearrange("p h b -> p (h b)"),
@@ -413,7 +413,6 @@ def tile_graphmessagelayer_pa_kernel(tc, node_state, positions, We1, be1, We2, b
                 out=spread[DIST + k : DIST + k + 1, :, :].rearrange("o b q -> o (b q)"), in_=dist_rows[rows, :]
             )
         nc.sync.dma_start(out=be2_all[:], in_=be2.partition_broadcast(P))
-        nc.scalar.activation(out=warm[:, 1:2], in_=warm[:, 0:1], func=ACT.Silu)
         regroup(4)
         quantise_piece(3)
         product(1, 0, 1)
@@ -432,6 +431,7 @@ def tile_graphmessagelayer_pa_kernel(tc, node_state, positions, We1, be1, We2, b
         regroup(7)
         quantise_piece(6)
         product(1, 1, 0)
+        nc.scalar.activation(out=warm[:, 1:2], in_=warm[:, 0:1], func=ACT.Silu)
         split_products(0, 1)
         for b in range(EARLY_GRAPHS):
             place_terms(b, 1, slice(0, BANK))
@@ -493,8 +493,10 @@ def tile_graphmessagelayer_pa_kernel(tc, node_state, positions, We1, be1, We2, b
                 if 0 <= n < SIDE_GRAPHS * F_TILES:
                     side_sums(*divmod(n, F_TILES))
             if u >= 2:
-                multiply(u - 2)
+                multiply(u - 2, 0)
             if u + 1 < UNITS:
                 form_pre(u + 1, 1)
+            if u >= 2:
+                multiply(u - 2, 1)
             if u + LEAD + 1 < UNITS:
                 form_pre(u + LEAD + 1, 0)

@@ -31,11 +31,13 @@ HALF = NODES // HALVES
 POS_COLUMNS = 64
 TINY = 1e-30
 
+ROW_STEP = P // NODES
 HI = 0
-LO = 32
-ONE = 64
-DIST = 65
+LO = 4
+ONE = 1
+DIST = 3
 DIST_PARTS = 3
+DIST_END = DIST + 2 * DIST_PARTS
 
 SIDE_GRAPHS = 3
 TENSOR_GRAPHS = GRAPHS - SIDE_GRAPHS
@@ -156,11 +158,11 @@ def tile_graphmessagelayer_pa_kernel(tc, node_state, positions, We1, be1, We2, b
             )
 
         def place_terms(b, w, columns):
-            a, n0 = divmod(b * NODES, P)
+            a, place = divmod(b, TILE_GRAPHS)
             for s in range(2):
-                row = (2 * s + w) * NODES
+                row = (LO if s else HI) + 2 * w
                 nc.sync.dma_start(
-                    out=terms[row : row + NODES, b % SLOTS, columns], in_=parts[n0 : n0 + NODES, a, w, s, columns]
+                    out=terms[row:P:ROW_STEP, b % SLOTS, columns], in_=parts[place:P:TILE_GRAPHS, a, w, s, columns]
                 )
 
         def side_product(c, w):
@@ -179,8 +181,10 @@ def tile_graphmessagelayer_pa_kernel(tc, node_state, positions, We1, be1, We2, b
                     )
 
         def copy_side(c, w):
+            by_graph = side_ps[c, w][:].rearrange("p e (n b) -> p e b n", b=TILE_GRAPHS)
             nc.scalar.copy(
-                out=a_side[:, w, c * PIECE_F : (c + 1) * PIECE_F, :], in_=side_ps[c, w][:, :, P - SIDE_GRAPHS * NODES : P]
+                out=a_side[:, w, c * PIECE_F : (c + 1) * PIECE_F, :].rearrange("p e (v n) -> p e v n", n=NODES),
+                in_=by_graph[:, :, TILE_GRAPHS - SIDE_GRAPHS : TILE_GRAPHS, :],
             )
 
         def form_pre(u, c):
@@ -271,7 +275,7 @@ def tile_graphmessagelayer_pa_kernel(tc, node_state, positions, We1, be1, We2, b
         nc.vector.memset(vec_rows[:], 0.0)
         dist_columns = keep.tile([P, P], BF16)
         nc.vector.memset(dist_columns[:], 0.0)
-        nc.vector.memset(terms[ONE:P, :, :].rearrange("p s f -> p (s f)").bitcast(I32), 0)
+        nc.vector.memset(terms[:].rearrange("p s f -> p (s f)").bitcast(I32), 0)
         nc.scalar.dma_start(out=vec_rows[0:F_TILES, :], in_=be1.rearrange("(r c) -> r c", c=P))
         nc.scalar.dma_start(
             out=vec_rows[F_TILES : 2 * F_TILES, :],
@@ -298,7 +302,7 @@ def tile_graphmessagelayer_pa_kernel(tc, node_state, positions, We1, be1, We2, b
             in_=be1.partition_broadcast(1).unsqueeze(1).to_broadcast([1, SLOTS, WIDTH]),
         )
         nc.sync.dma_start(
-            out=terms[DIST : DIST + DIST_PARTS, :, :],
+            out=terms[DIST:DIST_END:2, :, :],
             in_=We1[2 * WIDTH : 2 * WIDTH + 1, :]
             .rearrange("o f -> (o f)")
             .partition_broadcast(DIST_PARTS)
@@ -315,29 +319,38 @@ def tile_graphmessagelayer_pa_kernel(tc, node_state, positions, We1, be1, We2, b
                 in1=ident_bf[:, 0:NODES].unsqueeze(1).to_broadcast([P, HALF, NODES]),
                 op=ALU.subtract,
             )
-        pick = keep.tile([P, 2 * NODES], BF16)
+        pick = keep.tile([P, 2, NODES], BF16)
+        for w in range(2):
+            nc.gpsimd.tensor_tensor(
+                out=pick[:, w, :],
+                in0=ident_bf[:, HI + 2 * w : P : ROW_STEP],
+                in1=ident_bf[:, LO + 2 * w : P : ROW_STEP],
+                op=ALU.add,
+            )
         nc.gpsimd.tensor_tensor(
-            out=pick[:], in0=ident_bf[:, HI : HI + 2 * NODES], in1=ident_bf[:, LO : LO + 2 * NODES], op=ALU.add
-        )
-        nc.gpsimd.tensor_tensor(
-            out=pick[:, 0:NODES],
-            in0=pick[:, 0:NODES],
+            out=pick[:, 0, :],
+            in0=pick[:, 0, :],
             in1=ident_bf[:, ONE : ONE + 1].to_broadcast([P, NODES]),
             op=ALU.add,
         )
         pick_pairs = keep.tile([P, NODES, NODES], BF16)
         nc.gpsimd.tensor_tensor(
             out=pick_pairs[:],
-            in0=pick[:, 0:NODES].unsqueeze(2).to_broadcast([P, NODES, NODES]),
-            in1=pick[:, NODES : 2 * NODES].unsqueeze(1).to_broadcast([P, NODES, NODES]),
+            in0=pick[:, 0, :].unsqueeze(2).to_broadcast([P, NODES, NODES]),
+            in1=pick[:, 1, :].unsqueeze(1).to_broadcast([P, NODES, NODES]),
             op=ALU.add,
         )
         dist_ones = keep.tile([P, 1], BF16)
         nc.gpsimd.tensor_tensor(
-            out=dist_ones[:], in0=ident_bf[:, DIST : DIST + 1], in1=ident_bf[:, DIST + 1 : DIST + 2], op=ALU.add
+            out=dist_ones[:], in0=ident_bf[:, DIST : DIST + 1], in1=ident_bf[:, DIST + 2 : DIST + 3], op=ALU.add
         )
         nc.gpsimd.tensor_tensor(
-            out=dist_ones[:], in0=dist_ones[:], in1=ident_bf[:, DIST + 2 : DIST + 3], op=ALU.add
+            out=dist_ones[:], in0=dist_ones[:], in1=ident_bf[:, DIST + 4 : DIST + 5], op=ALU.add
+        )
+        by_node = keep.tile([P, P], BF16)
+        nc.vector.tensor_copy(
+            out=by_node[:].rearrange("p (n b) -> p n b", b=TILE_GRAPHS),
+            in_=ident_bf[:].rearrange("p (b n) -> p n b", n=NODES),
         )
         nc.vector.tensor_copy(
             out=spread[:],
@@ -379,7 +392,7 @@ def tile_graphmessagelayer_pa_kernel(tc, node_state, positions, We1, be1, We2, b
                 x_t = psum_pre.tile([P, PACK, P], BF16, tag="pre")
                 for t in range(PACK):
                     columns = slice(g * K_PASS + t, (g + 1) * K_PASS, PACK)
-                    nc.tensor.transpose(x_t[:, t, :], x_rows[:, a, columns], ident_bf[:])
+                    nc.tensor.transpose(x_t[:, t, :], x_rows[:, a, columns], by_node[:])
                 nc.scalar.copy(out=x_grouped[:, g, a * P : (a + 1) * P, :], in_=x_t[:].rearrange("p t r -> p r t"))
         vec_t = psum_acc.tile([P, P], BF16, tag="acc")
         nc.tensor.transpose(vec_t[:], vec_rows[:], ident_bf[:])
@@ -410,7 +423,7 @@ def tile_graphmessagelayer_pa_kernel(tc, node_state, positions, We1, be1, We2, b
         for k in range(DIST_PARTS):
             rows = slice(k * HALVES * GRAPHS, (k + 1) * HALVES * GRAPHS)
             nc.sync.dma_start(
-                out=spread[DIST + k : DIST + k + 1, :, :].rearrange("o b q -> o (b q)"), in_=dist_rows[rows, :]
+                out=spread[DIST + 2 * k : DIST + 2 * k + 1, :, :].rearrange("o b q -> o (b q)"), in_=dist_rows[rows, :]
             )
         nc.sync.dma_start(out=be2_all[:], in_=be2.partition_broadcast(P))
         regroup(4)

@@ -39,7 +39,7 @@ DIST = 3
 DIST_PARTS = 3
 DIST_END = DIST + 2 * DIST_PARTS
 
-SIDE_GRAPHS = 3
+SIDE_GRAPHS = 2
 TENSOR_GRAPHS = GRAPHS - SIDE_GRAPHS
 SIDE_EVERY = 4
 UNITS = GRAPHS * HALVES
@@ -50,6 +50,7 @@ PIECE_F = BANK // P
 RUN = 4
 VECTOR_COLUMNS = 320
 SIDE_RATE = 1
+SIDE_NODES = 8
 LEAD = 2
 EARLY_GRAPHS = (LEAD + HALVES) // HALVES
 SLOTS = 5
@@ -103,7 +104,6 @@ def tile_graphmessagelayer_pa_kernel(tc, node_state, positions, We1, be1, We2, b
         pre = {}
         h_grouped = {}
         h_words = {}
-        msgs = {}
 
         def load_weight(w, g, columns=slice(0, WIDTH)):
             if (w, g) not in raw:
@@ -212,18 +212,18 @@ def tile_graphmessagelayer_pa_kernel(tc, node_state, positions, We1, be1, We2, b
                 scale=vecs[:, 1, f : f + 1],
                 bias=vecs[:, 0, f : f + 1],
             )
-            nc.gpsimd.tensor_tensor(
-                out=by_pair,
-                in0=by_pair,
-                in1=a_side[:, 0, f, nodes].unsqueeze(2).to_broadcast([P, NODES, NODES]),
-                op=ALU.add,
-            )
-            nc.gpsimd.tensor_tensor(
-                out=by_pair,
-                in0=by_pair,
-                in1=a_side[:, 1, f, nodes].unsqueeze(1).to_broadcast([P, NODES, NODES]),
-                op=ALU.add,
-            )
+            for i0 in range(0, NODES, SIDE_NODES):
+                piece = by_pair[:, i0 : i0 + SIDE_NODES, :]
+                shape = [P, SIDE_NODES, NODES]
+                nc.gpsimd.tensor_tensor(
+                    out=piece,
+                    in0=piece,
+                    in1=a_side[:, 0, f, v * NODES + i0 : v * NODES + i0 + SIDE_NODES].unsqueeze(2).to_broadcast(shape),
+                    op=ALU.add,
+                )
+                nc.gpsimd.tensor_tensor(
+                    out=piece, in0=piece, in1=a_side[:, 1, f, nodes].unsqueeze(1).to_broadcast(shape), op=ALU.add
+                )
 
         def activate(u, c):
             if c == 0:
@@ -246,28 +246,34 @@ def tile_graphmessagelayer_pa_kernel(tc, node_state, positions, We1, be1, We2, b
             )
             h_words[u] = (h_codes, h_scales)
 
-        def multiply(u, m):
+        def multiply(u):
             h_codes, h_scales = h_words[u]
-            if m == 0:
-                msgs[u] = store_pool.tile([P, WIDTH], F32, tag="msg", name="msg")
-            columns = slice(m * BANK, (m + 1) * BANK)
-            acc = psum_acc.tile([P, BANK], F32, tag="acc")
-            for g in range(PASSES):
-                nc.tensor.matmul_mx(
-                    out=acc[:],
-                    lhsT=h_codes[:, g, :].bitcast(FP8X4),
-                    lhsT_scale=h_scales[:, g, :],
-                    rhs=w_codes[:, 2, g, columns].bitcast(FP8X4),
-                    rhs_scale=w_scales[:, 2, g, columns],
-                    start=(g == 0),
-                    stop=(g == PASSES - 1),
-                )
-            nc.vector.tensor_tensor(out=msgs[u][:, columns], in0=acc[:], in1=be2_all[:, columns], op=ALU.add)
+            msg = store_pool.tile([P, WIDTH], F32)
             r0 = order[u // HALVES] * PAIRS + u % HALVES * P
-            if u == UNITS - 1:
-                nc.sync.dma_start(out=out_rows[r0 : r0 + P, columns], in_=msgs[u][:, columns])
-            elif m == SIDES - 1:
-                nc.sync.dma_start(out=out_rows[r0 : r0 + P, :], in_=msgs[u][:])
+            unit_rows = out_rows[r0 : r0 + P, :]
+            for m in range(SIDES):
+                columns = slice(m * BANK, (m + 1) * BANK)
+                acc = psum_acc.tile([P, BANK], F32, tag="acc")
+                for g in range(PASSES):
+                    nc.tensor.matmul_mx(
+                        out=acc[:],
+                        lhsT=h_codes[:, g, :].bitcast(FP8X4),
+                        lhsT_scale=h_scales[:, g, :],
+                        rhs=w_codes[:, 2, g, m * BANK : (m + 1) * BANK].bitcast(FP8X4),
+                        rhs_scale=w_scales[:, 2, g, m * BANK : (m + 1) * BANK],
+                        start=(g == 0),
+                        stop=(g == PASSES - 1),
+                    )
+                nc.vector.tensor_tensor(
+                    out=msg[:, m * BANK : (m + 1) * BANK],
+                    in0=acc[:],
+                    in1=be2_all[:, m * BANK : (m + 1) * BANK],
+                    op=ALU.add,
+                )
+                if u == UNITS - 1:
+                    nc.sync.dma_start(out=unit_rows[:, columns], in_=msg[:, columns])
+            if u < UNITS - 1:
+                nc.sync.dma_start(out=unit_rows, in_=msg[:])
 
         warm = keep.tile([P, 2], F32)
         nc.vector.memset(warm[:], 1.0)
@@ -282,16 +288,17 @@ def tile_graphmessagelayer_pa_kernel(tc, node_state, positions, We1, be1, We2, b
             in_=We1[2 * WIDTH : 2 * WIDTH + 1, :].rearrange("o (r c) -> (o r) c", c=P),
         )
         nc.scalar.activation(out=warm[:, 1:2], in_=warm[:, 0:1], func=ACT.Sqrt)
-        load_weight(0, 0, slice(0, BANK))
+        load_weight(0, 0, slice(0, VECTOR_COLUMNS))
+        load_weight(0, 0, slice(VECTOR_COLUMNS, BANK))
         with nc.allow_non_contiguous_dma(reason="768 values in runs of 3, once"):
             nc.sync.dma_start(
                 out=pos_nodes[0:NODES, 0 : GRAPHS * COORDS].rearrange("n (b c) -> n b c", c=COORDS),
                 in_=positions.rearrange("b n c -> n b c"),
             )
+        load_weight(0, 0, slice(BANK, WIDTH))
         nc.sync.dma_start(
             out=x_rows[:], in_=node_state.rearrange("b n h -> (b n) h").rearrange("(a p) h -> p a h", p=P)
         )
-        load_weight(0, 0, slice(BANK, WIDTH))
         load_weight(0, 1)
         load_weight(1, 0)
         load_weight(1, 1)
@@ -311,14 +318,6 @@ def tile_graphmessagelayer_pa_kernel(tc, node_state, positions, We1, be1, We2, b
         )
         make_identity(nc, ident_bf[:])
 
-        sel = keep.tile([P, HALVES, P], BF16)
-        for h in range(HALVES):
-            nc.gpsimd.tensor_tensor(
-                out=sel[:, h, :].rearrange("p (i j) -> p i j", j=NODES),
-                in0=ident_bf[:, h * HALF : (h + 1) * HALF].unsqueeze(2).to_broadcast([P, HALF, NODES]),
-                in1=ident_bf[:, 0:NODES].unsqueeze(1).to_broadcast([P, HALF, NODES]),
-                op=ALU.subtract,
-            )
         pick = keep.tile([P, 2, NODES], BF16)
         for w in range(2):
             nc.gpsimd.tensor_tensor(
@@ -340,6 +339,14 @@ def tile_graphmessagelayer_pa_kernel(tc, node_state, positions, We1, be1, We2, b
             in1=pick[:, 1, :].unsqueeze(1).to_broadcast([P, NODES, NODES]),
             op=ALU.add,
         )
+        sel = keep.tile([P, HALVES, P], BF16)
+        for h in range(HALVES):
+            nc.gpsimd.tensor_tensor(
+                out=sel[:, h, :].rearrange("p (i j) -> p i j", j=NODES),
+                in0=ident_bf[:, h * HALF : (h + 1) * HALF].unsqueeze(2).to_broadcast([P, HALF, NODES]),
+                in1=ident_bf[:, 0:NODES].unsqueeze(1).to_broadcast([P, HALF, NODES]),
+                op=ALU.subtract,
+            )
         dist_ones = keep.tile([P, 1], BF16)
         nc.gpsimd.tensor_tensor(
             out=dist_ones[:], in0=ident_bf[:, DIST : DIST + 1], in1=ident_bf[:, DIST + 2 : DIST + 3], op=ALU.add
@@ -387,13 +394,6 @@ def tile_graphmessagelayer_pa_kernel(tc, node_state, positions, We1, be1, We2, b
             dist_columns[:, k * HALVES * GRAPHS : (k + 1) * HALVES * GRAPHS].rearrange("p (b h) -> p h b", h=HALVES)
             for k in range(DIST_PARTS)
         ]
-        for a in range(NODE_TILES):
-            for g in range(PASSES):
-                x_t = psum_pre.tile([P, PACK, P], BF16, tag="pre")
-                for t in range(PACK):
-                    columns = slice(g * K_PASS + t, (g + 1) * K_PASS, PACK)
-                    nc.tensor.transpose(x_t[:, t, :], x_rows[:, a, columns], by_node[:])
-                nc.scalar.copy(out=x_grouped[:, g, a * P : (a + 1) * P, :], in_=x_t[:].rearrange("p t r -> p r t"))
         vec_t = psum_acc.tile([P, P], BF16, tag="acc")
         nc.tensor.transpose(vec_t[:], vec_rows[:], ident_bf[:])
         rest = keep.tile([P, HALVES, GRAPHS], F32)
@@ -401,17 +401,24 @@ def tile_graphmessagelayer_pa_kernel(tc, node_state, positions, We1, be1, We2, b
         regroup(1)
         nc.vector.tensor_tensor(out=rest[:], in0=dist[:], in1=part[0], op=ALU.subtract)
         quantise_piece(0)
+        for a in range(NODE_TILES):
+            for g in range(PASSES):
+                x_t = psum_pre.tile([P, PACK, P], BF16, tag="pre")
+                for t in range(PACK):
+                    columns = slice(g * K_PASS + t, (g + 1) * K_PASS, PACK)
+                    nc.tensor.transpose(x_t[:, t, :], x_rows[:, a, columns], by_node[:])
+                nc.scalar.copy(out=x_grouped[:, g, a * P : (a + 1) * P, :], in_=x_t[:].rearrange("p t r -> p r t"))
         nc.vector.tensor_copy(out=part[1], in_=rest[:])
+        quantise_piece(1)
+        nc.vector.tensor_tensor(out=part[2], in0=rest[:], in1=part[1], op=ALU.subtract)
+        dist_rows_ps = psum_acc.tile([P, P], BF16, tag="acc")
+        nc.tensor.transpose(dist_rows_ps[:], dist_columns[:], ident_bf[:])
+        regroup(2)
         nc.vector.quantize_mx(
             out=x_codes[:].rearrange("p g r -> p (g r)").bitcast(FP8X4),
             scales=x_scales[:].rearrange("p g r -> p (g r)"),
             in_=x_grouped[:].rearrange("p g r t -> p (g r t)"),
         )
-        nc.vector.tensor_tensor(out=part[2], in0=rest[:], in1=part[1], op=ALU.subtract)
-        dist_rows_ps = psum_acc.tile([P, P], BF16, tag="acc")
-        nc.tensor.transpose(dist_rows_ps[:], dist_columns[:], ident_bf[:])
-        regroup(2)
-        quantise_piece(1)
         nc.vector.tensor_copy(out=vecs[:].rearrange("p v f -> p (v f)"), in_=vec_t[:, 0 : 2 * F_TILES])
         product(0, 0, 0)
         product(1, 0, 0)
@@ -506,10 +513,8 @@ def tile_graphmessagelayer_pa_kernel(tc, node_state, positions, We1, be1, We2, b
                 if 0 <= n < SIDE_GRAPHS * F_TILES:
                     side_sums(*divmod(n, F_TILES))
             if u >= 2:
-                multiply(u - 2, 0)
+                multiply(u - 2)
             if u + 1 < UNITS:
                 form_pre(u + 1, 1)
-            if u >= 2:
-                multiply(u - 2, 1)
             if u + LEAD + 1 < UNITS:
                 form_pre(u + LEAD + 1, 0)

from contextlib import ExitStack

import concourse.mybir as mybir
from concourse.masks import make_identity

F32 = mybir.dt.float32
BF16 = mybir.dt.bfloat16
I32 = mybir.dt.int32
U32 = mybir.dt.uint32
U8 = mybir.dt.uint8
FP8X4 = mybir.dt.float8_e4m3fn_x4
ALU = mybir.AluOpType
ACT = mybir.ActivationFunctionType

P = 128
PACK = 4
K_PASS = P * PACK
BANK = 512
GRAPHS = 16
NODES = 16
COORDS = 3
WIDTH = 1024
PASSES = WIDTH // K_PASS
F_TILES = WIDTH // P
ALL_NODES = GRAPHS * NODES
NODE_TILES = ALL_NODES // P
TILE_GRAPHS = P // NODES
PAIRS = NODES * NODES
HALVES = PAIRS // P
HALF = NODES // HALVES
POS_COLUMNS = 64
TINY = 1e-30

ROW_STEP = P // NODES
HI = 0
LO = 4
ONE = 1
DIST = 3
DIST_PARTS = 3
DIST_END = DIST + 2 * DIST_PARTS

SIDE_GRAPHS = 2
TENSOR_GRAPHS = GRAPHS - SIDE_GRAPHS
SIDE_EVERY = 4
UNITS = GRAPHS * HALVES


SIDES = WIDTH // BANK
PIECE_F = BANK // P
RUN = 4
VECTOR_COLUMNS = 320
SIDE_RATE = 1
SIDE_NODES = 8
LEAD = 2
EARLY_GRAPHS = (LEAD + HALVES) // HALVES
SLOTS = 5

FLOPS = 2 * ALL_NODES * WIDTH * 2 * WIDTH + 2 * GRAPHS * PAIRS * WIDTH * WIDTH


def tile_graphmessagelayer_pa_kernel(tc, node_state, positions, We1, be1, We2, be2, out):
    nc = tc.nc
    out_rows = out.rearrange("b i j m -> (b i j) m")
    weight_rows = [We1[0:WIDTH, :], We1[WIDTH : 2 * WIDTH, :], We2]
    pieces = [(0, g, c) for g in range(PASSES) for c in range(SIDES)]
    pieces += [(w, g, c) for w in (1, 2) for c in range(SIDES) for g in range(PASSES)]
    side_places = [GRAPHS - 1 - SIDE_EVERY * v for v in reversed(range(SIDE_GRAPHS))]
    order = list(range(TENSOR_GRAPHS))
    for v, place in enumerate(side_places):
        order.insert(place, TENSOR_GRAPHS + v)

    with ExitStack() as ctx:
        keep = ctx.enter_context(tc.tile_pool(name="keep", bufs=1))
        raw_pool = ctx.enter_context(tc.tile_pool(name="raw", bufs=6))
        grouped_pool = ctx.enter_context(tc.tile_pool(name="grouped", bufs=3))
        unit_pool = ctx.enter_context(tc.tile_pool(name="unit", bufs=LEAD + 4))
        work = ctx.enter_context(tc.tile_pool(name="work", bufs=4))
        store_pool = ctx.enter_context(tc.tile_pool(name="store", bufs=6))
        psum_pre = ctx.enter_context(tc.psum_pool(name="psum_pre", bufs=4))
        psum_acc = ctx.enter_context(tc.psum_pool(name="psum_acc", bufs=4))
        ctx.enter_context(tc.manual_schedule())

        vec_rows = keep.tile([P, P], BF16)
        pos_nodes = keep.tile([P, POS_COLUMNS], BF16)
        parts = keep.tile([P, NODE_TILES, 2, 2, WIDTH], BF16)
        terms = keep.tile([P, SLOTS, WIDTH], BF16)
        spread = keep.tile([P, GRAPHS, PAIRS], BF16)
        x_rows = keep.tile([P, NODE_TILES, WIDTH], BF16)
        ident_bf = keep.tile([P, P], BF16)
        x_grouped = keep.tile([P, PASSES, ALL_NODES, PACK], BF16, align_bytes=64)
        x_codes = keep.tile([P, PASSES, ALL_NODES], U32, align_bytes=64)
        x_scales = keep.tile([P, PASSES, ALL_NODES], U8, align_bytes=64)
        vecs = keep.tile([P, 2, F_TILES], F32)
        w_codes = keep.tile([P, 3, PASSES, WIDTH], U32, align_bytes=64)
        w_scales = keep.tile([P, 3, PASSES, WIDTH], U8, align_bytes=64)
        a_side = keep.tile([P, 2, F_TILES, SIDE_GRAPHS * NODES], F32)
        dist_all = keep.tile([P, SIDE_GRAPHS, PAIRS], F32)
        sums = keep.tile([P, SIDE_GRAPHS, F_TILES, PAIRS], F32)
        be2_all = keep.tile([P, WIDTH], BF16)
        raw = {}
        grouped = {}
        a_ps = {}
        side_ps = {}
        pre = {}
        h_grouped = {}
        h_words = {}

        def load_weight(w, g, columns=slice(0, WIDTH)):
            if (w, g) not in raw:
                raw[w, g] = raw_pool.tile([P, PACK, WIDTH], BF16, tag="raw", name="raw")
            words = "(p t) n -> p t n" if w < 2 else "(t p) n -> p t n"
            source = weight_rows[w][g * K_PASS : (g + 1) * K_PASS, :].rearrange(words, p=P)
            nc.sync.dma_start(out=raw[w, g][:, :, columns], in_=source[:, :, columns])

        def regroup_columns(k, engine_copy, columns):
            w, g, c = pieces[k]
            engine_copy(
                out=grouped[k][:, columns, :].rearrange("p (c i) t -> p c t i", i=RUN),
                in_=raw[w, g][:, :, c * BANK : (c + 1) * BANK][:, :, columns].rearrange("p t (c i) -> p c t i", i=RUN),
            )

        def regroup(k):
            grouped[k] = grouped_pool.tile([P, BANK, PACK], BF16, align_bytes=64, tag="grouped", name="grouped")
            regroup_columns(k, nc.vector.tensor_copy, slice(0, VECTOR_COLUMNS))
            regroup_columns(k, nc.scalar.copy, slice(VECTOR_COLUMNS, BANK))

        def quantise_piece(k):
            w, g, c = pieces[k]
            nc.vector.quantize_mx(
                out=w_codes[:, w, g, c * BANK : (c + 1) * BANK].bitcast(FP8X4),
                scales=w_scales[:, w, g, c * BANK : (c + 1) * BANK],
                in_=grouped[k][:].rearrange("p n t -> p (n t)"),
            )

        def product(c, w, g):
            for a in range(NODE_TILES):
                if g == 0:
                    a_ps[c, w, a] = psum_pre.tile([P, BANK], F32, tag="pre", name="a_ps")
                nc.tensor.matmul_mx(
                    out=a_ps[c, w, a][:],
                    lhsT=x_codes[:, g, a * P : (a + 1) * P].bitcast(FP8X4),
                    lhsT_scale=x_scales[:, g, a * P : (a + 1) * P],
                    rhs=w_codes[:, w, g, c * BANK : (c + 1) * BANK].bitcast(FP8X4),
                    rhs_scale=w_scales[:, w, g, c * BANK : (c + 1) * BANK],
                    start=(g == 0),
                    stop=(g == PASSES - 1),
                )

        def split_products(c, w):
            for a in range(NODE_TILES):
                split_product(c, w, a)

        def split_product(c, w, a):
            columns = slice(c * BANK, (c + 1) * BANK)
            nc.scalar.copy(out=parts[:, a, w, 0, columns], in_=a_ps[c, w, a][:])
            nc.vector.tensor_tensor(
                out=parts[:, a, w, 1, columns], in0=a_ps[c, w, a][:], in1=parts[:, a, w, 0, columns], op=ALU.subtract
            )

        def place_terms(b, w, columns):
            a, place = divmod(b, TILE_GRAPHS)
            for s in range(2):
                row = (LO if s else HI) + 2 * w
                nc.sync.dma_start(
                    out=terms[row:P:ROW_STEP, b % SLOTS, columns], in_=parts[place:P:TILE_GRAPHS, a, w, s, columns]
                )

        def side_product(c, w):
            side_ps[c, w] = psum_acc.tile([P, PIECE_F, P], F32, tag="acc", name="side_ps")
            for e in range(PIECE_F):
                f0 = c * BANK + e * P
                for g in range(PASSES):
                    nc.tensor.matmul_mx(
                        out=side_ps[c, w][:, e, :],
                        lhsT=w_codes[:, w, g, f0 : f0 + P].bitcast(FP8X4),
                        lhsT_scale=w_scales[:, w, g, f0 : f0 + P],
                        rhs=x_codes[:, g, ALL_NODES - P : ALL_NODES].bitcast(FP8X4),
                        rhs_scale=x_scales[:, g, ALL_NODES - P : ALL_NODES],
                        start=(g == 0),
                        stop=(g == PASSES - 1),
                    )

        def copy_side(c, w):
            by_graph = side_ps[c, w][:].rearrange("p e (n b) -> p e b n", b=TILE_GRAPHS)
            nc.scalar.copy(
                out=a_side[:, w, c * PIECE_F : (c + 1) * PIECE_F, :].rearrange("p e (v n) -> p e v n", n=NODES),
                in_=by_graph[:, :, TILE_GRAPHS - SIDE_GRAPHS : TILE_GRAPHS, :],
            )

        def form_pre(u, c):
            b, h = order[u // HALVES], u % HALVES
            if b >= TENSOR_GRAPHS:
                return
            pre[u, c] = psum_pre.tile([P, PACK, P], F32, tag="pre", name="pre_ps")
            for t in range(PACK):
                f = c * PIECE_F + t
                nc.tensor.matmul(
                    out=pre[u, c][:, t, :],
                    lhsT=terms[:, b % SLOTS, f * P : (f + 1) * P],
                    rhs=spread[:, b, h * P : (h + 1) * P],
                    start=True,
                    stop=True,
                )

        def side_sums(v, f):
            nodes = slice(v * NODES, (v + 1) * NODES)
            by_pair = sums[:, v, f, :].rearrange("p (i j) -> p i j", j=NODES)
            nc.scalar.activation(
                out=sums[:, v, f, :],
                in_=dist_all[:, v, :],
                func=ACT.Identity,
                scale=vecs[:, 1, f : f + 1],
                bias=vecs[:, 0, f : f + 1],
            )
            for i0 in range(0, NODES, SIDE_NODES):
                piece = by_pair[:, i0 : i0 + SIDE_NODES, :]
                shape = [P, SIDE_NODES, NODES]
                nc.gpsimd.tensor_tensor(
                    out=piece,
                    in0=piece,
                    in1=a_side[:, 0, f, v * NODES + i0 : v * NODES + i0 + SIDE_NODES].unsqueeze(2).to_broadcast(shape),
                    op=ALU.add,
                )
                nc.gpsimd.tensor_tensor(
                    out=piece, in0=piece, in1=a_side[:, 1, f, nodes].unsqueeze(1).to_broadcast(shape), op=ALU.add
                )

        def activate(u, c):
            if c == 0:
                h_grouped[u] = unit_pool.tile([P, PASSES, P, PACK], BF16, align_bytes=64, tag="h", name="h_grouped")
            b, h = order[u // HALVES], u % HALVES
            if b < TENSOR_GRAPHS:
                source = pre[u, c][:]
            else:
                v = b - TENSOR_GRAPHS
                source = sums[:, v, c * PACK : (c + 1) * PACK, h * P : (h + 1) * P]
            nc.scalar.activation(out=h_grouped[u][:, c, :, :], in_=source.rearrange("p t r -> p r t"), func=ACT.Silu)

        def quantise(u):
            h_codes = work.tile([P, PASSES, P], U32, align_bytes=64)
            h_scales = work.tile([P, PASSES, P], U8, align_bytes=64)
            nc.vector.quantize_mx(
                out=h_codes[:].rearrange("p g r -> p (g r)").bitcast(FP8X4),
                scales=h_scales[:].rearrange("p g r -> p (g r)"),
                in_=h_grouped[u][:].rearrange("p g r t -> p (g r t)"),
            )
            h_words[u] = (h_codes, h_scales)

        def multiply(u):
            h_codes, h_scales = h_words[u]
            msg = store_pool.tile([P, WIDTH], F32)
            r0 = order[u // HALVES] * PAIRS + u % HALVES * P
            unit_rows = out_rows[r0 : r0 + P, :]
            for m in range(SIDES):
                columns = slice(m * BANK, (m + 1) * BANK)
                acc = psum_acc.tile([P, BANK], F32, tag="acc")
                for g in range(PASSES):
                    nc.tensor.matmul_mx(
                        out=acc[:],
                        lhsT=h_codes[:, g, :].bitcast(FP8X4),
                        lhsT_scale=h_scales[:, g, :],
                        rhs=w_codes[:, 2, g, m * BANK : (m + 1) * BANK].bitcast(FP8X4),
                        rhs_scale=w_scales[:, 2, g, m * BANK : (m + 1) * BANK],
                        start=(g == 0),
                        stop=(g == PASSES - 1),
                    )
                nc.vector.tensor_tensor(
                    out=msg[:, m * BANK : (m + 1) * BANK],
                    in0=acc[:],
                    in1=be2_all[:, m * BANK : (m + 1) * BANK],
                    op=ALU.add,
                )
                if u == UNITS - 1:
                    nc.sync.dma_start(out=unit_rows[:, columns], in_=msg[:, columns])
            if u < UNITS - 1:
                nc.sync.dma_start(out=unit_rows, in_=msg[:])

        warm = keep.tile([P, 2], F32)
        nc.vector.memset(warm[:], 1.0)
        nc.vector.memset(pos_nodes[:], 0.0)
        nc.vector.memset(vec_rows[:], 0.0)
        dist_columns = keep.tile([P, P], BF16)
        nc.vector.memset(dist_columns[:], 0.0)
        nc.vector.memset(terms[:].rearrange("p s f -> p (s f)").bitcast(I32), 0)
        nc.scalar.dma_start(out=vec_rows[0:F_TILES, :], in_=be1.rearrange("(r c) -> r c", c=P))
        nc.scalar.dma_start(
            out=vec_rows[F_TILES : 2 * F_TILES, :],
            in_=We1[2 * WIDTH : 2 * WIDTH + 1, :].rearrange("o (r c) -> (o r) c", c=P),
        )
        nc.scalar.activation(out=warm[:, 1:2], in_=warm[:, 0:1], func=ACT.Sqrt)
        load_weight(0, 0, slice(0, VECTOR_COLUMNS))
        load_weight(0, 0, slice(VECTOR_COLUMNS, BANK))
        with nc.allow_non_contiguous_dma(reason="768 values in runs of 3, once"):
            nc.sync.dma_start(
                out=pos_nodes[0:NODES, 0 : GRAPHS * COORDS].rearrange("n (b c) -> n b c", c=COORDS),
                in_=positions.rearrange("b n c -> n b c"),
            )
        load_weight(0, 0, slice(BANK, WIDTH))
        nc.sync.dma_start(
            out=x_rows[:], in_=node_state.rearrange("b n h -> (b n) h").rearrange("(a p) h -> p a h", p=P)
        )
        load_weight(0, 1)
        load_weight(1, 0)
        load_weight(1, 1)
        load_weight(2, 0)
        load_weight(2, 1)
        nc.sync.dma_start(
            out=terms[ONE : ONE + 1, :, :],
            in_=be1.partition_broadcast(1).unsqueeze(1).to_broadcast([1, SLOTS, WIDTH]),
        )
        nc.sync.dma_start(
            out=terms[DIST:DIST_END:2, :, :],
            in_=We1[2 * WIDTH : 2 * WIDTH + 1, :]
            .rearrange("o f -> (o f)")
            .partition_broadcast(DIST_PARTS)
            .unsqueeze(1)
            .to_broadcast([DIST_PARTS, SLOTS, WIDTH]),
        )
        make_identity(nc, ident_bf[:])

        pick = keep.tile([P, 2, NODES], BF16)
        for w in range(2):
            nc.gpsimd.tensor_tensor(
                out=pick[:, w, :],
                in0=ident_bf[:, HI + 2 * w : P : ROW_STEP],
                in1=ident_bf[:, LO + 2 * w : P : ROW_STEP],
                op=ALU.add,
            )
        nc.gpsimd.tensor_tensor(
            out=pick[:, 0, :],
            in0=pick[:, 0, :],
            in1=ident_bf[:, ONE : ONE + 1].to_broadcast([P, NODES]),
            op=ALU.add,
        )
        pick_pairs = keep.tile([P, NODES, NODES], BF16)
        nc.gpsimd.tensor_tensor(
            out=pick_pairs[:],
            in0=pick[:, 0, :].unsqueeze(2).to_broadcast([P, NODES, NODES]),
            in1=pick[:, 1, :].unsqueeze(1).to_broadcast([P, NODES, NODES]),
            op=ALU.add,
        )
        sel = keep.tile([P, HALVES, P], BF16)
        for h in range(HALVES):
            nc.gpsimd.tensor_tensor(
                out=sel[:, h, :].rearrange("p (i j) -> p i j", j=NODES),
                in0=ident_bf[:, h * HALF : (h + 1) * HALF].unsqueeze(2).to_broadcast([P, HALF, NODES]),
                in1=ident_bf[:, 0:NODES].unsqueeze(1).to_broadcast([P, HALF, NODES]),
                op=ALU.subtract,
            )
        dist_ones = keep.tile([P, 1], BF16)
        nc.gpsimd.tensor_tensor(
            out=dist_ones[:], in0=ident_bf[:, DIST : DIST + 1], in1=ident_bf[:, DIST + 2 : DIST + 3], op=ALU.add
        )
        nc.gpsimd.tensor_tensor(
            out=dist_ones[:], in0=dist_ones[:], in1=ident_bf[:, DIST + 4 : DIST + 5], op=ALU.add
        )
        by_node = keep.tile([P, P], BF16)
        nc.vector.tensor_copy(
            out=by_node[:].rearrange("p (n b) -> p n b", b=TILE_GRAPHS),
            in_=ident_bf[:].rearrange("p (b n) -> p n b", n=NODES),
        )
        nc.vector.tensor_copy(
            out=spread[:],
            in_=pick_pairs[:].rearrange("p i j -> p (i j)").unsqueeze(1).to_broadcast([P, GRAPHS, PAIRS]),
        )
        rel = psum_acc.tile([P, HALVES, POS_COLUMNS], F32, tag="acc")
        for h in range(HALVES):
            nc.tensor.matmul(out=rel[:, h, :], lhsT=sel[:, h, :], rhs=pos_nodes[:], start=True, stop=True)
        rel_sq = keep.tile([P, HALVES, POS_COLUMNS], F32)
        nc.scalar.activation(out=rel_sq[:], in_=rel[:], func=ACT.Square)
        regroup(0)
        sq = keep.tile([P, HALVES, GRAPHS], F32)
        nc.vector.tensor_reduce(
            out=sq[:],
            in_=rel_sq[:, :, 0 : GRAPHS * COORDS].rearrange("p h (b c) -> p h b c", c=COORDS),
            axis=mybir.AxisListType.X,
            op=ALU.add,
        )
        sq_floor = keep.tile([P, HALVES, GRAPHS], F32)
        nc.vector.tensor_scalar_max(out=sq_floor[:], in0=sq[:], scalar1=TINY)
        root = keep.tile([P, HALVES, GRAPHS], F32)
        nc.scalar.activation(out=root[:], in_=sq_floor[:], func=ACT.Sqrt)

        dist = keep.tile([P, HALVES, GRAPHS], F32)
        nc.vector.scalar_tensor_tensor(
            out=dist[:].rearrange("p h b -> p (h b)"),
            in0=sq[:].rearrange("p h b -> p (h b)"),
            scalar=0.0,
            in1=root[:].rearrange("p h b -> p (h b)"),
            op0=ALU.is_gt,
            op1=ALU.mult,
        )
        part = [
            dist_columns[:, k * HALVES * GRAPHS : (k + 1) * HALVES * GRAPHS].rearrange("p (b h) -> p h b", h=HALVES)
            for k in range(DIST_PARTS)
        ]
        vec_t = psum_acc.tile([P, P], BF16, tag="acc")
        nc.tensor.transpose(vec_t[:], vec_rows[:], ident_bf[:])
        rest = keep.tile([P, HALVES, GRAPHS], F32)
        nc.vector.tensor_copy(out=part[0], in_=dist[:])
        regroup(1)
        nc.vector.tensor_tensor(out=rest[:], in0=dist[:], in1=part[0], op=ALU.subtract)
        quantise_piece(0)
        for a in range(NODE_TILES):
            for g in range(PASSES):
                x_t = psum_pre.tile([P, PACK, P], BF16, tag="pre")
                for t in range(PACK):
                    columns = slice(g * K_PASS + t, (g + 1) * K_PASS, PACK)
                    nc.tensor.transpose(x_t[:, t, :], x_rows[:, a, columns], by_node[:])
                nc.scalar.copy(out=x_grouped[:, g, a * P : (a + 1) * P, :], in_=x_t[:].rearrange("p t r -> p r t"))
        nc.vector.tensor_copy(out=part[1], in_=rest[:])
        quantise_piece(1)
        nc.vector.tensor_tensor(out=part[2], in0=rest[:], in1=part[1], op=ALU.subtract)
        dist_rows_ps = psum_acc.tile([P, P], BF16, tag="acc")
        nc.tensor.transpose(dist_rows_ps[:], dist_columns[:], ident_bf[:])
        regroup(2)
        nc.vector.quantize_mx(
            out=x_codes[:].rearrange("p g r -> p (g r)").bitcast(FP8X4),
            scales=x_scales[:].rearrange("p g r -> p (g r)"),
            in_=x_grouped[:].rearrange("p g r t -> p (g r t)"),
        )
        nc.vector.tensor_copy(out=vecs[:].rearrange("p v f -> p (v f)"), in_=vec_t[:, 0 : 2 * F_TILES])
        product(0, 0, 0)
        product(1, 0, 0)
        regroup(3)
        quantise_piece(2)
        product(0, 0, 1)
        dist_rows = keep.tile([P, P], BF16)
        nc.scalar.copy(out=dist_rows[:], in_=dist_rows_ps[:])
        for k in range(DIST_PARTS):
            rows = slice(k * HALVES * GRAPHS, (k + 1) * HALVES * GRAPHS)
            nc.sync.dma_start(
                out=spread[DIST + 2 * k : DIST + 2 * k + 1, :, :].rearrange("o b q -> o (b q)"), in_=dist_rows[rows, :]
            )
        nc.sync.dma_start(out=be2_all[:], in_=be2.partition_broadcast(P))
        regroup(4)
        quantise_piece(3)
        product(1, 0, 1)
        split_products(0, 0)
        regroup(5)
        quantise_piece(4)
        product(0, 1, 0)
        split_products(1, 0)
        for b in range(EARLY_GRAPHS):
            place_terms(b, 0, slice(0, WIDTH))
        side_product(0, 0)
        side_product(1, 0)
        regroup(6)
        quantise_piece(5)
        product(0, 1, 1)
        regroup(7)
        quantise_piece(6)
        product(1, 1, 0)
        nc.scalar.activation(out=warm[:, 1:2], in_=warm[:, 0:1], func=ACT.Silu)
        split_products(0, 1)
        for b in range(EARLY_GRAPHS):
            place_terms(b, 1, slice(0, BANK))
        copy_side(0, 0)
        copy_side(1, 0)
        regroup(8)
        quantise_piece(7)
        product(1, 1, 1)
        regroup(9)
        split_products(1, 1)
        for b in range(EARLY_GRAPHS):
            place_terms(b, 1, slice(BANK, WIDTH))
        for b in range(EARLY_GRAPHS, SLOTS):
            for w in range(2):
                place_terms(b, w, slice(0, WIDTH))
        form_pre(0, 0)
        form_pre(1, 0)
        side_product(0, 1)
        side_product(1, 1)
        quantise_piece(8)
        regroup(10)
        quantise_piece(9)
        activate(0, 0)
        regroup(11)
        activate(1, 0)
        form_pre(0, 1)
        form_pre(LEAD, 0)
        quantise_piece(10)
        copy_side(0, 1)
        copy_side(1, 1)
        quantise_piece(11)

        for u in range(UNITS + 2):
            if u < UNITS:
                activate(u, 1)
            if u + LEAD < UNITS:
                activate(u + LEAD, 0)
            k, h = divmod(u, HALVES)
            if h == HALVES - 1 and k < GRAPHS and order[k] + SLOTS < TENSOR_GRAPHS:
                for w in range(2):
                    place_terms(order[k] + SLOTS, w, slice(0, WIDTH))
            if u == 1:
                dist_ps = []
                for v in range(0, SIDE_GRAPHS, 2):
                    n = min(2, SIDE_GRAPHS - v)
                    dist_ps.append(psum_acc.tile([P, n, PAIRS], F32, tag="acc", name="dist_ps"))
                    nc.tensor.matmul(
                        out=dist_ps[-1][:].rearrange("p v q -> p (v q)"),
                        lhsT=dist_ones[:].to_broadcast([P, P]),
                        rhs=spread[:, TENSOR_GRAPHS + v : TENSOR_GRAPHS + v + n, :].rearrange("p v q -> p (v q)"),
                        start=True,
                        stop=True,
                    )
                for k, d in enumerate(dist_ps):
                    nc.scalar.copy(out=dist_all[:, 2 * k : min(2 * k + 2, SIDE_GRAPHS), :], in_=d[:])
            if 1 <= u <= UNITS:
                quantise(u - 1)
            for n in range(SIDE_RATE * (u - 1), SIDE_RATE * u):
                if 0 <= n < SIDE_GRAPHS * F_TILES:
                    side_sums(*divmod(n, F_TILES))
            if u >= 2:
                multiply(u - 2)
            if u + 1 < UNITS:
                form_pre(u + 1, 1)
            if u + LEAD + 1 < UNITS:
                form_pre(u + LEAD + 1, 0)
